import numpy as np
import ml_dtypes


def mxq(x, axis, fmt="e4m3"):
    dtype, down = {"e4m3": (ml_dtypes.float8_e4m3fn, 7), "e5m2": (ml_dtypes.float8_e5m2, 14)}[fmt]
    v = np.moveaxis(np.asarray(x, np.float32).astype(ml_dtypes.bfloat16).astype(np.float64), axis, -1)
    blocks = v.reshape(v.shape[:-1] + (-1, 32))
    amax = np.abs(blocks).max(-1, keepdims=True)
    byte = np.maximum(np.where(amax > 0, np.frexp(amax)[1] - 1 + 127, 0) - down, 1)
    scale = np.exp2(byte - 127.0)
    codes = (blocks / scale).astype(np.float32).astype(dtype).astype(np.float64)
    return np.moveaxis((codes * scale).reshape(v.shape), -1, axis)


WIDE = False


def mx_kscale(k):
    if not WIDE:
        return np.ones(k)
    levels = np.array([10, -10, 5, -5, 0])
    a = np.random.permutation(np.resize(levels, k // 512 * 4)).reshape(k // 512, 4)
    idx = np.arange(k)
    return np.exp2(a[idx // 512, idx % 128 // 32])


BF16 = ml_dtypes.bfloat16


def bf(x):
    return np.asarray(x, np.float32).astype(BF16)


def f64(x):
    return np.asarray(x).astype(np.float64)


B, S, D, H, KH, HD, W = 4, 2048, 512, 1, 1, 128, 512
EPS = 1e-6
BASE = 10000.0


def rope_cos_sin():
    inv_freq = 1.0 / BASE ** (np.arange(0, HD, 2) / HD)
    ang = np.arange(S)[:, None] * inv_freq[None, :]
    return np.cos(ang)[None, :, None, :], np.sin(ang)[None, :, None, :]


def rotate(t, cos, sin):
    te, to = t[..., ::2], t[..., 1::2]
    return np.stack([te * cos - to * sin, te * sin + to * cos], axis=-1).reshape(t.shape)


def setup_inputs():
    s = mx_kscale(D)
    c = 1.0 / np.sqrt(D)
    return {"x": bf(np.random.standard_normal((B, S, D)) * 5.0 * np.sqrt(EPS)),
            "ln_w": bf((1.0 + 0.1 * np.random.standard_normal(D)) * s),
            "wq": bf(np.random.standard_normal((D, H * HD)) * c / s[:, None]),
            "wk": bf(np.random.standard_normal((D, KH * HD)) * c / s[:, None]),
            "wv": bf(np.random.standard_normal((D, KH * HD)) * 2.0 * c / s[:, None])}


def reference(x, ln_w, wq, wk, wv):
    x = f64(x)
    xn = x / np.sqrt(np.mean(x * x, axis=-1, keepdims=True) + EPS) * f64(ln_w)
    xq = mxq(xn, 2, "e4m3")
    q = (xq @ mxq(f64(wq), 0, "e4m3")).reshape(B, S, H, HD)
    k = (xq @ mxq(f64(wk), 0, "e4m3")).reshape(B, S, KH, HD)
    v = (xq @ mxq(f64(wv), 0, "e4m3")).reshape(B, S, KH, HD)
    cos, sin = rope_cos_sin()
    return rotate(q, cos, sin), rotate(k, cos, sin), v

@@ -1,0 +1,265 @@
+import math
+from contextlib import ExitStack
+
+import concourse.mybir as mybir
+from concourse.masks import make_identity
+
+F32 = mybir.dt.float32
+BF16 = mybir.dt.bfloat16
+I32 = mybir.dt.int32
+U32 = mybir.dt.uint32
+U8 = mybir.dt.uint8
+FP8X4 = mybir.dt.float8_e4m3fn_x4
+ALU = mybir.AluOpType
+ACT = mybir.ActivationFunctionType
+
+BATCH, SEQ, D, HD = 4, 2048, 512, 128
+EPS = 1e-6
+BASE = 10000.0
+
+P = 128
+PACK = 4
+PAIRS = HD // 2
+TILES = 4
+GROUP = TILES * P
+GROUPS = BATCH * SEQ // GROUP
+GROUPS_PER_SEQ = SEQ // GROUP
+SEQ_TILES = GROUPS_PER_SEQ * TILES
+ROUND_TO_INTEGER = 1.5 * 2.0**23
+
+FLOPS = 2 * BATCH * SEQ * D * 3 * HD
+
+
+def broadcast_gain(nc, const, psum_const, ln_w):
+    gain_row = const.tile([P, D], BF16, name="gain_row")
+    nc.vector.memset(gain_row[:], 0.0)
+    nc.scalar.dma_start(out=gain_row[0:1, :], in_=ln_w.rearrange("(o d) -> o d", o=1))
+    ones = const.tile([P, P], BF16, name="ones")
+    nc.vector.memset(ones[:], 1.0)
+    gain = psum_const.tile([P, D], F32, name="gain")
+    nc.tensor.matmul(out=gain[:], lhsT=ones[:], rhs=gain_row[:], start=True, stop=True)
+    return gain
+
+
+def quantise_weights(nc, const, wq, wk, wv):
+    raw = const.tile([P, 3, PACK, HD], BF16, name="w_raw")
+    grouped = const.tile([P, 3, HD, PACK], BF16, name="w_grouped", align_bytes=64)
+    codes = const.tile([P, 3, HD], U32, name="w_codes", align_bytes=64)
+    scales = const.tile([P, 3, HD], U8, name="w_scales", align_bytes=64)
+    for c, w in enumerate((wq, wk, wv)):
+        nc.scalar.dma_start(
+            out=raw[:, c].rearrange("p (u e) n -> p u (e n)", u=2),
+            in_=w.rearrange("(u p e) n -> p u (e n)", u=2, e=2),
+        )
+    for c in range(3):
+        if c < 2:
+            nc.vector.tensor_copy(
+                out=grouped[:, c].rearrange("p (h i) t -> p h i t", h=2),
+                in_=raw[:, c].rearrange("p t (i h) -> p h i t", h=2),
+            )
+        else:
+            nc.vector.tensor_copy(out=grouped[:, c], in_=raw[:, c].rearrange("p t n -> p n t"))
+    for c in range(3):
+        nc.vector.quantize_mx(
+            out=codes[:, c].bitcast(FP8X4),
+            scales=scales[:, c],
+            in_=grouped[:, c].rearrange("p n t -> p (n t)"),
+        )
+    return codes, scales
+
+
+def rotation_tables(nc, const):
+    position_int = const.tile([P, SEQ_TILES], I32, name="position_int")
+    nc.gpsimd.iota(
+        position_int[:], pattern=[[GROUP, GROUPS_PER_SEQ], [1, TILES]], base=0, channel_multiplier=TILES
+    )
+    position = const.tile([P, SEQ_TILES], F32, name="position")
+    nc.vector.tensor_copy(out=position[:], in_=position_int[:])
+
+    one = const.tile([P, 1], F32, name="one")
+    nc.vector.memset(one[:], 1.0)
+    coarse = const.tile([P, 8], F32, name="coarse")
+    fine = const.tile([P, 8], F32, name="fine")
+    for a in range(8):
+        nc.vector.tensor_scalar_mul(
+            out=coarse[:, a : a + 1], in0=one[:], scalar1=BASE ** (-8.0 * a / PAIRS) / (2.0 * math.pi)
+        )
+    for b in range(8):
+        nc.vector.tensor_scalar_mul(out=fine[:, b : b + 1], in0=one[:], scalar1=BASE ** (-1.0 * b / PAIRS))
+    frequency = const.tile([P, 8, 8], F32, name="frequency")
+    nc.vector.tensor_tensor(
+        out=frequency[:],
+        in0=coarse[:].unsqueeze(2).to_broadcast([P, 8, 8]),
+        in1=fine[:].unsqueeze(1).to_broadcast([P, 8, 8]),
+        op=ALU.mult,
+    )
+
+    shape = [P, SEQ_TILES, PAIRS]
+    turns = const.tile(shape, F32, name="turns")
+    nc.vector.tensor_tensor(
+        out=turns[:],
+        in0=position[:].unsqueeze(2).to_broadcast(shape),
+        in1=frequency[:].rearrange("p a b -> p (a b)").unsqueeze(1).to_broadcast(shape),
+        op=ALU.mult,
+    )
+    whole = const.tile(shape, F32, name="whole")
+    nc.vector.tensor_scalar(
+        out=whole[:],
+        in0=turns[:],
+        scalar1=ROUND_TO_INTEGER,
+        scalar2=ROUND_TO_INTEGER,
+        op0=ALU.add,
+        op1=ALU.subtract,
+    )
+    part = const.tile(shape, F32, name="part")
+    nc.vector.tensor_tensor(out=part[:], in0=turns[:], in1=whole[:], op=ALU.subtract)
+    minus_abs = const.tile(shape, F32, name="minus_abs")
+    nc.vector.scalar_tensor_tensor(
+        out=minus_abs[:], in0=part[:], scalar=-1.0, in1=part[:], op0=ALU.mult, op1=ALU.min
+    )
+    quarter_less = const.tile(shape, F32, name="quarter_less")
+    nc.vector.tensor_scalar_add(out=quarter_less[:], in0=minus_abs[:], scalar1=0.25)
+
+    planes = const.tile([P, 3, SEQ_TILES * PAIRS], F32, name="planes")
+    flat = "p s i -> p (s i)"
+    nc.scalar.activation(out=planes[:, 0], in_=part[:].rearrange(flat), func=ACT.Sin, scale=-2.0 * math.pi)
+    nc.scalar.activation(
+        out=planes[:, 1], in_=quarter_less[:].rearrange(flat), func=ACT.Sin, scale=2.0 * math.pi
+    )
+    nc.scalar.activation(out=planes[:, 2], in_=part[:].rearrange(flat), func=ACT.Sin, scale=2.0 * math.pi)
+
+    msin_cos = const.tile([P, SEQ_TILES, PAIRS, 2], F32, name="msin_cos")
+    cos_sin = const.tile([P, SEQ_TILES, PAIRS, 2], F32, name="cos_sin")
+    for table, first in ((msin_cos, 0), (cos_sin, 1)):
+        nc.gpsimd.tensor_scalar(
+            out=table[:].rearrange("p s i h -> p (s i) h"),
+            in0=planes[:, first : first + 2].rearrange("p h n -> p n h"),
+            scalar1=1.0,
+            scalar2=0.0,
+            op0=ALU.mult,
+            op1=ALU.add,
+        )
+    return cos_sin, msin_cos
+
+
+def rotate(engine, pool, name, halves, cos_sin, msin_cos):
+    shape = [P, TILES, PAIRS, 2]
+    from_even = pool.tile(shape, F32, name=name + "_from_even")
+    from_odd = pool.tile(shape, F32, name=name + "_from_odd")
+    rotated = pool.tile(shape, F32, name=name + "_rotated")
+    engine.tensor_tensor(
+        out=from_even[:], in0=halves[:, :, 0:PAIRS].unsqueeze(3).to_broadcast(shape), in1=cos_sin, op=ALU.mult
+    )
+    engine.tensor_tensor(
+        out=from_odd[:], in0=halves[:, :, PAIRS:HD].unsqueeze(3).to_broadcast(shape), in1=msin_cos, op=ALU.mult
+    )
+    engine.tensor_tensor(out=rotated[:], in0=from_even[:], in1=from_odd[:], op=ALU.add)
+    return rotated
+
+
+def tile_slidingwindowattention_pa_t_kernel(tc, x, ln_w, wq, wk, wv, out_0, out_1, out_2):
+    nc = tc.nc
+    by_group = "(g p j) d -> g p (j d)"
+    x_groups = x.rearrange("b s d -> (b s) d").rearrange(by_group, p=P, j=TILES)
+    q_groups = out_0.rearrange("b s h d -> (b s h) d").rearrange(by_group, p=P, j=TILES)
+    k_groups = out_1.rearrange("b s h d -> (b s h) d").rearrange(by_group, p=P, j=TILES)
+    v_groups = out_2.rearrange("b s h d -> (b s h) d").rearrange(by_group, p=P, j=TILES)
+
+    with ExitStack() as ctx:
+        const = ctx.enter_context(tc.tile_pool(name="const", bufs=1))
+        loads = ctx.enter_context(tc.tile_pool(name="loads", bufs=8))
+        small = ctx.enter_context(tc.tile_pool(name="small", bufs=4))
+        work = ctx.enter_context(tc.tile_pool(name="work", bufs=3))
+        turn = ctx.enter_context(tc.tile_pool(name="turn", bufs=2))
+        psum_const = ctx.enter_context(tc.psum_pool(name="psum_const", bufs=1))
+        psum_turned = ctx.enter_context(tc.psum_pool(name="psum_turned", bufs=4))
+        psum_out = ctx.enter_context(tc.psum_pool(name="psum_out", bufs=1))
+
+        gain = broadcast_gain(nc, const, psum_const, ln_w)
+        w_codes, w_scales = quantise_weights(nc, const, wq, wk, wv)
+        cos_sin, msin_cos = rotation_tables(nc, const)
+        identity = const.tile([P, P], F32, name="identity")
+        make_identity(nc, identity[:])
+        minus_half = const.tile([P, TILES], F32, name="minus_half")
+        nc.vector.memset(minus_half[:], -0.5)
+
+        for g in range(GROUPS):
+            x_t = loads.tile([P, TILES * D], BF16, name="x_t")
+            nc.sync.dma_start(out=x_t[:], in_=x_groups[g])
+
+            mean_sq = small.tile([P, TILES], F32, name="mean_sq")
+            squares = work.tile([P, TILES * D], BF16, name="squares")
+            for j in range(TILES):
+                cols = slice(j * D, (j + 1) * D)
+                nc.scalar.activation(
+                    out=squares[:, cols],
+                    in_=x_t[:, cols],
+                    func=ACT.Square,
+                    scale=1.0 / math.sqrt(D),
+                    accum_out=mean_sq[:, j : j + 1],
+                )
+            shifted = small.tile([P, TILES], F32, name="shifted")
+            nc.gpsimd.tensor_scalar(
+                out=shifted[:], in0=mean_sq[:], scalar1=1.0, scalar2=EPS, op0=ALU.mult, op1=ALU.add
+            )
+            rstd = small.tile([P, TILES], F32, name="rstd")
+            nc.gpsimd.tensor_tensor(out=rstd[:], in0=shifted[:], in1=minus_half[:], op=ALU.pow)
+
+            xn = work.tile([P, TILES * D], BF16, name="xn")
+            for j in range(TILES):
+                cols = slice(j * D, (j + 1) * D)
+                nc.vector.scalar_tensor_tensor(
+                    out=xn[:, cols],
+                    in0=x_t[:, cols],
+                    scalar=rstd[:, j : j + 1],
+                    in1=gain[:],
+                    op0=ALU.mult,
+                    op1=ALU.mult,
+                )
+
+            xn_words = xn[:].bitcast(F32).rearrange("p (j u w) -> p j u w", j=TILES, u=2)
+            grouped = work.tile([P, GROUP * PACK], BF16, name="grouped", align_bytes=64)
+            grouped_words = grouped[:].bitcast(F32).rearrange("p (j t u) -> p j t u", j=TILES, u=2)
+            for first in range(0, TILES, 2):
+                turned = psum_turned.tile([P, 2, 2, P], F32, name="turned")
+                for j in range(2):
+                    for u in range(2):
+                        nc.tensor.transpose(
+                            out=turned[:, j, u, :], in_=xn_words[:, first + j, u, :], identity=identity[:]
+                        )
+                nc.scalar.copy(
+                    out=grouped_words[:, first : first + 2], in_=turned[:].rearrange("p j u t -> p j t u")
+                )
+            codes = work.tile([P, GROUP], U32, name="codes", align_bytes=64)
+            scales = work.tile([P, GROUP], U8, name="scales", align_bytes=64)
+            nc.vector.quantize_mx(out=codes[:].bitcast(FP8X4), scales=scales[:], in_=grouped[:])
+
+            q_ps = psum_out.tile([P, TILES, HD], F32, name="q_ps")
+            k_ps = psum_out.tile([P, TILES, HD], F32, name="k_ps")
+            v_ps = psum_out.tile([P, TILES, HD], F32, name="v_ps")
+            for j in range(TILES):
+                tokens = slice(j * P, (j + 1) * P)
+                for c, bank in enumerate((q_ps, k_ps, v_ps)):
+                    nc.tensor.matmul_mx(
+                        out=bank[:, j, :],
+                        lhsT=codes[:, tokens].bitcast(FP8X4),
+                        lhsT_scale=scales[:, tokens],
+                        rhs=w_codes[:, c].bitcast(FP8X4),
+                        rhs_scale=w_scales[:, c],
+                        start=True,
+                        stop=True,
+                    )
+
+            s = g % GROUPS_PER_SEQ
+            group_cos_sin = cos_sin[:, s * TILES : (s + 1) * TILES]
+            group_msin_cos = msin_cos[:, s * TILES : (s + 1) * TILES]
+            q_rot = rotate(nc.vector, turn, "q", q_ps, group_cos_sin, group_msin_cos)
+            k_sb = turn.tile([P, TILES, HD], F32, name="k_sb")
+            nc.scalar.copy(out=k_sb[:], in_=k_ps[:])
+            k_rot = rotate(nc.gpsimd, turn, "k", k_sb, group_cos_sin, group_msin_cos)
+            v_sb = turn.tile([P, TILES, HD], F32, name="v_sb")
+            nc.scalar.copy(out=v_sb[:], in_=v_ps[:])
+
+            nc.sync.dma_start(out=q_groups[g], in_=q_rot[:].rearrange("p j i h -> p (j i h)"))
+            nc.sync.dma_start(out=k_groups[g], in_=k_rot[:].rearrange("p j i h -> p (j i h)"))
+            nc.sync.dma_start(out=v_groups[g], in_=v_sb[:].rearrange("p j d -> p (j d)"))

@@ -142,18 +142,18 @@ def rotation_tables(nc, const):
     return cos_sin, msin_cos
 
 
-def rotate(engine, pool, name, halves, cos_sin, msin_cos):
+def rotate(nc, pool, name, halves, cos_sin, msin_cos):
     shape = [P, TILES, PAIRS, 2]
     from_even = pool.tile(shape, F32, name=name + "_from_even")
     from_odd = pool.tile(shape, F32, name=name + "_from_odd")
     rotated = pool.tile(shape, F32, name=name + "_rotated")
-    engine.tensor_tensor(
+    nc.vector.tensor_tensor(
         out=from_even[:], in0=halves[:, :, 0:PAIRS].unsqueeze(3).to_broadcast(shape), in1=cos_sin, op=ALU.mult
     )
-    engine.tensor_tensor(
+    nc.vector.tensor_tensor(
         out=from_odd[:], in0=halves[:, :, PAIRS:HD].unsqueeze(3).to_broadcast(shape), in1=msin_cos, op=ALU.mult
     )
-    engine.tensor_tensor(out=rotated[:], in0=from_even[:], in1=from_odd[:], op=ALU.add)
+    nc.gpsimd.tensor_tensor(out=rotated[:], in0=from_even[:], in1=from_odd[:], op=ALU.add)
     return rotated
 
 
@@ -253,10 +253,8 @@ def tile_slidingwindowattention_pa_t_kernel(tc, x, ln_w, wq, wk, wv, out_0, out_
             s = g % GROUPS_PER_SEQ
             group_cos_sin = cos_sin[:, s * TILES : (s + 1) * TILES]
             group_msin_cos = msin_cos[:, s * TILES : (s + 1) * TILES]
-            q_rot = rotate(nc.vector, turn, "q", q_ps, group_cos_sin, group_msin_cos)
-            k_sb = turn.tile([P, TILES, HD], F32, name="k_sb")
-            nc.scalar.copy(out=k_sb[:], in_=k_ps[:])
-            k_rot = rotate(nc.gpsimd, turn, "k", k_sb, group_cos_sin, group_msin_cos)
+            q_rot = rotate(nc, turn, "q", q_ps, group_cos_sin, group_msin_cos)
+            k_rot = rotate(nc, turn, "k", k_ps, group_cos_sin, group_msin_cos)
             v_sb = turn.tile([P, TILES, HD], F32, name="v_sb")
             nc.scalar.copy(out=v_sb[:], in_=v_ps[:])
 

@@ -23,17 +23,13 @@ PAIRS = HD // 2
 TILES = 4
 GROUP = TILES * P
 GROUPS = BATCH * SEQ // GROUP
-GROUPS_PER_SEQ = SEQ // GROUP
-SEQ_TILES = GROUPS_PER_SEQ * TILES
+BLOCKS = SEQ // GROUP
 ROUND_TO_INTEGER = 1.5 * 2.0**23
 
 FLOPS = 2 * BATCH * SEQ * D * 3 * HD
 
 
-def broadcast_gain(nc, const, psum_const, ln_w):
-    gain_row = const.tile([P, D], BF16, name="gain_row")
-    nc.vector.memset(gain_row[:], 0.0)
-    nc.scalar.dma_start(out=gain_row[0:1, :], in_=ln_w.rearrange("(o d) -> o d", o=1))
+def broadcast_gain(nc, const, psum_const, gain_row):
     ones = const.tile([P, P], BF16, name="ones")
     nc.vector.memset(ones[:], 1.0)
     gain = psum_const.tile([P, D], F32, name="gain")
@@ -41,24 +37,16 @@ def broadcast_gain(nc, const, psum_const, ln_w):
     return gain
 
 
-def quantise_weights(nc, const, wq, wk, wv):
-    raw = const.tile([P, 3, PACK, HD], BF16, name="w_raw")
+def quantise_weights(nc, const, raw):
     grouped = const.tile([P, 3, HD, PACK], BF16, name="w_grouped", align_bytes=64)
     codes = const.tile([P, 3, HD], U32, name="w_codes", align_bytes=64)
     scales = const.tile([P, 3, HD], U8, name="w_scales", align_bytes=64)
-    for c, w in enumerate((wq, wk, wv)):
-        nc.scalar.dma_start(
-            out=raw[:, c].rearrange("p (u e) n -> p u (e n)", u=2),
-            in_=w.rearrange("(u p e) n -> p u (e n)", u=2, e=2),
+    for m in range(2):
+        nc.vector.tensor_copy(
+            out=grouped[:, 0:2, m * PAIRS : (m + 1) * PAIRS, :],
+            in_=raw[:, m].rearrange("p t (i h) -> p h i t", h=2),
         )
-    for c in range(3):
-        if c < 2:
-            nc.vector.tensor_copy(
-                out=grouped[:, c].rearrange("p (h i) t -> p h i t", h=2),
-                in_=raw[:, c].rearrange("p t (i h) -> p h i t", h=2),
-            )
-        else:
-            nc.vector.tensor_copy(out=grouped[:, c], in_=raw[:, c].rearrange("p t n -> p n t"))
+    nc.vector.tensor_copy(out=grouped[:, 2], in_=raw[:, 2].rearrange("p t n -> p n t"))
     for c in range(3):
         nc.vector.quantize_mx(
             out=codes[:, c].bitcast(FP8X4),
@@ -68,12 +56,10 @@ def quantise_weights(nc, const, wq, wk, wv):
     return codes, scales
 
 
-def rotation_tables(nc, const):
-    position_int = const.tile([P, SEQ_TILES], I32, name="position_int")
-    nc.gpsimd.iota(
-        position_int[:], pattern=[[GROUP, GROUPS_PER_SEQ], [1, TILES]], base=0, channel_multiplier=TILES
-    )
-    position = const.tile([P, SEQ_TILES], F32, name="position")
+def rotation_angles(nc, const):
+    position_int = const.tile([P, BLOCKS * TILES], I32, name="position_int")
+    nc.gpsimd.iota(position_int[:], pattern=[[GROUP, BLOCKS], [1, TILES]], base=0, channel_multiplier=TILES)
+    position = const.tile([P, BLOCKS * TILES], F32, name="position")
     nc.vector.tensor_copy(out=position[:], in_=position_int[:])
 
     one = const.tile([P, 1], F32, name="one")
@@ -94,7 +80,7 @@ def rotation_tables(nc, const):
         op=ALU.mult,
     )
 
-    shape = [P, SEQ_TILES, PAIRS]
+    shape = [P, BLOCKS * TILES, PAIRS]
     turns = const.tile(shape, F32, name="turns")
     nc.vector.tensor_tensor(
         out=turns[:],
@@ -119,42 +105,7 @@ def rotation_tables(nc, const):
     )
     quarter_less = const.tile(shape, F32, name="quarter_less")
     nc.vector.tensor_scalar_add(out=quarter_less[:], in0=minus_abs[:], scalar1=0.25)
-
-    planes = const.tile([P, 3, SEQ_TILES * PAIRS], F32, name="planes")
-    flat = "p s i -> p (s i)"
-    nc.scalar.activation(out=planes[:, 0], in_=part[:].rearrange(flat), func=ACT.Sin, scale=-2.0 * math.pi)
-    nc.scalar.activation(
-        out=planes[:, 1], in_=quarter_less[:].rearrange(flat), func=ACT.Sin, scale=2.0 * math.pi
-    )
-    nc.scalar.activation(out=planes[:, 2], in_=part[:].rearrange(flat), func=ACT.Sin, scale=2.0 * math.pi)
-
-    msin_cos = const.tile([P, SEQ_TILES, PAIRS, 2], F32, name="msin_cos")
-    cos_sin = const.tile([P, SEQ_TILES, PAIRS, 2], F32, name="cos_sin")
-    for table, first in ((msin_cos, 0), (cos_sin, 1)):
-        nc.gpsimd.tensor_scalar(
-            out=table[:].rearrange("p s i h -> p (s i) h"),
-            in0=planes[:, first : first + 2].rearrange("p h n -> p n h"),
-            scalar1=1.0,
-            scalar2=0.0,
-            op0=ALU.mult,
-            op1=ALU.add,
-        )
-    return cos_sin, msin_cos
-
-
-def rotate(nc, pool, name, halves, cos_sin, msin_cos):
-    shape = [P, TILES, PAIRS, 2]
-    from_even = pool.tile(shape, F32, name=name + "_from_even")
-    from_odd = pool.tile(shape, F32, name=name + "_from_odd")
-    rotated = pool.tile(shape, F32, name=name + "_rotated")
-    nc.vector.tensor_tensor(
-        out=from_even[:], in0=halves[:, :, 0:PAIRS].unsqueeze(3).to_broadcast(shape), in1=cos_sin, op=ALU.mult
-    )
-    nc.vector.tensor_tensor(
-        out=from_odd[:], in0=halves[:, :, PAIRS:HD].unsqueeze(3).to_broadcast(shape), in1=msin_cos, op=ALU.mult
-    )
-    nc.gpsimd.tensor_tensor(out=rotated[:], in0=from_even[:], in1=from_odd[:], op=ALU.add)
-    return rotated
+    return part, quarter_less
 
 
 def tile_slidingwindowattention_pa_t_kernel(tc, x, ln_w, wq, wk, wv, out_0, out_1, out_2):
@@ -167,79 +118,130 @@ def tile_slidingwindowattention_pa_t_kernel(tc, x, ln_w, wq, wk, wv, out_0, out_
 
     with ExitStack() as ctx:
         const = ctx.enter_context(tc.tile_pool(name="const", bufs=1))
-        loads = ctx.enter_context(tc.tile_pool(name="loads", bufs=8))
+        loads = ctx.enter_context(tc.tile_pool(name="loads", bufs=GROUPS))
         small = ctx.enter_context(tc.tile_pool(name="small", bufs=4))
-        work = ctx.enter_context(tc.tile_pool(name="work", bufs=3))
-        turn = ctx.enter_context(tc.tile_pool(name="turn", bufs=2))
+        work = ctx.enter_context(tc.tile_pool(name="work", bufs=2))
+        stores = ctx.enter_context(tc.tile_pool(name="stores", bufs=3))
         psum_const = ctx.enter_context(tc.psum_pool(name="psum_const", bufs=1))
         psum_turned = ctx.enter_context(tc.psum_pool(name="psum_turned", bufs=4))
         psum_out = ctx.enter_context(tc.psum_pool(name="psum_out", bufs=1))
+        ctx.enter_context(tc.manual_schedule())
 
-        gain = broadcast_gain(nc, const, psum_const, ln_w)
-        w_codes, w_scales = quantise_weights(nc, const, wq, wk, wv)
-        cos_sin, msin_cos = rotation_tables(nc, const)
+        x_tiles = [loads.tile([P, TILES * D], BF16, name="x_t") for g in range(GROUPS)]
+        gain_row = const.tile([P, D], BF16, name="gain_row")
+        w_raw = const.tile([P, 3, PACK, HD], BF16, name="w_raw")
+        nc.vector.memset(gain_row[:], 0.0)
+        nc.sync.dma_start(out=x_tiles[0][:], in_=x_groups[0])
+        nc.sync.dma_start(out=gain_row[0:1, :], in_=ln_w.rearrange("(o d) -> o d", o=1))
+        for m, w in enumerate((wq, wk, wv)):
+            nc.sync.dma_start(
+                out=w_raw[:, m].rearrange("p (u e) n -> p u (e n)", u=2),
+                in_=w.rearrange("(u p e) n -> p u (e n)", u=2, e=2),
+            )
+        for g in range(1, GROUPS):
+            nc.sync.dma_start(out=x_tiles[g][:], in_=x_groups[g])
+
+        part, quarter_less = rotation_angles(nc, const)
         identity = const.tile([P, P], F32, name="identity")
         make_identity(nc, identity[:])
         minus_half = const.tile([P, TILES], F32, name="minus_half")
         nc.vector.memset(minus_half[:], -0.5)
+        gain = broadcast_gain(nc, const, psum_const, gain_row)
+        w_codes, w_scales = quantise_weights(nc, const, w_raw)
 
-        for g in range(GROUPS):
-            x_t = loads.tile([P, TILES * D], BF16, name="x_t")
-            nc.sync.dma_start(out=x_t[:], in_=x_groups[g])
+        planes = const.tile([P, 3, BLOCKS * TILES * PAIRS], F32, name="planes")
+        msin_cos = const.tile([P, BLOCKS * TILES, PAIRS, 2], F32, name="msin_cos")
+        cos_sin = const.tile([P, BLOCKS * TILES, PAIRS, 2], F32, name="cos_sin")
 
+        def sines(s):
+            rows = slice(s * TILES, (s + 1) * TILES)
+            cols = slice(s * TILES * PAIRS, (s + 1) * TILES * PAIRS)
+            for plane, angle, scale in ((0, part, -2.0 * math.pi), (1, quarter_less, 2.0 * math.pi), (2, part, 2.0 * math.pi)):
+                nc.scalar.activation(
+                    out=planes[:, plane, cols], in_=angle[:, rows].rearrange("p j i -> p (j i)"), func=ACT.Sin, scale=scale
+                )
+
+        def interleave(s):
+            rows = slice(s * TILES, (s + 1) * TILES)
+            cols = slice(s * TILES * PAIRS, (s + 1) * TILES * PAIRS)
+            for table, first in ((cos_sin, 1), (msin_cos, 0)):
+                nc.gpsimd.tensor_scalar(
+                    out=table[:, rows].rearrange("p j i h -> p (j i) h"),
+                    in0=planes[:, first : first + 2, cols].rearrange("p h n -> p n h"),
+                    scalar1=1.0,
+                    scalar2=0.0,
+                    op0=ALU.mult,
+                    op1=ALU.add,
+                )
+
+        rstds, xns, turneds, groupeds, operands, banks, products, v_copies = {}, {}, {}, {}, {}, {}, {}, {}
+
+        def mean_squares(g):
             mean_sq = small.tile([P, TILES], F32, name="mean_sq")
             squares = work.tile([P, TILES * D], BF16, name="squares")
             for j in range(TILES):
                 cols = slice(j * D, (j + 1) * D)
                 nc.scalar.activation(
                     out=squares[:, cols],
-                    in_=x_t[:, cols],
+                    in_=x_tiles[g][:, cols],
                     func=ACT.Square,
                     scale=1.0 / math.sqrt(D),
                     accum_out=mean_sq[:, j : j + 1],
                 )
+            rstds[g] = mean_sq
+
+        def inverse_rms(g):
             shifted = small.tile([P, TILES], F32, name="shifted")
             nc.gpsimd.tensor_scalar(
-                out=shifted[:], in0=mean_sq[:], scalar1=1.0, scalar2=EPS, op0=ALU.mult, op1=ALU.add
+                out=shifted[:], in0=rstds[g][:], scalar1=1.0, scalar2=EPS, op0=ALU.mult, op1=ALU.add
             )
             rstd = small.tile([P, TILES], F32, name="rstd")
             nc.gpsimd.tensor_tensor(out=rstd[:], in0=shifted[:], in1=minus_half[:], op=ALU.pow)
+            rstds[g] = rstd
 
+        def normalise(g):
             xn = work.tile([P, TILES * D], BF16, name="xn")
             for j in range(TILES):
                 cols = slice(j * D, (j + 1) * D)
                 nc.vector.scalar_tensor_tensor(
                     out=xn[:, cols],
-                    in0=x_t[:, cols],
-                    scalar=rstd[:, j : j + 1],
+                    in0=x_tiles[g][:, cols],
+                    scalar=rstds[g][:, j : j + 1],
                     in1=gain[:],
                     op0=ALU.mult,
                     op1=ALU.mult,
                 )
+            xns[g] = xn
 
-            xn_words = xn[:].bitcast(F32).rearrange("p (j u w) -> p j u w", j=TILES, u=2)
-            grouped = work.tile([P, GROUP * PACK], BF16, name="grouped", align_bytes=64)
-            grouped_words = grouped[:].bitcast(F32).rearrange("p (j t u) -> p j t u", j=TILES, u=2)
+        def turn(g):
+            words = xns[g][:].bitcast(F32).rearrange("p (j u w) -> p j u w", j=TILES, u=2)
+            turneds[g] = []
             for first in range(0, TILES, 2):
                 turned = psum_turned.tile([P, 2, 2, P], F32, name="turned")
                 for j in range(2):
                     for u in range(2):
-                        nc.tensor.transpose(
-                            out=turned[:, j, u, :], in_=xn_words[:, first + j, u, :], identity=identity[:]
-                        )
-                nc.scalar.copy(
-                    out=grouped_words[:, first : first + 2], in_=turned[:].rearrange("p j u t -> p j t u")
-                )
+                        nc.tensor.transpose(out=turned[:, j, u, :], in_=words[:, first + j, u, :], identity=identity[:])
+                turneds[g].append(turned)
+
+        def regroup(g):
+            grouped = work.tile([P, GROUP * PACK], BF16, name="grouped", align_bytes=64)
+            words = grouped[:].bitcast(F32).rearrange("p (b j t u) -> p b j t u", b=2, j=2, u=2)
+            for b, turned in enumerate(turneds[g]):
+                nc.scalar.copy(out=words[:, b], in_=turned[:].rearrange("p j u t -> p j t u"))
+            groupeds[g] = grouped
+
+        def quantise(g):
             codes = work.tile([P, GROUP], U32, name="codes", align_bytes=64)
             scales = work.tile([P, GROUP], U8, name="scales", align_bytes=64)
-            nc.vector.quantize_mx(out=codes[:].bitcast(FP8X4), scales=scales[:], in_=grouped[:])
+            nc.vector.quantize_mx(out=codes[:].bitcast(FP8X4), scales=scales[:], in_=groupeds[g][:])
+            operands[g] = (codes, scales)
 
-            q_ps = psum_out.tile([P, TILES, HD], F32, name="q_ps")
-            k_ps = psum_out.tile([P, TILES, HD], F32, name="k_ps")
-            v_ps = psum_out.tile([P, TILES, HD], F32, name="v_ps")
+        def project(g):
+            codes, scales = operands[g]
+            banks[g] = [psum_out.tile([P, TILES, HD], F32, name=name) for name in ("even_ps", "odd_ps", "v_ps")]
             for j in range(TILES):
                 tokens = slice(j * P, (j + 1) * P)
-                for c, bank in enumerate((q_ps, k_ps, v_ps)):
+                for c, bank in enumerate(banks[g]):
                     nc.tensor.matmul_mx(
                         out=bank[:, j, :],
                         lhsT=codes[:, tokens].bitcast(FP8X4),
@@ -250,14 +252,52 @@ def tile_slidingwindowattention_pa_t_kernel(tc, x, ln_w, wq, wk, wv, out_0, out_
                         stop=True,
                     )
 
-            s = g % GROUPS_PER_SEQ
-            group_cos_sin = cos_sin[:, s * TILES : (s + 1) * TILES]
-            group_msin_cos = msin_cos[:, s * TILES : (s + 1) * TILES]
-            q_rot = rotate(nc, turn, "q", q_ps, group_cos_sin, group_msin_cos)
-            k_rot = rotate(nc, turn, "k", k_ps, group_cos_sin, group_msin_cos)
-            v_sb = turn.tile([P, TILES, HD], F32, name="v_sb")
-            nc.scalar.copy(out=v_sb[:], in_=v_ps[:])
+        def multiply(g):
+            shape = [P, TILES, 2, PAIRS, 2]
+            rows = slice((g % BLOCKS) * TILES, (g % BLOCKS + 1) * TILES)
+            products[g] = []
+            for bank, table, name in ((banks[g][0], cos_sin, "from_even"), (banks[g][1], msin_cos, "from_odd")):
+                product = work.tile(shape, F32, name=name)
+                nc.vector.tensor_tensor(
+                    out=product[:],
+                    in0=bank[:].rearrange("p j (c i) -> p j c i", c=2).unsqueeze(4).to_broadcast(shape),
+                    in1=table[:, rows].unsqueeze(2).to_broadcast(shape),
+                    op=ALU.mult,
+                )
+                products[g].append(product)
 
-            nc.sync.dma_start(out=q_groups[g], in_=q_rot[:].rearrange("p j i h -> p (j i h)"))
-            nc.sync.dma_start(out=k_groups[g], in_=k_rot[:].rearrange("p j i h -> p (j i h)"))
-            nc.sync.dma_start(out=v_groups[g], in_=v_sb[:].rearrange("p j d -> p (j d)"))
+        def copy_v(g):
+            v_sb = stores.tile([P, TILES * HD], F32, name="v_sb")
+            nc.scalar.copy(out=v_sb[:], in_=banks[g][2][:].rearrange("p j d -> p (j d)"))
+            v_copies[g] = v_sb
+
+        def add_and_store(g):
+            from_even, from_odd = products[g]
+            rotated = stores.tile([P, 2, TILES, HD], F32, name="rotated")
+            nc.gpsimd.tensor_tensor(
+                out=rotated[:].rearrange("p c j d -> p j c d"),
+                in0=from_even[:].rearrange("p j c i h -> p j c (i h)"),
+                in1=from_odd[:].rearrange("p j c i h -> p j c (i h)"),
+                op=ALU.add,
+            )
+            nc.sync.dma_start(out=q_groups[g], in_=rotated[:, 0].rearrange("p j d -> p (j d)"))
+            nc.sync.dma_start(out=k_groups[g], in_=rotated[:, 1].rearrange("p j d -> p (j d)"))
+            nc.sync.dma_start(out=v_groups[g], in_=v_copies[g][:])
+
+        def run(stage, index, count):
+            if 0 <= index < count:
+                stage(index)
+
+        for step in range(-4, GROUPS + 1):
+            run(mean_squares, step + 4, GROUPS)
+            run(project, step, GROUPS)
+            run(normalise, step + 2, GROUPS)
+            run(turn, step + 2, GROUPS)
+            run(add_and_store, step - 1, GROUPS)
+            run(copy_v, step, GROUPS)
+            run(quantise, step + 1, GROUPS)
+            run(regroup, step + 2, GROUPS)
+            run(sines, step + 2, BLOCKS)
+            run(inverse_rms, step + 4, GROUPS)
+            run(interleave, step + 2, BLOCKS)
+            run(multiply, step, GROUPS)

@@ -37,10 +37,7 @@ def broadcast_gain(nc, const, psum_const, gain_row):
     return gain
 
 
-def quantise_weights(nc, const, raw):
-    grouped = const.tile([P, 3, HD, PACK], BF16, name="w_grouped", align_bytes=64)
-    codes = const.tile([P, 3, HD], U32, name="w_codes", align_bytes=64)
-    scales = const.tile([P, 3, HD], U8, name="w_scales", align_bytes=64)
+def quantise_weights(nc, raw, grouped, codes, scales):
     for m in range(2):
         nc.vector.tensor_copy(
             out=grouped[:, 0:2, m * PAIRS : (m + 1) * PAIRS, :],
@@ -53,7 +50,6 @@ def quantise_weights(nc, const, raw):
             scales=scales[:, c],
             in_=grouped[:, c].rearrange("p n t -> p (n t)"),
         )
-    return codes, scales
 
 
 def rotation_angles(nc, const):
@@ -141,13 +137,15 @@ def tile_slidingwindowattention_pa_t_kernel(tc, x, ln_w, wq, wk, wv, out_0, out_
         for g in range(1, GROUPS):
             nc.sync.dma_start(out=x_tiles[g][:], in_=x_groups[g])
 
+        gain = broadcast_gain(nc, const, psum_const, gain_row)
+        minus_half = const.tile([P, TILES], F32, name="minus_half")
+        nc.vector.memset(minus_half[:], -0.5)
         part, quarter_less = rotation_angles(nc, const)
         identity = const.tile([P, P], F32, name="identity")
         make_identity(nc, identity[:])
-        minus_half = const.tile([P, TILES], F32, name="minus_half")
-        nc.vector.memset(minus_half[:], -0.5)
-        gain = broadcast_gain(nc, const, psum_const, gain_row)
-        w_codes, w_scales = quantise_weights(nc, const, w_raw)
+        w_grouped = const.tile([P, 3, HD, PACK], BF16, name="w_grouped", align_bytes=64)
+        w_codes = const.tile([P, 3, HD], U32, name="w_codes", align_bytes=64)
+        w_scales = const.tile([P, 3, HD], U8, name="w_scales", align_bytes=64)
 
         planes = const.tile([P, 3, BLOCKS * TILES * PAIRS], F32, name="planes")
         msin_cos = const.tile([P, BLOCKS * TILES, PAIRS, 2], F32, name="msin_cos")
@@ -252,19 +250,26 @@ def tile_slidingwindowattention_pa_t_kernel(tc, x, ln_w, wq, wk, wv, out_0, out_
                         stop=True,
                     )
 
-        def multiply(g):
+        def multiply(g, bank, table, name):
             shape = [P, TILES, 2, PAIRS, 2]
             rows = slice((g % BLOCKS) * TILES, (g % BLOCKS + 1) * TILES)
-            products[g] = []
-            for bank, table, name in ((banks[g][0], cos_sin, "from_even"), (banks[g][1], msin_cos, "from_odd")):
-                product = work.tile(shape, F32, name=name)
-                nc.vector.tensor_tensor(
-                    out=product[:],
-                    in0=bank[:].rearrange("p j (c i) -> p j c i", c=2).unsqueeze(4).to_broadcast(shape),
-                    in1=table[:, rows].unsqueeze(2).to_broadcast(shape),
-                    op=ALU.mult,
-                )
-                products[g].append(product)
+            product = work.tile(shape, F32, name=name)
+            nc.vector.tensor_tensor(
+                out=product[:],
+                in0=bank[:].rearrange("p j (c i) -> p j c i", c=2).unsqueeze(4).to_broadcast(shape),
+                in1=table[:, rows].unsqueeze(2).to_broadcast(shape),
+                op=ALU.mult,
+            )
+            return product
+
+        def multiply_even(g):
+            products[g] = [multiply(g, banks[g][0], cos_sin, "from_even")]
+
+        def multiply_odd(g):
+            products[g].append(multiply(g, banks[g][1], msin_cos, "from_odd"))
+
+        def prepare_weights(unused):
+            quantise_weights(nc, w_raw, w_grouped, w_codes, w_scales)
 
         def copy_v(g):
             v_sb = stores.tile([P, TILES * HD], F32, name="v_sb")
@@ -288,16 +293,18 @@ def tile_slidingwindowattention_pa_t_kernel(tc, x, ln_w, wq, wk, wv, out_0, out_
             if 0 <= index < count:
                 stage(index)
 
-        for step in range(-4, GROUPS + 1):
+        for step in range(-4, GROUPS):
             run(mean_squares, step + 4, GROUPS)
             run(project, step, GROUPS)
             run(normalise, step + 2, GROUPS)
+            run(prepare_weights, step + 2, 1)
             run(turn, step + 2, GROUPS)
-            run(add_and_store, step - 1, GROUPS)
             run(copy_v, step, GROUPS)
+            run(multiply_even, step, GROUPS)
             run(quantise, step + 1, GROUPS)
             run(regroup, step + 2, GROUPS)
             run(sines, step + 2, BLOCKS)
+            run(multiply_odd, step, GROUPS)
+            run(add_and_store, step, GROUPS)
             run(inverse_rms, step + 4, GROUPS)
             run(interleave, step + 2, BLOCKS)
-            run(multiply, step, GROUPS)

@@ -107,27 +107,29 @@ def rotation_angles(nc, const):
 def tile_slidingwindowattention_pa_t_kernel(tc, x, ln_w, wq, wk, wv, out_0, out_1, out_2):
     nc = tc.nc
     by_group = "(g p j) d -> g p (j d)"
-    x_groups = x.rearrange("b s d -> (b s) d").rearrange(by_group, p=P, j=TILES)
+    x_tiles_hbm = x.rearrange("b s d -> (b s) d").rearrange("(g p j) d -> g j p d", p=P, j=TILES)
     q_groups = out_0.rearrange("b s h d -> (b s h) d").rearrange(by_group, p=P, j=TILES)
     k_groups = out_1.rearrange("b s h d -> (b s h) d").rearrange(by_group, p=P, j=TILES)
     v_groups = out_2.rearrange("b s h d -> (b s h) d").rearrange(by_group, p=P, j=TILES)
 
     with ExitStack() as ctx:
         const = ctx.enter_context(tc.tile_pool(name="const", bufs=1))
-        loads = ctx.enter_context(tc.tile_pool(name="loads", bufs=GROUPS))
+        loads = ctx.enter_context(tc.tile_pool(name="loads", bufs=GROUPS * TILES))
         small = ctx.enter_context(tc.tile_pool(name="small", bufs=4))
         work = ctx.enter_context(tc.tile_pool(name="work", bufs=2))
         stores = ctx.enter_context(tc.tile_pool(name="stores", bufs=3))
         psum_const = ctx.enter_context(tc.psum_pool(name="psum_const", bufs=1))
-        psum_turned = ctx.enter_context(tc.psum_pool(name="psum_turned", bufs=4))
-        psum_out = ctx.enter_context(tc.psum_pool(name="psum_out", bufs=1))
+        psum_turned = ctx.enter_context(tc.psum_pool(name="psum_turned", bufs=2))
+        psum_pairs = ctx.enter_context(tc.psum_pool(name="psum_pairs", bufs=2))
+        psum_v = ctx.enter_context(tc.psum_pool(name="psum_v", bufs=1))
         ctx.enter_context(tc.manual_schedule())
 
-        x_tiles = [loads.tile([P, TILES * D], BF16, name="x_t") for g in range(GROUPS)]
+        x_tiles = [[loads.tile([P, D], BF16, name="x_t") for j in range(TILES)] for g in range(GROUPS)]
         gain_row = const.tile([P, D], BF16, name="gain_row")
         w_raw = const.tile([P, 3, PACK, HD], BF16, name="w_raw")
         nc.vector.memset(gain_row[:], 0.0)
-        nc.sync.dma_start(out=x_tiles[0][:], in_=x_groups[0])
+        for j in range(TILES):
+            nc.sync.dma_start(out=x_tiles[0][j][:], in_=x_tiles_hbm[0, j])
         nc.sync.dma_start(out=gain_row[0:1, :], in_=ln_w.rearrange("(o d) -> o d", o=1))
         for m, w in enumerate((wq, wk, wv)):
             nc.sync.dma_start(
@@ -135,7 +137,8 @@ def tile_slidingwindowattention_pa_t_kernel(tc, x, ln_w, wq, wk, wv, out_0, out_
                 in_=w.rearrange("(u p e) n -> p u (e n)", u=2, e=2),
             )
         for g in range(1, GROUPS):
-            nc.sync.dma_start(out=x_tiles[g][:], in_=x_groups[g])
+            for j in range(TILES):
+                nc.sync.dma_start(out=x_tiles[g][j][:], in_=x_tiles_hbm[g, j])
 
         gain = broadcast_gain(nc, const, psum_const, gain_row)
         minus_half = const.tile([P, TILES], F32, name="minus_half")
@@ -146,6 +149,7 @@ def tile_slidingwindowattention_pa_t_kernel(tc, x, ln_w, wq, wk, wv, out_0, out_
         w_grouped = const.tile([P, 3, HD, PACK], BF16, name="w_grouped", align_bytes=64)
         w_codes = const.tile([P, 3, HD], U32, name="w_codes", align_bytes=64)
         w_scales = const.tile([P, 3, HD], U8, name="w_scales", align_bytes=64)
+        quantise_weights(nc, w_raw, w_grouped, w_codes, w_scales)
 
         planes = const.tile([P, 3, BLOCKS * TILES * PAIRS], F32, name="planes")
         msin_cos = const.tile([P, BLOCKS * TILES, PAIRS, 2], F32, name="msin_cos")
@@ -181,7 +185,7 @@ def tile_slidingwindowattention_pa_t_kernel(tc, x, ln_w, wq, wk, wv, out_0, out_
                 cols = slice(j * D, (j + 1) * D)
                 nc.scalar.activation(
                     out=squares[:, cols],
-                    in_=x_tiles[g][:, cols],
+                    in_=x_tiles[g][j][:],
                     func=ACT.Square,
                     scale=1.0 / math.sqrt(D),
                     accum_out=mean_sq[:, j : j + 1],
@@ -203,7 +207,7 @@ def tile_slidingwindowattention_pa_t_kernel(tc, x, ln_w, wq, wk, wv, out_0, out_
                 cols = slice(j * D, (j + 1) * D)
                 nc.vector.scalar_tensor_tensor(
                     out=xn[:, cols],
-                    in0=x_tiles[g][:, cols],
+                    in0=x_tiles[g][j][:],
                     scalar=rstds[g][:, j : j + 1],
                     in1=gain[:],
                     op0=ALU.mult,
@@ -236,10 +240,14 @@ def tile_slidingwindowattention_pa_t_kernel(tc, x, ln_w, wq, wk, wv, out_0, out_
 
         def project(g):
             codes, scales = operands[g]
-            banks[g] = [psum_out.tile([P, TILES, HD], F32, name=name) for name in ("even_ps", "odd_ps", "v_ps")]
-            for j in range(TILES):
-                tokens = slice(j * P, (j + 1) * P)
-                for c, bank in enumerate(banks[g]):
+            banks[g] = [
+                psum_pairs.tile([P, TILES, HD], F32, name="even_ps"),
+                psum_pairs.tile([P, TILES, HD], F32, name="odd_ps"),
+                psum_v.tile([P, TILES, HD], F32, name="v_ps"),
+            ]
+            for c, bank in enumerate(banks[g]):
+                for j in range(TILES):
+                    tokens = slice(j * P, (j + 1) * P)
                     nc.tensor.matmul_mx(
                         out=bank[:, j, :],
                         lhsT=codes[:, tokens].bitcast(FP8X4),
@@ -268,9 +276,6 @@ def tile_slidingwindowattention_pa_t_kernel(tc, x, ln_w, wq, wk, wv, out_0, out_
         def multiply_odd(g):
             products[g].append(multiply(g, banks[g][1], msin_cos, "from_odd"))
 
-        def prepare_weights(unused):
-            quantise_weights(nc, w_raw, w_grouped, w_codes, w_scales)
-
         def copy_v(g):
             v_sb = stores.tile([P, TILES * HD], F32, name="v_sb")
             nc.scalar.copy(out=v_sb[:], in_=banks[g][2][:].rearrange("p j d -> p (j d)"))
@@ -279,7 +284,8 @@ def tile_slidingwindowattention_pa_t_kernel(tc, x, ln_w, wq, wk, wv, out_0, out_
         def add_and_store(g):
             from_even, from_odd = products[g]
             rotated = stores.tile([P, 2, TILES, HD], F32, name="rotated")
-            nc.gpsimd.tensor_tensor(
+            adder = nc.vector if g == GROUPS - 1 else nc.gpsimd
+            adder.tensor_tensor(
                 out=rotated[:].rearrange("p c j d -> p j c d"),
                 in0=from_even[:].rearrange("p j c i h -> p j c (i h)"),
                 in1=from_odd[:].rearrange("p j c i h -> p j c (i h)"),
@@ -294,17 +300,16 @@ def tile_slidingwindowattention_pa_t_kernel(tc, x, ln_w, wq, wk, wv, out_0, out_
                 stage(index)
 
         for step in range(-4, GROUPS):
-            run(mean_squares, step + 4, GROUPS)
-            run(project, step, GROUPS)
-            run(normalise, step + 2, GROUPS)
-            run(prepare_weights, step + 2, 1)
-            run(turn, step + 2, GROUPS)
             run(copy_v, step, GROUPS)
+            run(mean_squares, step + 4, GROUPS)
+            run(normalise, step + 2, GROUPS)
+            run(turn, step + 2, GROUPS)
             run(multiply_even, step, GROUPS)
             run(quantise, step + 1, GROUPS)
+            run(project, step + 1, GROUPS)
             run(regroup, step + 2, GROUPS)
-            run(sines, step + 2, BLOCKS)
+            run(sines, step + 3, BLOCKS)
             run(multiply_odd, step, GROUPS)
             run(add_and_store, step, GROUPS)
             run(inverse_rms, step + 4, GROUPS)
-            run(interleave, step + 2, BLOCKS)
+            run(interleave, step + 3, BLOCKS)

@@ -39,16 +39,17 @@ def broadcast_gain(nc, const, psum_const, gain_row):
 
 def quantise_weights(nc, raw, grouped, codes, scales):
     for m in range(2):
-        nc.vector.tensor_copy(
-            out=grouped[:, 0:2, m * PAIRS : (m + 1) * PAIRS, :],
-            in_=raw[:, m].rearrange("p t (i h) -> p h i t", h=2),
-        )
-    nc.vector.tensor_copy(out=grouped[:, 2], in_=raw[:, 2].rearrange("p t n -> p n t"))
-    for c in range(3):
+        halves = raw[:, m].rearrange("p t (i h) -> p h i t", h=2)
+        nc.vector.tensor_copy(out=grouped[:, 0:2, m * PAIRS : (m + 1) * PAIRS, :], in_=halves)
+        swapped = grouped[:, 2 + m].rearrange("p (i h) t -> p h i t", h=2)
+        nc.vector.tensor_copy(out=swapped[:, 0], in_=halves[:, 1])
+        nc.vector.tensor_copy(out=swapped[:, 1], in_=halves[:, 0])
+    nc.vector.tensor_copy(out=grouped[:, 4], in_=raw[:, 2].rearrange("p t n -> p n t"))
+    for operands in (slice(0, 4), slice(4, 5)):
         nc.vector.quantize_mx(
-            out=codes[:, c].bitcast(FP8X4),
-            scales=scales[:, c],
-            in_=grouped[:, c].rearrange("p n t -> p (n t)"),
+            out=codes[:, operands].rearrange("p c n -> p (c n)").bitcast(FP8X4),
+            scales=scales[:, operands].rearrange("p c n -> p (c n)"),
+            in_=grouped[:, operands].rearrange("p c n t -> p (c n t)"),
         )
 
 
@@ -120,8 +121,8 @@ def tile_slidingwindowattention_pa_t_kernel(tc, x, ln_w, wq, wk, wv, out_0, out_
         stores = ctx.enter_context(tc.tile_pool(name="stores", bufs=3))
         psum_const = ctx.enter_context(tc.psum_pool(name="psum_const", bufs=1))
         psum_turned = ctx.enter_context(tc.psum_pool(name="psum_turned", bufs=2))
-        psum_pairs = ctx.enter_context(tc.psum_pool(name="psum_pairs", bufs=2))
-        psum_v = ctx.enter_context(tc.psum_pool(name="psum_v", bufs=1))
+        psum_sums = ctx.enter_context(tc.psum_pool(name="psum_sums", bufs=2))
+        psum_out = ctx.enter_context(tc.psum_pool(name="psum_out", bufs=1))
         ctx.enter_context(tc.manual_schedule())
 
         x_tiles = [[loads.tile([P, D], BF16, name="x_t") for j in range(TILES)] for g in range(GROUPS)]
@@ -146,14 +147,13 @@ def tile_slidingwindowattention_pa_t_kernel(tc, x, ln_w, wq, wk, wv, out_0, out_
         part, quarter_less = rotation_angles(nc, const)
         identity = const.tile([P, P], F32, name="identity")
         make_identity(nc, identity[:])
-        w_grouped = const.tile([P, 3, HD, PACK], BF16, name="w_grouped", align_bytes=64)
-        w_codes = const.tile([P, 3, HD], U32, name="w_codes", align_bytes=64)
-        w_scales = const.tile([P, 3, HD], U8, name="w_scales", align_bytes=64)
+        w_grouped = const.tile([P, 5, HD, PACK], BF16, name="w_grouped", align_bytes=64)
+        w_codes = const.tile([P, 5, HD], U32, name="w_codes", align_bytes=64)
+        w_scales = const.tile([P, 5, HD], U8, name="w_scales", align_bytes=64)
         quantise_weights(nc, w_raw, w_grouped, w_codes, w_scales)
 
         planes = const.tile([P, 3, BLOCKS * TILES * PAIRS], F32, name="planes")
-        msin_cos = const.tile([P, BLOCKS * TILES, PAIRS, 2], F32, name="msin_cos")
-        cos_sin = const.tile([P, BLOCKS * TILES, PAIRS, 2], F32, name="cos_sin")
+        cross = const.tile([P, BLOCKS * TILES, PAIRS, 2], F32, name="cross")
 
         def sines(s):
             rows = slice(s * TILES, (s + 1) * TILES)
@@ -163,17 +163,15 @@ def tile_slidingwindowattention_pa_t_kernel(tc, x, ln_w, wq, wk, wv, out_0, out_
                     out=planes[:, plane, cols], in_=angle[:, rows].rearrange("p j i -> p (j i)"), func=ACT.Sin, scale=scale
                 )
 
-        def interleave(s):
+        def cross_terms(s):
             rows = slice(s * TILES, (s + 1) * TILES)
             cols = slice(s * TILES * PAIRS, (s + 1) * TILES * PAIRS)
-            for table, first in ((cos_sin, 1), (msin_cos, 0)):
-                nc.gpsimd.tensor_scalar(
-                    out=table[:, rows].rearrange("p j i h -> p (j i) h"),
-                    in0=planes[:, first : first + 2, cols].rearrange("p h n -> p n h"),
-                    scalar1=1.0,
-                    scalar2=0.0,
-                    op0=ALU.mult,
-                    op1=ALU.add,
+            for h, plane in ((0, 0), (1, 2)):
+                nc.gpsimd.tensor_tensor(
+                    out=cross[:, rows, :, h],
+                    in0=planes[:, plane, cols].rearrange("p (j i) -> p j i", j=TILES),
+                    in1=planes[:, 1, cols].rearrange("p (j i) -> p j i", j=TILES),
+                    op=ALU.subtract,
                 )
 
         rstds, xns, turneds, groupeds, operands, banks, products, v_copies = {}, {}, {}, {}, {}, {}, {}, {}
@@ -240,59 +238,86 @@ def tile_slidingwindowattention_pa_t_kernel(tc, x, ln_w, wq, wk, wv, out_0, out_
 
         def project(g):
             codes, scales = operands[g]
-            banks[g] = [
-                psum_pairs.tile([P, TILES, HD], F32, name="even_ps"),
-                psum_pairs.tile([P, TILES, HD], F32, name="odd_ps"),
-                psum_v.tile([P, TILES, HD], F32, name="v_ps"),
-            ]
-            for c, bank in enumerate(banks[g]):
+
+            def passes(bank, operand, start, stop):
                 for j in range(TILES):
                     tokens = slice(j * P, (j + 1) * P)
                     nc.tensor.matmul_mx(
                         out=bank[:, j, :],
                         lhsT=codes[:, tokens].bitcast(FP8X4),
                         lhsT_scale=scales[:, tokens],
-                        rhs=w_codes[:, c].bitcast(FP8X4),
-                        rhs_scale=w_scales[:, c],
-                        start=True,
-                        stop=True,
+                        rhs=w_codes[:, operand].bitcast(FP8X4),
+                        rhs_scale=w_scales[:, operand],
+                        start=start,
+                        stop=stop,
                     )
 
-        def multiply(g, bank, table, name):
-            shape = [P, TILES, 2, PAIRS, 2]
+            sum_ps = psum_sums.tile([P, TILES, HD], F32, name="sum_ps")
+            for j in range(TILES):
+                tokens = slice(j * P, (j + 1) * P)
+                for operand in range(2):
+                    nc.tensor.matmul_mx(
+                        out=sum_ps[:, j, :],
+                        lhsT=codes[:, tokens].bitcast(FP8X4),
+                        lhsT_scale=scales[:, tokens],
+                        rhs=w_codes[:, operand].bitcast(FP8X4),
+                        rhs_scale=w_scales[:, operand],
+                        start=(operand == 0),
+                        stop=(operand == 1),
+                    )
+            v_ps = psum_out.tile([P, TILES, HD], F32, name="v_ps")
+            q_ps = psum_out.tile([P, TILES, HD], F32, name="q_ps")
+            k_ps = psum_out.tile([P, TILES, HD], F32, name="k_ps")
+            passes(v_ps, 4, True, True)
+            passes(q_ps, 2, True, True)
+            passes(k_ps, 3, True, True)
+            banks[g] = (sum_ps, q_ps, k_ps, v_ps)
+
+        def multiply_shared(g):
             rows = slice((g % BLOCKS) * TILES, (g % BLOCKS + 1) * TILES)
-            product = work.tile(shape, F32, name=name)
+            shape = [P, TILES, 2, PAIRS]
+            shared = work.tile([P, 2, TILES, PAIRS], F32, name="shared")
             nc.vector.tensor_tensor(
-                out=product[:],
-                in0=bank[:].rearrange("p j (c i) -> p j c i", c=2).unsqueeze(4).to_broadcast(shape),
-                in1=table[:, rows].unsqueeze(2).to_broadcast(shape),
+                out=shared[:].rearrange("p c j i -> p j c i"),
+                in0=banks[g][0][:].rearrange("p j (c i) -> p j c i", c=2),
+                in1=planes[:, 1].rearrange("p (s i) -> p s i", i=PAIRS)[:, rows].unsqueeze(2).to_broadcast(shape),
                 op=ALU.mult,
             )
-            return product
+            own = work.tile([P, 2, TILES, PAIRS, 2], F32, name="own")
+            products[g] = (shared, own)
 
-        def multiply_even(g):
-            products[g] = [multiply(g, banks[g][0], cos_sin, "from_even")]
+        def multiply_own(g, c):
+            rows = slice((g % BLOCKS) * TILES, (g % BLOCKS + 1) * TILES)
+            nc.vector.tensor_tensor(
+                out=products[g][1][:, c],
+                in0=banks[g][1 + c][:].rearrange("p j (i h) -> p j i h", h=2),
+                in1=cross[:, rows],
+                op=ALU.mult,
+            )
 
-        def multiply_odd(g):
-            products[g].append(multiply(g, banks[g][1], msin_cos, "from_odd"))
+        def multiply_own_q(g):
+            multiply_own(g, 0)
+
+        def multiply_own_k(g):
+            multiply_own(g, 1)
 
         def copy_v(g):
             v_sb = stores.tile([P, TILES * HD], F32, name="v_sb")
-            nc.scalar.copy(out=v_sb[:], in_=banks[g][2][:].rearrange("p j d -> p (j d)"))
+            nc.scalar.copy(out=v_sb[:], in_=banks[g][3][:].rearrange("p j d -> p (j d)"))
             v_copies[g] = v_sb
 
         def add_and_store(g):
-            from_even, from_odd = products[g]
-            rotated = stores.tile([P, 2, TILES, HD], F32, name="rotated")
+            shared, own = products[g]
+            rotated = stores.tile([P, 2, TILES, PAIRS, 2], F32, name="rotated")
             adder = nc.vector if g == GROUPS - 1 else nc.gpsimd
             adder.tensor_tensor(
-                out=rotated[:].rearrange("p c j d -> p j c d"),
-                in0=from_even[:].rearrange("p j c i h -> p j c (i h)"),
-                in1=from_odd[:].rearrange("p j c i h -> p j c (i h)"),
+                out=rotated[:],
+                in0=shared[:].unsqueeze(4).to_broadcast([P, 2, TILES, PAIRS, 2]),
+                in1=own[:],
                 op=ALU.add,
             )
-            nc.sync.dma_start(out=q_groups[g], in_=rotated[:, 0].rearrange("p j d -> p (j d)"))
-            nc.sync.dma_start(out=k_groups[g], in_=rotated[:, 1].rearrange("p j d -> p (j d)"))
+            nc.sync.dma_start(out=q_groups[g], in_=rotated[:, 0].rearrange("p j i h -> p (j i h)"))
+            nc.sync.dma_start(out=k_groups[g], in_=rotated[:, 1].rearrange("p j i h -> p (j i h)"))
             nc.sync.dma_start(out=v_groups[g], in_=v_copies[g][:])
 
         def run(stage, index, count):
@@ -304,12 +329,13 @@ def tile_slidingwindowattention_pa_t_kernel(tc, x, ln_w, wq, wk, wv, out_0, out_
             run(mean_squares, step + 4, GROUPS)
             run(normalise, step + 2, GROUPS)
             run(turn, step + 2, GROUPS)
-            run(multiply_even, step, GROUPS)
+            run(multiply_shared, step, GROUPS)
+            run(multiply_own_q, step, GROUPS)
             run(quantise, step + 1, GROUPS)
-            run(project, step + 1, GROUPS)
             run(regroup, step + 2, GROUPS)
             run(sines, step + 3, BLOCKS)
-            run(multiply_odd, step, GROUPS)
+            run(multiply_own_k, step, GROUPS)
+            run(project, step + 1, GROUPS)
             run(add_and_store, step, GROUPS)
             run(inverse_rms, step + 4, GROUPS)
-            run(interleave, step + 3, BLOCKS)
+            run(cross_terms, step + 3, BLOCKS)

@@ -31,7 +31,7 @@ FLOPS = 2 * BATCH * SEQ * D * 3 * HD
 
 def broadcast_gain(nc, const, psum_const, gain_row):
     ones = const.tile([P, P], BF16, name="ones")
-    nc.vector.memset(ones[:], 1.0)
+    nc.gpsimd.memset(ones[:], 1.0)
     gain = psum_const.tile([P, D], F32, name="gain")
     nc.tensor.matmul(out=gain[:], lhsT=ones[:], rhs=gain_row[:], start=True, stop=True)
     return gain
@@ -60,7 +60,7 @@ def rotation_angles(nc, const):
     nc.vector.tensor_copy(out=position[:], in_=position_int[:])
 
     one = const.tile([P, 1], F32, name="one")
-    nc.vector.memset(one[:], 1.0)
+    nc.gpsimd.memset(one[:], 1.0)
     coarse = const.tile([P, 8], F32, name="coarse")
     fine = const.tile([P, 8], F32, name="fine")
     for a in range(8):
@@ -125,10 +125,12 @@ def tile_slidingwindowattention_pa_t_kernel(tc, x, ln_w, wq, wk, wv, out_0, out_
         psum_out = ctx.enter_context(tc.psum_pool(name="psum_out", bufs=1))
         ctx.enter_context(tc.manual_schedule())
 
+        part, quarter_less = rotation_angles(nc, const)
+
         x_tiles = [[loads.tile([P, D], BF16, name="x_t") for j in range(TILES)] for g in range(GROUPS)]
         gain_row = const.tile([P, D], BF16, name="gain_row")
         w_raw = const.tile([P, 3, PACK, HD], BF16, name="w_raw")
-        nc.vector.memset(gain_row[:], 0.0)
+        nc.gpsimd.memset(gain_row[:], 0.0)
         for j in range(TILES):
             nc.sync.dma_start(out=x_tiles[0][j][:], in_=x_tiles_hbm[0, j])
         nc.sync.dma_start(out=gain_row[0:1, :], in_=ln_w.rearrange("(o d) -> o d", o=1))
@@ -143,8 +145,7 @@ def tile_slidingwindowattention_pa_t_kernel(tc, x, ln_w, wq, wk, wv, out_0, out_
 
         gain = broadcast_gain(nc, const, psum_const, gain_row)
         minus_half = const.tile([P, TILES], F32, name="minus_half")
-        nc.vector.memset(minus_half[:], -0.5)
-        part, quarter_less = rotation_angles(nc, const)
+        nc.gpsimd.memset(minus_half[:], -0.5)
         identity = const.tile([P, P], F32, name="identity")
         make_identity(nc, identity[:])
         w_grouped = const.tile([P, 5, HD, PACK], BF16, name="w_grouped", align_bytes=64)
@@ -252,6 +253,11 @@ def tile_slidingwindowattention_pa_t_kernel(tc, x, ln_w, wq, wk, wv, out_0, out_
                         stop=stop,
                     )
 
+            q_ps = psum_out.tile([P, TILES, HD], F32, name="q_ps")
+            k_ps = psum_out.tile([P, TILES, HD], F32, name="k_ps")
+            v_ps = psum_out.tile([P, TILES, HD], F32, name="v_ps")
+            passes(q_ps, 2, True, True)
+            passes(k_ps, 3, True, True)
             sum_ps = psum_sums.tile([P, TILES, HD], F32, name="sum_ps")
             for j in range(TILES):
                 tokens = slice(j * P, (j + 1) * P)
@@ -265,12 +271,7 @@ def tile_slidingwindowattention_pa_t_kernel(tc, x, ln_w, wq, wk, wv, out_0, out_
                         start=(operand == 0),
                         stop=(operand == 1),
                     )
-            v_ps = psum_out.tile([P, TILES, HD], F32, name="v_ps")
-            q_ps = psum_out.tile([P, TILES, HD], F32, name="q_ps")
-            k_ps = psum_out.tile([P, TILES, HD], F32, name="k_ps")
             passes(v_ps, 4, True, True)
-            passes(q_ps, 2, True, True)
-            passes(k_ps, 3, True, True)
             banks[g] = (sum_ps, q_ps, k_ps, v_ps)
 
         def multiply_shared(g):
@@ -283,19 +284,19 @@ def tile_slidingwindowattention_pa_t_kernel(tc, x, ln_w, wq, wk, wv, out_0, out_
                 in1=planes[:, 1].rearrange("p (s i) -> p s i", i=PAIRS)[:, rows].unsqueeze(2).to_broadcast(shape),
                 op=ALU.mult,
             )
-            own = work.tile([P, 2, TILES, PAIRS, 2], F32, name="own")
-            products[g] = (shared, own)
+            products[g].append(shared)
 
         def multiply_own(g, c):
             rows = slice((g % BLOCKS) * TILES, (g % BLOCKS + 1) * TILES)
             nc.vector.tensor_tensor(
-                out=products[g][1][:, c],
+                out=products[g][0][:, c],
                 in0=banks[g][1 + c][:].rearrange("p j (i h) -> p j i h", h=2),
                 in1=cross[:, rows],
                 op=ALU.mult,
             )
 
         def multiply_own_q(g):
+            products[g] = [work.tile([P, 2, TILES, PAIRS, 2], F32, name="own")]
             multiply_own(g, 0)
 
         def multiply_own_k(g):
@@ -307,7 +308,7 @@ def tile_slidingwindowattention_pa_t_kernel(tc, x, ln_w, wq, wk, wv, out_0, out_
             v_copies[g] = v_sb
 
         def add_and_store(g):
-            shared, own = products[g]
+            own, shared = products[g]
             rotated = stores.tile([P, 2, TILES, PAIRS, 2], F32, name="rotated")
             adder = nc.vector if g == GROUPS - 1 else nc.gpsimd
             adder.tensor_tensor(
@@ -329,13 +330,13 @@ def tile_slidingwindowattention_pa_t_kernel(tc, x, ln_w, wq, wk, wv, out_0, out_
             run(mean_squares, step + 4, GROUPS)
             run(normalise, step + 2, GROUPS)
             run(turn, step + 2, GROUPS)
-            run(multiply_shared, step, GROUPS)
             run(multiply_own_q, step, GROUPS)
+            run(multiply_own_k, step, GROUPS)
             run(quantise, step + 1, GROUPS)
+            run(project, step + 1, GROUPS)
             run(regroup, step + 2, GROUPS)
             run(sines, step + 3, BLOCKS)
-            run(multiply_own_k, step, GROUPS)
-            run(project, step + 1, GROUPS)
+            run(multiply_shared, step, GROUPS)
             run(add_and_store, step, GROUPS)
             run(inverse_rms, step + 4, GROUPS)
             run(cross_terms, step + 3, BLOCKS)

@@ -24,6 +24,7 @@ TILES = 4
 GROUP = TILES * P
 GROUPS = BATCH * SEQ // GROUP
 BLOCKS = SEQ // GROUP
+FIRST_ON_SCALAR = 8
 ROUND_TO_INTEGER = 1.5 * 2.0**23
 
 FLOPS = 2 * BATCH * SEQ * D * 3 * HD
@@ -125,6 +126,11 @@ def tile_slidingwindowattention_pa_t_kernel(tc, x, ln_w, wq, wk, wv, out_0, out_
         psum_out = ctx.enter_context(tc.psum_pool(name="psum_out", bufs=1))
         ctx.enter_context(tc.manual_schedule())
 
+        unit = const.tile([P, 1], F32, name="unit")
+        nc.gpsimd.memset(unit[:], 1.0)
+        eps = const.tile([P, 1], F32, name="eps")
+        nc.vector.tensor_scalar_mul(out=eps[:], in0=unit[:], scalar1=EPS)
+
         part, quarter_less = rotation_angles(nc, const)
 
         x_tiles = [[loads.tile([P, D], BF16, name="x_t") for j in range(TILES)] for g in range(GROUPS)]
@@ -190,6 +196,10 @@ def tile_slidingwindowattention_pa_t_kernel(tc, x, ln_w, wq, wk, wv, out_0, out_
                     accum_out=mean_sq[:, j : j + 1],
                 )
             rstds[g] = mean_sq
+            if g >= FIRST_ON_SCALAR:
+                rstd = small.tile([P, TILES], F32, name="rstd")
+                nc.scalar.activation(out=rstd[:], in_=mean_sq[:], func=ACT.Abs_reciprocal_sqrt, bias=eps[:], scale=1.0)
+                rstds[g] = rstd
 
         def inverse_rms(g):
             shifted = small.tile([P, TILES], F32, name="shifted")
@@ -338,5 +348,5 @@ def tile_slidingwindowattention_pa_t_kernel(tc, x, ln_w, wq, wk, wv, out_0, out_
             run(sines, step + 3, BLOCKS)
             run(multiply_shared, step, GROUPS)
             run(add_and_store, step, GROUPS)
-            run(inverse_rms, step + 4, GROUPS)
+            run(inverse_rms, step + 4, FIRST_ON_SCALAR)
             run(cross_terms, step + 3, BLOCKS)

@@ -38,14 +38,17 @@ def broadcast_gain(nc, const, psum_const, gain_row):
     return gain
 
 
-def quantise_weights(nc, raw, grouped, codes, scales):
-    for m in range(2):
-        halves = raw[:, m].rearrange("p t (i h) -> p h i t", h=2)
-        nc.vector.tensor_copy(out=grouped[:, 0:2, m * PAIRS : (m + 1) * PAIRS, :], in_=halves)
-        swapped = grouped[:, 2 + m].rearrange("p (i h) t -> p h i t", h=2)
-        nc.vector.tensor_copy(out=swapped[:, 0], in_=halves[:, 1])
-        nc.vector.tensor_copy(out=swapped[:, 1], in_=halves[:, 0])
+def group_weights(nc, raw, grouped):
+    halves = raw[:, 0:2].rearrange("p m t (i h) -> p h m i t", h=2)
+    swapped = grouped[:, 2:4].rearrange("p m (i h) t -> p h m i t", h=2)
+    for h in range(2):
+        nc.vector.tensor_copy(out=grouped[:, h].rearrange("p (m i) t -> p m i t", m=2), in_=halves[:, h])
+    nc.vector.tensor_scalar_mul(out=swapped[:, 0], in0=halves[:, 1], scalar1=-1.0)
+    nc.vector.tensor_copy(out=swapped[:, 1], in_=halves[:, 0])
     nc.vector.tensor_copy(out=grouped[:, 4], in_=raw[:, 2].rearrange("p t n -> p n t"))
+
+
+def quantise_weights(nc, grouped, codes, scales):
     for operands in (slice(0, 4), slice(4, 5)):
         nc.vector.quantize_mx(
             out=codes[:, operands].rearrange("p c n -> p (c n)").bitcast(FP8X4),
@@ -101,9 +104,7 @@ def rotation_angles(nc, const):
     nc.vector.scalar_tensor_tensor(
         out=minus_abs[:], in0=part[:], scalar=-1.0, in1=part[:], op0=ALU.mult, op1=ALU.min
     )
-    quarter_less = const.tile(shape, F32, name="quarter_less")
-    nc.vector.tensor_scalar_add(out=quarter_less[:], in0=minus_abs[:], scalar1=0.25)
-    return part, quarter_less
+    return part, minus_abs
 
 
 def tile_slidingwindowattention_pa_t_kernel(tc, x, ln_w, wq, wk, wv, out_0, out_1, out_2):
@@ -131,7 +132,12 @@ def tile_slidingwindowattention_pa_t_kernel(tc, x, ln_w, wq, wk, wv, out_0, out_
         eps = const.tile([P, 1], F32, name="eps")
         nc.vector.tensor_scalar_mul(out=eps[:], in0=unit[:], scalar1=EPS)
 
-        part, quarter_less = rotation_angles(nc, const)
+        quarter_turn = const.tile([P, 1], F32, name="quarter_turn")
+        nc.vector.tensor_scalar_mul(out=quarter_turn[:], in0=unit[:], scalar1=0.5 * math.pi)
+        zero = const.tile([P, 1], F32, name="zero")
+        nc.gpsimd.memset(zero[:], 0.0)
+
+        part, minus_abs = rotation_angles(nc, const)
 
         x_tiles = [[loads.tile([P, D], BF16, name="x_t") for j in range(TILES)] for g in range(GROUPS)]
         gain_row = const.tile([P, D], BF16, name="gain_row")
@@ -157,31 +163,35 @@ def tile_slidingwindowattention_pa_t_kernel(tc, x, ln_w, wq, wk, wv, out_0, out_
         w_grouped = const.tile([P, 5, HD, PACK], BF16, name="w_grouped", align_bytes=64)
         w_codes = const.tile([P, 5, HD], U32, name="w_codes", align_bytes=64)
         w_scales = const.tile([P, 5, HD], U8, name="w_scales", align_bytes=64)
-        quantise_weights(nc, w_raw, w_grouped, w_codes, w_scales)
+        group_weights(nc, w_raw, w_grouped)
 
-        planes = const.tile([P, 3, BLOCKS * TILES * PAIRS], F32, name="planes")
+        planes = const.tile([P, 2, BLOCKS * TILES * PAIRS], F32, name="planes")
         cross = const.tile([P, BLOCKS * TILES, PAIRS, 2], F32, name="cross")
 
         def sines(s):
             rows = slice(s * TILES, (s + 1) * TILES)
             cols = slice(s * TILES * PAIRS, (s + 1) * TILES * PAIRS)
-            for plane, angle, scale in ((0, part, -2.0 * math.pi), (1, quarter_less, 2.0 * math.pi), (2, part, 2.0 * math.pi)):
+            for plane, angle, bias in ((0, minus_abs, quarter_turn), (1, part, zero)):
                 nc.scalar.activation(
-                    out=planes[:, plane, cols], in_=angle[:, rows].rearrange("p j i -> p (j i)"), func=ACT.Sin, scale=scale
+                    out=planes[:, plane, cols],
+                    in_=angle[:, rows].rearrange("p j i -> p (j i)"),
+                    func=ACT.Sin,
+                    bias=bias[:],
+                    scale=2.0 * math.pi,
                 )
 
         def cross_terms(s):
             rows = slice(s * TILES, (s + 1) * TILES)
             cols = slice(s * TILES * PAIRS, (s + 1) * TILES * PAIRS)
-            for h, plane in ((0, 0), (1, 2)):
+            for h, op in ((0, ALU.add), (1, ALU.subtract)):
                 nc.gpsimd.tensor_tensor(
                     out=cross[:, rows, :, h],
-                    in0=planes[:, plane, cols].rearrange("p (j i) -> p j i", j=TILES),
-                    in1=planes[:, 1, cols].rearrange("p (j i) -> p j i", j=TILES),
-                    op=ALU.subtract,
+                    in0=planes[:, 1, cols].rearrange("p (j i) -> p j i", j=TILES),
+                    in1=planes[:, 0, cols].rearrange("p (j i) -> p j i", j=TILES),
+                    op=op,
                 )
 
-        rstds, xns, turneds, groupeds, operands, banks, products, v_copies = {}, {}, {}, {}, {}, {}, {}, {}
+        rstds, xns, turneds, groupeds, operands, banks, products = {}, {}, {}, {}, {}, {}, {}
 
         def mean_squares(g):
             mean_sq = small.tile([P, TILES], F32, name="mean_sq")
@@ -291,7 +301,7 @@ def tile_slidingwindowattention_pa_t_kernel(tc, x, ln_w, wq, wk, wv, out_0, out_
             nc.vector.tensor_tensor(
                 out=shared[:].rearrange("p c j i -> p j c i"),
                 in0=banks[g][0][:].rearrange("p j (c i) -> p j c i", c=2),
-                in1=planes[:, 1].rearrange("p (s i) -> p s i", i=PAIRS)[:, rows].unsqueeze(2).to_broadcast(shape),
+                in1=planes[:, 0].rearrange("p (s i) -> p s i", i=PAIRS)[:, rows].unsqueeze(2).to_broadcast(shape),
                 op=ALU.mult,
             )
             products[g].append(shared)
@@ -315,21 +325,27 @@ def tile_slidingwindowattention_pa_t_kernel(tc, x, ln_w, wq, wk, wv, out_0, out_
         def copy_v(g):
             v_sb = stores.tile([P, TILES * HD], F32, name="v_sb")
             nc.scalar.copy(out=v_sb[:], in_=banks[g][3][:].rearrange("p j d -> p (j d)"))
-            v_copies[g] = v_sb
+            nc.sync.dma_start(out=v_groups[g], in_=v_sb[:])
 
         def add_and_store(g):
             own, shared = products[g]
             rotated = stores.tile([P, 2, TILES, PAIRS, 2], F32, name="rotated")
-            adder = nc.vector if g == GROUPS - 1 else nc.gpsimd
-            adder.tensor_tensor(
-                out=rotated[:],
-                in0=shared[:].unsqueeze(4).to_broadcast([P, 2, TILES, PAIRS, 2]),
-                in1=own[:],
-                op=ALU.add,
-            )
-            nc.sync.dma_start(out=q_groups[g], in_=rotated[:, 0].rearrange("p j i h -> p (j i h)"))
-            nc.sync.dma_start(out=k_groups[g], in_=rotated[:, 1].rearrange("p j i h -> p (j i h)"))
-            nc.sync.dma_start(out=v_groups[g], in_=v_copies[g][:])
+            if g < GROUPS - 1:
+                nc.gpsimd.tensor_tensor(
+                    out=rotated[:],
+                    in0=shared[:].unsqueeze(4).to_broadcast([P, 2, TILES, PAIRS, 2]),
+                    in1=own[:],
+                    op=ALU.add,
+                )
+            for c, hbm in enumerate((q_groups, k_groups)):
+                if g == GROUPS - 1:
+                    nc.vector.tensor_tensor(
+                        out=rotated[:, c],
+                        in0=shared[:, c].unsqueeze(3).to_broadcast([P, TILES, PAIRS, 2]),
+                        in1=own[:, c],
+                        op=ALU.add,
+                    )
+                nc.sync.dma_start(out=hbm[g], in_=rotated[:, c].rearrange("p j i h -> p (j i h)"))
 
         def run(stage, index, count):
             if 0 <= index < count:
@@ -342,6 +358,8 @@ def tile_slidingwindowattention_pa_t_kernel(tc, x, ln_w, wq, wk, wv, out_0, out_
             run(turn, step + 2, GROUPS)
             run(multiply_own_q, step, GROUPS)
             run(multiply_own_k, step, GROUPS)
+            if step + 1 == 0:
+                quantise_weights(nc, w_grouped, w_codes, w_scales)
             run(quantise, step + 1, GROUPS)
             run(project, step + 1, GROUPS)
             run(regroup, step + 2, GROUPS)

@@ -57,14 +57,10 @@ def quantise_weights(nc, grouped, codes, scales):
         )
 
 
-def rotation_angles(nc, const):
+def rotation_angles(nc, const, one):
     position_int = const.tile([P, BLOCKS * TILES], I32, name="position_int")
     nc.gpsimd.iota(position_int[:], pattern=[[GROUP, BLOCKS], [1, TILES]], base=0, channel_multiplier=TILES)
-    position = const.tile([P, BLOCKS * TILES], F32, name="position")
-    nc.vector.tensor_copy(out=position[:], in_=position_int[:])
 
-    one = const.tile([P, 1], F32, name="one")
-    nc.gpsimd.memset(one[:], 1.0)
     coarse = const.tile([P, 8], F32, name="coarse")
     fine = const.tile([P, 8], F32, name="fine")
     for a in range(8):
@@ -80,6 +76,8 @@ def rotation_angles(nc, const):
         in1=fine[:].unsqueeze(1).to_broadcast([P, 8, 8]),
         op=ALU.mult,
     )
+    position = const.tile([P, BLOCKS * TILES], F32, name="position")
+    nc.vector.tensor_copy(out=position[:], in_=position_int[:])
 
     shape = [P, BLOCKS * TILES, PAIRS]
     turns = const.tile(shape, F32, name="turns")
@@ -128,7 +126,7 @@ def tile_slidingwindowattention_pa_t_kernel(tc, x, ln_w, wq, wk, wv, out_0, out_
         ctx.enter_context(tc.manual_schedule())
 
         unit = const.tile([P, 1], F32, name="unit")
-        nc.gpsimd.memset(unit[:], 1.0)
+        nc.vector.memset(unit[:], 1.0)
         eps = const.tile([P, 1], F32, name="eps")
         nc.vector.tensor_scalar_mul(out=eps[:], in0=unit[:], scalar1=EPS)
 
@@ -137,7 +135,7 @@ def tile_slidingwindowattention_pa_t_kernel(tc, x, ln_w, wq, wk, wv, out_0, out_
         zero = const.tile([P, 1], F32, name="zero")
         nc.gpsimd.memset(zero[:], 0.0)
 
-        part, minus_abs = rotation_angles(nc, const)
+        part, minus_abs = rotation_angles(nc, const, unit)
 
         x_tiles = [[loads.tile([P, D], BF16, name="x_t") for j in range(TILES)] for g in range(GROUPS)]
         gain_row = const.tile([P, D], BF16, name="gain_row")

@@ -120,10 +120,13 @@ def tile_slidingwindowattention_pa_t_kernel(tc, x, ln_w, wq, wk, wv, out_0, out_
         work = ctx.enter_context(tc.tile_pool(name="work", bufs=2))
         stores = ctx.enter_context(tc.tile_pool(name="stores", bufs=3))
         psum_const = ctx.enter_context(tc.psum_pool(name="psum_const", bufs=1))
-        psum_turned = ctx.enter_context(tc.psum_pool(name="psum_turned", bufs=2))
-        psum_sums = ctx.enter_context(tc.psum_pool(name="psum_sums", bufs=2))
+        psum_turned = ctx.enter_context(tc.psum_pool(name="psum_turned", bufs=3))
+        psum_sums = ctx.enter_context(tc.psum_pool(name="psum_sums", bufs=1))
         psum_out = ctx.enter_context(tc.psum_pool(name="psum_out", bufs=1))
         ctx.enter_context(tc.manual_schedule())
+
+        gain_row = const.tile([P, D], BF16, name="gain_row")
+        nc.gpsimd.memset(gain_row[:], 0.0)
 
         unit = const.tile([P, 1], F32, name="unit")
         nc.vector.memset(unit[:], 1.0)
@@ -138,9 +141,7 @@ def tile_slidingwindowattention_pa_t_kernel(tc, x, ln_w, wq, wk, wv, out_0, out_
         part, minus_abs = rotation_angles(nc, const, unit)
 
         x_tiles = [[loads.tile([P, D], BF16, name="x_t") for j in range(TILES)] for g in range(GROUPS)]
-        gain_row = const.tile([P, D], BF16, name="gain_row")
         w_raw = const.tile([P, 3, PACK, HD], BF16, name="w_raw")
-        nc.gpsimd.memset(gain_row[:], 0.0)
         for j in range(TILES):
             nc.sync.dma_start(out=x_tiles[0][j][:], in_=x_tiles_hbm[0, j])
         nc.sync.dma_start(out=gain_row[0:1, :], in_=ln_w.rearrange("(o d) -> o d", o=1))
@@ -203,19 +204,18 @@ def tile_slidingwindowattention_pa_t_kernel(tc, x, ln_w, wq, wk, wv, out_0, out_
                     scale=1.0 / math.sqrt(D),
                     accum_out=mean_sq[:, j : j + 1],
                 )
-            rstds[g] = mean_sq
-            if g >= FIRST_ON_SCALAR:
+            if g < FIRST_ON_SCALAR:
+                shifted = small.tile([P, TILES], F32, name="shifted")
+                nc.scalar.activation(out=shifted[:], in_=mean_sq[:], func=ACT.Identity, bias=eps[:], scale=1.0)
+                rstds[g] = shifted
+            else:
                 rstd = small.tile([P, TILES], F32, name="rstd")
                 nc.scalar.activation(out=rstd[:], in_=mean_sq[:], func=ACT.Abs_reciprocal_sqrt, bias=eps[:], scale=1.0)
                 rstds[g] = rstd
 
         def inverse_rms(g):
-            shifted = small.tile([P, TILES], F32, name="shifted")
-            nc.gpsimd.tensor_scalar(
-                out=shifted[:], in0=rstds[g][:], scalar1=1.0, scalar2=EPS, op0=ALU.mult, op1=ALU.add
-            )
             rstd = small.tile([P, TILES], F32, name="rstd")
-            nc.gpsimd.tensor_tensor(out=rstd[:], in0=shifted[:], in1=minus_half[:], op=ALU.pow)
+            nc.gpsimd.tensor_tensor(out=rstd[:], in0=rstds[g][:], in1=minus_half[:], op=ALU.pow)
             rstds[g] = rstd
 
         def normalise(g):

@@ -24,7 +24,7 @@ TILES = 4
 GROUP = TILES * P
 GROUPS = BATCH * SEQ // GROUP
 BLOCKS = SEQ // GROUP
-FIRST_ON_SCALAR = 8
+FIRST_ON_SCALAR = 6
 ROUND_TO_INTEGER = 1.5 * 2.0**23
 
 FLOPS = 2 * BATCH * SEQ * D * 3 * HD
@@ -116,9 +116,9 @@ def tile_slidingwindowattention_pa_t_kernel(tc, x, ln_w, wq, wk, wv, out_0, out_
     with ExitStack() as ctx:
         const = ctx.enter_context(tc.tile_pool(name="const", bufs=1))
         loads = ctx.enter_context(tc.tile_pool(name="loads", bufs=GROUPS * TILES))
-        small = ctx.enter_context(tc.tile_pool(name="small", bufs=4))
-        work = ctx.enter_context(tc.tile_pool(name="work", bufs=2))
-        stores = ctx.enter_context(tc.tile_pool(name="stores", bufs=3))
+        small = ctx.enter_context(tc.tile_pool(name="small", bufs=6))
+        work = ctx.enter_context(tc.tile_pool(name="work", bufs=3))
+        stores = ctx.enter_context(tc.tile_pool(name="stores", bufs=4))
         psum_const = ctx.enter_context(tc.psum_pool(name="psum_const", bufs=1))
         psum_turned = ctx.enter_context(tc.psum_pool(name="psum_turned", bufs=3))
         psum_sums = ctx.enter_context(tc.psum_pool(name="psum_sums", bufs=1))

@@ -131,26 +131,24 @@ def tile_slidingwindowattention_pa_t_kernel(tc, x, ln_w, wq, wk, wv, out_0, out_
         unit = const.tile([P, 1], F32, name="unit")
         nc.vector.memset(unit[:], 1.0)
         eps = const.tile([P, 1], F32, name="eps")
-        nc.vector.tensor_scalar_mul(out=eps[:], in0=unit[:], scalar1=EPS)
-
+        nc.scalar.mul(out=eps[:], in_=unit[:], mul=EPS)
         quarter_turn = const.tile([P, 1], F32, name="quarter_turn")
-        nc.vector.tensor_scalar_mul(out=quarter_turn[:], in0=unit[:], scalar1=0.5 * math.pi)
-        zero = const.tile([P, 1], F32, name="zero")
-        nc.gpsimd.memset(zero[:], 0.0)
+        nc.scalar.mul(out=quarter_turn[:], in_=unit[:], mul=0.5 * math.pi)
+        nc.scalar.dma_start(out=gain_row[0:1, :], in_=ln_w.rearrange("(o d) -> o d", o=1))
 
         part, minus_abs = rotation_angles(nc, const, unit)
 
         x_tiles = [[loads.tile([P, D], BF16, name="x_t") for j in range(TILES)] for g in range(GROUPS)]
         w_raw = const.tile([P, 3, PACK, HD], BF16, name="w_raw")
-        for j in range(TILES):
-            nc.sync.dma_start(out=x_tiles[0][j][:], in_=x_tiles_hbm[0, j])
-        nc.sync.dma_start(out=gain_row[0:1, :], in_=ln_w.rearrange("(o d) -> o d", o=1))
+        for g in range(2):
+            for j in range(TILES):
+                nc.sync.dma_start(out=x_tiles[g][j][:], in_=x_tiles_hbm[g, j])
         for m, w in enumerate((wq, wk, wv)):
             nc.sync.dma_start(
                 out=w_raw[:, m].rearrange("p (u e) n -> p u (e n)", u=2),
                 in_=w.rearrange("(u p e) n -> p u (e n)", u=2, e=2),
             )
-        for g in range(1, GROUPS):
+        for g in range(2, GROUPS):
             for j in range(TILES):
                 nc.sync.dma_start(out=x_tiles[g][j][:], in_=x_tiles_hbm[g, j])
 
@@ -158,7 +156,6 @@ def tile_slidingwindowattention_pa_t_kernel(tc, x, ln_w, wq, wk, wv, out_0, out_
         minus_half = const.tile([P, TILES], F32, name="minus_half")
         nc.gpsimd.memset(minus_half[:], -0.5)
         identity = const.tile([P, P], F32, name="identity")
-        make_identity(nc, identity[:])
         w_grouped = const.tile([P, 5, HD, PACK], BF16, name="w_grouped", align_bytes=64)
         w_codes = const.tile([P, 5, HD], U32, name="w_codes", align_bytes=64)
         w_scales = const.tile([P, 5, HD], U8, name="w_scales", align_bytes=64)
@@ -170,14 +167,16 @@ def tile_slidingwindowattention_pa_t_kernel(tc, x, ln_w, wq, wk, wv, out_0, out_
         def sines(s):
             rows = slice(s * TILES, (s + 1) * TILES)
             cols = slice(s * TILES * PAIRS, (s + 1) * TILES * PAIRS)
-            for plane, angle, bias in ((0, minus_abs, quarter_turn), (1, part, zero)):
-                nc.scalar.activation(
-                    out=planes[:, plane, cols],
-                    in_=angle[:, rows].rearrange("p j i -> p (j i)"),
-                    func=ACT.Sin,
-                    bias=bias[:],
-                    scale=2.0 * math.pi,
-                )
+            nc.scalar.activation(
+                out=planes[:, 0, cols],
+                in_=minus_abs[:, rows].rearrange("p j i -> p (j i)"),
+                func=ACT.Sin,
+                bias=quarter_turn[:],
+                scale=2.0 * math.pi,
+            )
+            nc.scalar.activation(
+                out=planes[:, 1, cols], in_=part[:, rows].rearrange("p j i -> p (j i)"), func=ACT.Sin, scale=2.0 * math.pi
+            )
 
         def cross_terms(s):
             rows = slice(s * TILES, (s + 1) * TILES)
@@ -365,4 +364,6 @@ def tile_slidingwindowattention_pa_t_kernel(tc, x, ln_w, wq, wk, wv, out_0, out_
             run(multiply_shared, step, GROUPS)
             run(add_and_store, step, GROUPS)
             run(inverse_rms, step + 4, FIRST_ON_SCALAR)
+            if step + 4 == 0:
+                make_identity(nc, identity[:])
             run(cross_terms, step + 3, BLOCKS)

@@ -130,6 +130,8 @@ def tile_slidingwindowattention_pa_t_kernel(tc, x, ln_w, wq, wk, wv, out_0, out_
 
         unit = const.tile([P, 1], F32, name="unit")
         nc.vector.memset(unit[:], 1.0)
+        warm = const.tile([P, 1], F32, name="warm")
+        nc.scalar.activation(out=warm[:], in_=unit[:], func=ACT.Sin, scale=1.0)
         eps = const.tile([P, 1], F32, name="eps")
         nc.scalar.mul(out=eps[:], in_=unit[:], mul=EPS)
         quarter_turn = const.tile([P, 1], F32, name="quarter_turn")

@@ -24,7 +24,6 @@ TILES = 4
 GROUP = TILES * P
 GROUPS = BATCH * SEQ // GROUP
 BLOCKS = SEQ // GROUP
-FIRST_ON_SCALAR = 6
 ROUND_TO_INTEGER = 1.5 * 2.0**23
 
 FLOPS = 2 * BATCH * SEQ * D * 3 * HD
@@ -39,27 +38,28 @@ def broadcast_gain(nc, const, psum_const, gain_row):
 
 
 def group_weights(nc, raw, grouped):
-    halves = raw[:, 0:2].rearrange("p m t (i h) -> p h m i t", h=2)
-    swapped = grouped[:, 2:4].rearrange("p m (i h) t -> p h m i t", h=2)
-    for h in range(2):
-        nc.vector.tensor_copy(out=grouped[:, h].rearrange("p (m i) t -> p m i t", m=2), in_=halves[:, h])
-    nc.vector.tensor_scalar_mul(out=swapped[:, 0], in0=halves[:, 1], scalar1=-1.0)
-    nc.vector.tensor_copy(out=swapped[:, 1], in_=halves[:, 0])
-    nc.vector.tensor_copy(out=grouped[:, 4], in_=raw[:, 2].rearrange("p t n -> p n t"))
+    nc.vector.tensor_copy(out=grouped[:], in_=raw[:].rearrange("p m t n -> p m n t"))
 
 
-def quantise_weights(nc, grouped, codes, scales):
-    for operands in (slice(0, 4), slice(4, 5)):
+def quantise_weights(nc, grouped, codes, scales, split_codes, split_scales):
+    for operands in (slice(0, 2), slice(2, 3)):
         nc.vector.quantize_mx(
-            out=codes[:, operands].rearrange("p c n -> p (c n)").bitcast(FP8X4),
-            scales=scales[:, operands].rearrange("p c n -> p (c n)"),
-            in_=grouped[:, operands].rearrange("p c n t -> p (c n t)"),
+            out=codes[:, operands].rearrange("p m n -> p (m n)").bitcast(FP8X4),
+            scales=scales[:, operands].rearrange("p m n -> p (m n)"),
+            in_=grouped[:, operands].rearrange("p m n t -> p (m n t)"),
+        )
+    for src, dst, dtype in ((codes, split_codes, I32), (scales, split_scales, U8)):
+        source = src[:, 0:2].rearrange("p m n -> p (m n)").bitcast(dtype)
+        target = dst[:].rearrange("p h n -> p (h n)").bitcast(dtype)
+        nc.vector.tensor_copy(
+            out=target.rearrange("p (h c) -> p c h", h=2), in_=source.rearrange("p (c h) -> p c h", h=2)
         )
 
 
 def rotation_angles(nc, const, one):
-    position_int = const.tile([P, BLOCKS * TILES], I32, name="position_int")
-    nc.gpsimd.iota(position_int[:], pattern=[[GROUP, BLOCKS], [1, TILES]], base=0, channel_multiplier=TILES)
+    position = const.tile([P, TILES + 1], F32, name="position")
+    nc.gpsimd.iota(position[:, 0:TILES], pattern=[[1, TILES]], base=0, channel_multiplier=TILES, allow_small_or_imprecise_dtypes=True)
+    nc.gpsimd.memset(position[:, TILES : TILES + 1], float(GROUP))
 
     coarse = const.tile([P, 8], F32, name="coarse")
     fine = const.tile([P, 8], F32, name="fine")
@@ -76,10 +76,8 @@ def rotation_angles(nc, const, one):
         in1=fine[:].unsqueeze(1).to_broadcast([P, 8, 8]),
         op=ALU.mult,
     )
-    position = const.tile([P, BLOCKS * TILES], F32, name="position")
-    nc.vector.tensor_copy(out=position[:], in_=position_int[:])
 
-    shape = [P, BLOCKS * TILES, PAIRS]
+    shape = [P, TILES + 1, PAIRS]
     turns = const.tile(shape, F32, name="turns")
     nc.vector.tensor_tensor(
         out=turns[:],
@@ -107,11 +105,11 @@ def rotation_angles(nc, const, one):
 
 def tile_slidingwindowattention_pa_t_kernel(tc, x, ln_w, wq, wk, wv, out_0, out_1, out_2):
     nc = tc.nc
-    by_group = "(g p j) d -> g p (j d)"
-    x_tiles_hbm = x.rearrange("b s d -> (b s) d").rearrange("(g p j) d -> g j p d", p=P, j=TILES)
-    q_groups = out_0.rearrange("b s h d -> (b s h) d").rearrange(by_group, p=P, j=TILES)
-    k_groups = out_1.rearrange("b s h d -> (b s h) d").rearrange(by_group, p=P, j=TILES)
-    v_groups = out_2.rearrange("b s h d -> (b s h) d").rearrange(by_group, p=P, j=TILES)
+    by_group = "b (s p j) h d -> s b p (j h d)"
+    x_tiles_hbm = x.rearrange("b (s p j) d -> s b j p d", p=P, j=TILES)
+    q_groups = out_0.rearrange(by_group, p=P, j=TILES)
+    k_groups = out_1.rearrange(by_group, p=P, j=TILES)
+    v_groups = out_2.rearrange(by_group, p=P, j=TILES)
 
     with ExitStack() as ctx:
         const = ctx.enter_context(tc.tile_pool(name="const", bufs=1))
@@ -136,88 +134,117 @@ def tile_slidingwindowattention_pa_t_kernel(tc, x, ln_w, wq, wk, wv, out_0, out_
         nc.scalar.mul(out=eps[:], in_=unit[:], mul=EPS)
         quarter_turn = const.tile([P, 1], F32, name="quarter_turn")
         nc.scalar.mul(out=quarter_turn[:], in_=unit[:], mul=0.5 * math.pi)
+        minus_quarter = const.tile([P, 1], F32, name="minus_quarter")
+        nc.scalar.mul(out=minus_quarter[:], in_=unit[:], mul=-0.5 * math.pi)
         nc.scalar.dma_start(out=gain_row[0:1, :], in_=ln_w.rearrange("(o d) -> o d", o=1))
 
         part, minus_abs = rotation_angles(nc, const, unit)
 
         x_tiles = [[loads.tile([P, D], BF16, name="x_t") for j in range(TILES)] for g in range(GROUPS)]
         w_raw = const.tile([P, 3, PACK, HD], BF16, name="w_raw")
-        for g in range(2):
+        for g in range(1):
             for j in range(TILES):
-                nc.sync.dma_start(out=x_tiles[g][j][:], in_=x_tiles_hbm[g, j])
+                nc.sync.dma_start(out=x_tiles[g][j][:], in_=x_tiles_hbm[g // BATCH, g % BATCH, j])
         for m, w in enumerate((wq, wk, wv)):
             nc.sync.dma_start(
                 out=w_raw[:, m].rearrange("p (u e) n -> p u (e n)", u=2),
                 in_=w.rearrange("(u p e) n -> p u (e n)", u=2, e=2),
             )
-        for g in range(2, GROUPS):
+        for g in range(1, GROUPS):
             for j in range(TILES):
-                nc.sync.dma_start(out=x_tiles[g][j][:], in_=x_tiles_hbm[g, j])
+                nc.sync.dma_start(out=x_tiles[g][j][:], in_=x_tiles_hbm[g // BATCH, g % BATCH, j])
 
         gain = broadcast_gain(nc, const, psum_const, gain_row)
-        minus_half = const.tile([P, TILES], F32, name="minus_half")
-        nc.gpsimd.memset(minus_half[:], -0.5)
         identity = const.tile([P, P], F32, name="identity")
-        w_grouped = const.tile([P, 5, HD, PACK], BF16, name="w_grouped", align_bytes=64)
-        w_codes = const.tile([P, 5, HD], U32, name="w_codes", align_bytes=64)
-        w_scales = const.tile([P, 5, HD], U8, name="w_scales", align_bytes=64)
-        group_weights(nc, w_raw, w_grouped)
+        make_identity(nc, identity[:])
+        w_grouped = const.tile([P, 3, HD, PACK], BF16, name="w_grouped", align_bytes=64)
+        w_codes = const.tile([P, 3, HD], U32, name="w_codes", align_bytes=64)
+        w_scales = const.tile([P, 3, HD], U8, name="w_scales", align_bytes=64)
+        split_codes = const.tile([P, 2, HD], U32, name="split_codes", align_bytes=64)
+        split_scales = const.tile([P, 2, HD], U8, name="split_scales", align_bytes=64)
 
-        planes = const.tile([P, 2, BLOCKS * TILES * PAIRS], F32, name="planes")
+        minus_cos = const.tile([P, BLOCKS * TILES, PAIRS], F32, name="minus_cos")
+        sin = const.tile([P, BLOCKS * TILES, PAIRS], F32, name="sin")
         cross = const.tile([P, BLOCKS * TILES, PAIRS, 2], F32, name="cross")
+        step_cos = const.tile([P, 1, PAIRS], F32, name="step_cos")
+        step_sin = const.tile([P, 1, PAIRS], F32, name="step_sin")
 
-        def sines(s):
-            rows = slice(s * TILES, (s + 1) * TILES)
-            cols = slice(s * TILES * PAIRS, (s + 1) * TILES * PAIRS)
-            nc.scalar.activation(
-                out=planes[:, 0, cols],
-                in_=minus_abs[:, rows].rearrange("p j i -> p (j i)"),
-                func=ACT.Sin,
-                bias=quarter_turn[:],
-                scale=2.0 * math.pi,
-            )
-            nc.scalar.activation(
-                out=planes[:, 1, cols], in_=part[:, rows].rearrange("p j i -> p (j i)"), func=ACT.Sin, scale=2.0 * math.pi
-            )
+        def block_rows(s):
+            return slice(s * TILES, (s + 1) * TILES)
 
-        def cross_terms(s):
-            rows = slice(s * TILES, (s + 1) * TILES)
-            cols = slice(s * TILES * PAIRS, (s + 1) * TILES * PAIRS)
-            for h, op in ((0, ALU.add), (1, ALU.subtract)):
-                nc.gpsimd.tensor_tensor(
-                    out=cross[:, rows, :, h],
-                    in0=planes[:, 1, cols].rearrange("p (j i) -> p j i", j=TILES),
-                    in1=planes[:, 0, cols].rearrange("p (j i) -> p j i", j=TILES),
-                    op=op,
-                )
+        def first_sines():
+            for out, angle, rows, bias, scale in (
+                (minus_cos[:, 0:TILES], minus_abs, slice(0, TILES), minus_quarter, -2.0 * math.pi),
+                (step_cos[:], minus_abs, slice(TILES, TILES + 1), quarter_turn, 2.0 * math.pi),
+            ):
+                nc.scalar.activation(out=out, in_=angle[:, rows], func=ACT.Sin, bias=bias[:], scale=scale)
+            for out, rows in ((sin[:, 0:TILES], slice(0, TILES)), (step_sin[:], slice(TILES, TILES + 1))):
+                nc.scalar.activation(out=out, in_=part[:, rows], func=ACT.Sin, scale=2.0 * math.pi)
 
-        rstds, xns, turneds, groupeds, operands, banks, products = {}, {}, {}, {}, {}, {}, {}
+        def cross_work(s):
+            rows = block_rows(s)
+            return [
+                (cross[:, rows, :, h], minus_cos[:, rows], sin[:, rows], op)
+                for h, op in ((0, ALU.subtract), (1, ALU.add))
+            ]
 
-        def mean_squares(g):
-            mean_sq = small.tile([P, TILES], F32, name="mean_sq")
-            squares = work.tile([P, TILES * D], BF16, name="squares")
-            for j in range(TILES):
-                cols = slice(j * D, (j + 1) * D)
+        def block_work(s):
+            shape = [P, TILES, PAIRS]
+            c, r = step_cos[:].to_broadcast(shape), step_sin[:].to_broadcast(shape)
+            n_old, s_old = minus_cos[:, block_rows(s - 1)], sin[:, block_rows(s - 1)]
+            parts = [const.tile(shape, F32, name="part_%d" % i) for i in range(4)]
+            return [
+                (parts[0][:], n_old, c, ALU.mult),
+                (parts[1][:], s_old, r, ALU.mult),
+                (minus_cos[:, block_rows(s)], parts[0][:], parts[1][:], ALU.add),
+                (parts[2][:], s_old, c, ALU.mult),
+                (parts[3][:], n_old, r, ALU.mult),
+                (sin[:, block_rows(s)], parts[2][:], parts[3][:], ALU.subtract),
+            ] + cross_work(s)
+
+        def on_gpsimd(work_list):
+            for out, in0, in1, op in work_list:
+                nc.gpsimd.tensor_tensor(out=out, in0=in0, in1=in1, op=op)
+
+        mean_sqs, rstds, xns, turneds, groupeds, operands, banks, products = {}, {}, {}, {}, {}, {}, {}, {}
+
+        def square(g, tiles):
+            if g not in mean_sqs:
+                mean_sqs[g] = small.tile([P, TILES], F32, name="mean_sq")
+            for j in tiles:
+                squares = work.tile([P, D], BF16, name="squares")
                 nc.scalar.activation(
-                    out=squares[:, cols],
+                    out=squares[:],
                     in_=x_tiles[g][j][:],
                     func=ACT.Square,
                     scale=1.0 / math.sqrt(D),
-                    accum_out=mean_sq[:, j : j + 1],
+                    accum_out=mean_sqs[g][:, j : j + 1],
                 )
-            if g < FIRST_ON_SCALAR:
-                shifted = small.tile([P, TILES], F32, name="shifted")
-                nc.scalar.activation(out=shifted[:], in_=mean_sq[:], func=ACT.Identity, bias=eps[:], scale=1.0)
-                rstds[g] = shifted
-            else:
-                rstd = small.tile([P, TILES], F32, name="rstd")
-                nc.scalar.activation(out=rstd[:], in_=mean_sq[:], func=ACT.Abs_reciprocal_sqrt, bias=eps[:], scale=1.0)
-                rstds[g] = rstd
 
-        def inverse_rms(g):
-            rstd = small.tile([P, TILES], F32, name="rstd")
-            nc.gpsimd.tensor_tensor(out=rstd[:], in0=rstds[g][:], in1=minus_half[:], op=ALU.pow)
-            rstds[g] = rstd
+        def square_on_vector(g, tiles):
+            mean_sqs[g] = small.tile([P, TILES], F32, name="mean_sq")
+            for j in tiles:
+                squares = work.tile([P, D], BF16, name="squares_v")
+                nc.vector.scalar_tensor_tensor(
+                    out=squares[:],
+                    in0=x_tiles[g][j][:],
+                    scalar=1.0 / D,
+                    in1=x_tiles[g][j][:],
+                    op0=ALU.mult,
+                    op1=ALU.mult,
+                    accum_out=mean_sqs[g][:, j : j + 1],
+                )
+
+        def first_squares(g):
+            square(g, range(0, TILES // 2))
+
+        def last_squares(g):
+            if g > 0:
+                square(g, range(TILES // 2, TILES))
+            rstds[g] = small.tile([P, TILES], F32, name="rstd")
+            nc.scalar.activation(
+                out=rstds[g][:], in_=mean_sqs[g][:], func=ACT.Abs_reciprocal_sqrt, bias=eps[:], scale=1.0
+            )
 
         def normalise(g):
             xn = work.tile([P, TILES * D], BF16, name="xn")
@@ -275,8 +302,8 @@ def tile_slidingwindowattention_pa_t_kernel(tc, x, ln_w, wq, wk, wv, out_0, out_
             q_ps = psum_out.tile([P, TILES, HD], F32, name="q_ps")
             k_ps = psum_out.tile([P, TILES, HD], F32, name="k_ps")
             v_ps = psum_out.tile([P, TILES, HD], F32, name="v_ps")
-            passes(q_ps, 2, True, True)
-            passes(k_ps, 3, True, True)
+            passes(q_ps, 0, True, True)
+            passes(k_ps, 1, True, True)
             sum_ps = psum_sums.tile([P, TILES, HD], F32, name="sum_ps")
             for j in range(TILES):
                 tokens = slice(j * P, (j + 1) * P)
@@ -285,31 +312,31 @@ def tile_slidingwindowattention_pa_t_kernel(tc, x, ln_w, wq, wk, wv, out_0, out_
                         out=sum_ps[:, j, :],
                         lhsT=codes[:, tokens].bitcast(FP8X4),
                         lhsT_scale=scales[:, tokens],
-                        rhs=w_codes[:, operand].bitcast(FP8X4),
-                        rhs_scale=w_scales[:, operand],
+                        rhs=split_codes[:, operand].bitcast(FP8X4),
+                        rhs_scale=split_scales[:, operand],
                         start=(operand == 0),
                         stop=(operand == 1),
                     )
-            passes(v_ps, 4, True, True)
+            passes(v_ps, 2, True, True)
             banks[g] = (sum_ps, q_ps, k_ps, v_ps)
 
         def multiply_shared(g):
-            rows = slice((g % BLOCKS) * TILES, (g % BLOCKS + 1) * TILES)
+            rows = slice((g // BATCH) * TILES, (g // BATCH + 1) * TILES)
             shape = [P, TILES, 2, PAIRS]
             shared = work.tile([P, 2, TILES, PAIRS], F32, name="shared")
             nc.vector.tensor_tensor(
                 out=shared[:].rearrange("p c j i -> p j c i"),
                 in0=banks[g][0][:].rearrange("p j (c i) -> p j c i", c=2),
-                in1=planes[:, 0].rearrange("p (s i) -> p s i", i=PAIRS)[:, rows].unsqueeze(2).to_broadcast(shape),
+                in1=minus_cos[:, rows].unsqueeze(2).to_broadcast(shape),
                 op=ALU.mult,
             )
             products[g].append(shared)
 
         def multiply_own(g, c):
-            rows = slice((g % BLOCKS) * TILES, (g % BLOCKS + 1) * TILES)
+            rows = slice((g // BATCH) * TILES, (g // BATCH + 1) * TILES)
             nc.vector.tensor_tensor(
                 out=products[g][0][:, c],
-                in0=banks[g][1 + c][:].rearrange("p j (i h) -> p j i h", h=2),
+                in0=banks[g][1 + c][:].rearrange("p j (i h) -> p j i h", h=2)[:, :, :, ::-1],
                 in1=cross[:, rows],
                 op=ALU.mult,
             )
@@ -324,7 +351,7 @@ def tile_slidingwindowattention_pa_t_kernel(tc, x, ln_w, wq, wk, wv, out_0, out_
         def copy_v(g):
             v_sb = stores.tile([P, TILES * HD], F32, name="v_sb")
             nc.scalar.copy(out=v_sb[:], in_=banks[g][3][:].rearrange("p j d -> p (j d)"))
-            nc.sync.dma_start(out=v_groups[g], in_=v_sb[:])
+            nc.sync.dma_start(out=v_groups[g // BATCH, g % BATCH], in_=v_sb[:])
 
         def add_and_store(g):
             own, shared = products[g]
@@ -332,40 +359,45 @@ def tile_slidingwindowattention_pa_t_kernel(tc, x, ln_w, wq, wk, wv, out_0, out_
             if g < GROUPS - 1:
                 nc.gpsimd.tensor_tensor(
                     out=rotated[:],
-                    in0=shared[:].unsqueeze(4).to_broadcast([P, 2, TILES, PAIRS, 2]),
-                    in1=own[:],
-                    op=ALU.add,
+                    in0=own[:],
+                    in1=shared[:].unsqueeze(4).to_broadcast([P, 2, TILES, PAIRS, 2]),
+                    op=ALU.subtract,
                 )
             for c, hbm in enumerate((q_groups, k_groups)):
                 if g == GROUPS - 1:
                     nc.vector.tensor_tensor(
                         out=rotated[:, c],
-                        in0=shared[:, c].unsqueeze(3).to_broadcast([P, TILES, PAIRS, 2]),
-                        in1=own[:, c],
-                        op=ALU.add,
+                        in0=own[:, c],
+                        in1=shared[:, c].unsqueeze(3).to_broadcast([P, TILES, PAIRS, 2]),
+                        op=ALU.subtract,
                     )
-                nc.sync.dma_start(out=hbm[g], in_=rotated[:, c].rearrange("p j i h -> p (j i h)"))
+                nc.sync.dma_start(out=hbm[g // BATCH, g % BATCH], in_=rotated[:, c].rearrange("p j i h -> p (j i h)"))
 
         def run(stage, index, count):
             if 0 <= index < count:
                 stage(index)
 
-        for step in range(-4, GROUPS):
+        first_sines()
+        on_gpsimd(cross_work(0))
+        square_on_vector(0, range(TILES))
+        group_weights(nc, w_raw, w_grouped)
+        on_gpsimd(block_work(1))
+        on_gpsimd(block_work(2))
+        later = block_work(3)
+        for step in range(-3, GROUPS):
             run(copy_v, step, GROUPS)
-            run(mean_squares, step + 4, GROUPS)
+            run(last_squares, step + 3, GROUPS)
+            run(first_squares, step + 4, GROUPS)
             run(normalise, step + 2, GROUPS)
             run(turn, step + 2, GROUPS)
             run(multiply_own_q, step, GROUPS)
             run(multiply_own_k, step, GROUPS)
             if step + 1 == 0:
-                quantise_weights(nc, w_grouped, w_codes, w_scales)
+                quantise_weights(nc, w_grouped, w_codes, w_scales, split_codes, split_scales)
             run(quantise, step + 1, GROUPS)
             run(project, step + 1, GROUPS)
             run(regroup, step + 2, GROUPS)
-            run(sines, step + 3, BLOCKS)
             run(multiply_shared, step, GROUPS)
             run(add_and_store, step, GROUPS)
-            run(inverse_rms, step + 4, FIRST_ON_SCALAR)
-            if step + 4 == 0:
-                make_identity(nc, identity[:])
-            run(cross_terms, step + 3, BLOCKS)
+            if 4 <= step < 8:
+                on_gpsimd(later[2 * (step - 4) : 2 * (step - 3)])

@@ -38,7 +38,11 @@ def broadcast_gain(nc, const, psum_const, gain_row):
 
 
 def group_weights(nc, raw, grouped):
-    nc.vector.tensor_copy(out=grouped[:], in_=raw[:].rearrange("p m t n -> p m n t"))
+    pairs = grouped[:, 0:2].rearrange("p m (i h) t -> p h m i t", h=2)
+    raw_pairs = raw[:, 0:2].rearrange("p m t (i h) -> p h m i t", h=2)
+    for h in range(2):
+        nc.vector.tensor_copy(out=pairs[:, h], in_=raw_pairs[:, 1 - h])
+    nc.vector.tensor_copy(out=grouped[:, 2], in_=raw[:, 2].rearrange("p t n -> p n t"))
 
 
 def quantise_weights(nc, grouped, codes, scales, split_codes, split_scales):
@@ -336,7 +340,7 @@ def tile_slidingwindowattention_pa_t_kernel(tc, x, ln_w, wq, wk, wv, out_0, out_
             rows = slice((g // BATCH) * TILES, (g // BATCH + 1) * TILES)
             nc.vector.tensor_tensor(
                 out=products[g][0][:, c],
-                in0=banks[g][1 + c][:].rearrange("p j (i h) -> p j i h", h=2)[:, :, :, ::-1],
+                in0=banks[g][1 + c][:].rearrange("p j (i h) -> p j i h", h=2),
                 in1=cross[:, rows],
                 op=ALU.mult,
             )

@@ -2,7 +2,6 @@ import math
 from contextlib import ExitStack
 
 import concourse.mybir as mybir
-from concourse.masks import make_identity
 
 F32 = mybir.dt.float32
 BF16 = mybir.dt.bfloat16
@@ -19,6 +18,7 @@ BASE = 10000.0
 
 P = 128
 PACK = 4
+TABLE_STEPS = 11
 PAIRS = HD // 2
 TILES = 4
 GROUP = TILES * P
@@ -29,9 +29,7 @@ ROUND_TO_INTEGER = 1.5 * 2.0**23
 FLOPS = 2 * BATCH * SEQ * D * 3 * HD
 
 
-def broadcast_gain(nc, const, psum_const, gain_row):
-    ones = const.tile([P, P], BF16, name="ones")
-    nc.gpsimd.memset(ones[:], 1.0)
+def broadcast_gain(nc, psum_const, ones, gain_row):
     gain = psum_const.tile([P, D], F32, name="gain")
     nc.tensor.matmul(out=gain[:], lhsT=ones[:], rhs=gain_row[:], start=True, stop=True)
     return gain
@@ -46,39 +44,40 @@ def group_weights(nc, raw, grouped):
 
 
 def quantise_weights(nc, grouped, codes, scales, split_codes, split_scales):
-    for operands in (slice(0, 2), slice(2, 3)):
+    def quantise(operands):
         nc.vector.quantize_mx(
             out=codes[:, operands].rearrange("p m n -> p (m n)").bitcast(FP8X4),
             scales=scales[:, operands].rearrange("p m n -> p (m n)"),
             in_=grouped[:, operands].rearrange("p m n t -> p (m n t)"),
         )
+
+    quantise(slice(0, 2))
     for src, dst, dtype in ((codes, split_codes, I32), (scales, split_scales, U8)):
         source = src[:, 0:2].rearrange("p m n -> p (m n)").bitcast(dtype)
         target = dst[:].rearrange("p h n -> p (h n)").bitcast(dtype)
         nc.vector.tensor_copy(
             out=target.rearrange("p (h c) -> p c h", h=2), in_=source.rearrange("p (c h) -> p c h", h=2)
         )
+    quantise(slice(2, 3))
 
 
-def rotation_angles(nc, const, one):
-    position = const.tile([P, TILES + 1], F32, name="position")
-    nc.gpsimd.iota(position[:, 0:TILES], pattern=[[1, TILES]], base=0, channel_multiplier=TILES, allow_small_or_imprecise_dtypes=True)
-    nc.gpsimd.memset(position[:, TILES : TILES + 1], float(GROUP))
-
-    coarse = const.tile([P, 8], F32, name="coarse")
-    fine = const.tile([P, 8], F32, name="fine")
-    for a in range(8):
-        nc.vector.tensor_scalar_mul(
-            out=coarse[:, a : a + 1], in0=one[:], scalar1=BASE ** (-8.0 * a / PAIRS) / (2.0 * math.pi)
-        )
-    for b in range(8):
-        nc.vector.tensor_scalar_mul(out=fine[:, b : b + 1], in0=one[:], scalar1=BASE ** (-1.0 * b / PAIRS))
-    frequency = const.tile([P, 8, 8], F32, name="frequency")
-    nc.vector.tensor_tensor(
+def rotation_angles(nc, const, ones, ramp, partition_4):
+    ratio = BASE ** (-1.0 / PAIRS)
+    ratios = const.tile([P, PAIRS], F32, name="ratios")
+    nc.vector.tensor_scalar_mul(out=ratios[:], in0=ones[:, 0:PAIRS], scalar1=ratio)
+    frequency = const.tile([P, PAIRS], F32, name="frequency")
+    nc.vector.tensor_tensor_scan(
         out=frequency[:],
-        in0=coarse[:].unsqueeze(2).to_broadcast([P, 8, 8]),
-        in1=fine[:].unsqueeze(1).to_broadcast([P, 8, 8]),
-        op=ALU.mult,
+        data0=ratios[:],
+        data1=ones[:, 0:PAIRS],
+        initial=1.0 / (2.0 * math.pi * ratio),
+        op0=ALU.mult,
+        op1=ALU.mult,
+    )
+    position = const.tile([P, TILES + 1], F32, name="position")
+    nc.vector.memset(position[:, TILES : TILES + 1], float(GROUP))
+    nc.vector.tensor_scalar(
+        out=position[:, 0:TILES], in0=ramp[:, 0:TILES], scalar1=partition_4, scalar2=None, op0=ALU.add
     )
 
     shape = [P, TILES + 1, PAIRS]
@@ -86,7 +85,7 @@ def rotation_angles(nc, const, one):
     nc.vector.tensor_tensor(
         out=turns[:],
         in0=position[:].unsqueeze(2).to_broadcast(shape),
-        in1=frequency[:].rearrange("p a b -> p (a b)").unsqueeze(1).to_broadcast(shape),
+        in1=frequency[:].unsqueeze(1).to_broadcast(shape),
         op=ALU.mult,
     )
     whole = const.tile(shape, F32, name="whole")
@@ -127,11 +126,24 @@ def tile_slidingwindowattention_pa_t_kernel(tc, x, ln_w, wq, wk, wv, out_0, out_
         psum_out = ctx.enter_context(tc.psum_pool(name="psum_out", bufs=1))
         ctx.enter_context(tc.manual_schedule())
 
-        gain_row = const.tile([P, D], BF16, name="gain_row")
-        nc.gpsimd.memset(gain_row[:], 0.0)
-
         unit = const.tile([P, 1], F32, name="unit")
         nc.vector.memset(unit[:], 1.0)
+        ones = const.tile([P, P], F32, name="ones")
+        nc.vector.memset(ones[:], 1.0)
+        ramp = const.tile([P, P], F32, name="ramp")
+        nc.vector.tensor_tensor_scan(
+            out=ramp[:], data0=ones[:], data1=ones[:], initial=-1.0, op0=ALU.mult, op1=ALU.add
+        )
+        fraction = const.tile([P, 8], F32, name="fraction")
+        nc.vector.memset(fraction[:], TILES / P)
+        start_ps = psum_out.tile([P, TILES, HD], F32, name="q_ps")
+        nc.tensor.matmul(out=start_ps[:, 0, 0:8], lhsT=ramp[:], rhs=fraction[:], start=True, stop=True)
+        partition_4 = start_ps[:, 0, 0:1]
+        gain_row = const.tile([P, D], BF16, name="gain_row")
+        nc.vector.memset(gain_row[:], 0.0)
+        ones_bf16 = const.tile([P, P], BF16, name="ones_bf16")
+        nc.vector.memset(ones_bf16[:], 1.0)
+
         warm = const.tile([P, 1], F32, name="warm")
         nc.scalar.activation(out=warm[:], in_=unit[:], func=ACT.Sin, scale=1.0)
         eps = const.tile([P, 1], F32, name="eps")
@@ -142,7 +154,7 @@ def tile_slidingwindowattention_pa_t_kernel(tc, x, ln_w, wq, wk, wv, out_0, out_
         nc.scalar.mul(out=minus_quarter[:], in_=unit[:], mul=-0.5 * math.pi)
         nc.scalar.dma_start(out=gain_row[0:1, :], in_=ln_w.rearrange("(o d) -> o d", o=1))
 
-        part, minus_abs = rotation_angles(nc, const, unit)
+        part, minus_abs = rotation_angles(nc, const, ones, ramp, partition_4)
 
         x_tiles = [[loads.tile([P, D], BF16, name="x_t") for j in range(TILES)] for g in range(GROUPS)]
         w_raw = const.tile([P, 3, PACK, HD], BF16, name="w_raw")
@@ -158,9 +170,8 @@ def tile_slidingwindowattention_pa_t_kernel(tc, x, ln_w, wq, wk, wv, out_0, out_
             for j in range(TILES):
                 nc.sync.dma_start(out=x_tiles[g][j][:], in_=x_tiles_hbm[g // BATCH, g % BATCH, j])
 
-        gain = broadcast_gain(nc, const, psum_const, gain_row)
+        gain = broadcast_gain(nc, psum_const, ones_bf16, gain_row)
         identity = const.tile([P, P], F32, name="identity")
-        make_identity(nc, identity[:])
         w_grouped = const.tile([P, 3, HD, PACK], BF16, name="w_grouped", align_bytes=64)
         w_codes = const.tile([P, 3, HD], U32, name="w_codes", align_bytes=64)
         w_scales = const.tile([P, 3, HD], U8, name="w_scales", align_bytes=64)
@@ -170,8 +181,7 @@ def tile_slidingwindowattention_pa_t_kernel(tc, x, ln_w, wq, wk, wv, out_0, out_
         minus_cos = const.tile([P, BLOCKS * TILES, PAIRS], F32, name="minus_cos")
         sin = const.tile([P, BLOCKS * TILES, PAIRS], F32, name="sin")
         cross = const.tile([P, BLOCKS * TILES, PAIRS, 2], F32, name="cross")
-        step_cos = const.tile([P, 1, PAIRS], F32, name="step_cos")
-        step_sin = const.tile([P, 1, PAIRS], F32, name="step_sin")
+        advance = const.tile([P, 4, PAIRS], F32, name="advance")
 
         def block_rows(s):
             return slice(s * TILES, (s + 1) * TILES)
@@ -179,10 +189,10 @@ def tile_slidingwindowattention_pa_t_kernel(tc, x, ln_w, wq, wk, wv, out_0, out_
         def first_sines():
             for out, angle, rows, bias, scale in (
                 (minus_cos[:, 0:TILES], minus_abs, slice(0, TILES), minus_quarter, -2.0 * math.pi),
-                (step_cos[:], minus_abs, slice(TILES, TILES + 1), quarter_turn, 2.0 * math.pi),
+                (advance[:, 0:1], minus_abs, slice(TILES, TILES + 1), quarter_turn, 2.0 * math.pi),
             ):
                 nc.scalar.activation(out=out, in_=angle[:, rows], func=ACT.Sin, bias=bias[:], scale=scale)
-            for out, rows in ((sin[:, 0:TILES], slice(0, TILES)), (step_sin[:], slice(TILES, TILES + 1))):
+            for out, rows in ((sin[:, 0:TILES], slice(0, TILES)), (advance[:, 1:2], slice(TILES, TILES + 1))):
                 nc.scalar.activation(out=out, in_=part[:, rows], func=ACT.Sin, scale=2.0 * math.pi)
 
         def cross_work(s):
@@ -194,16 +204,16 @@ def tile_slidingwindowattention_pa_t_kernel(tc, x, ln_w, wq, wk, wv, out_0, out_
 
         def block_work(s):
             shape = [P, TILES, PAIRS]
-            c, r = step_cos[:].to_broadcast(shape), step_sin[:].to_broadcast(shape)
-            n_old, s_old = minus_cos[:, block_rows(s - 1)], sin[:, block_rows(s - 1)]
-            parts = [const.tile(shape, F32, name="part_%d" % i) for i in range(4)]
+            old, new = block_rows(s - 1), block_rows(s)
+            parts = w_grouped[:].rearrange("p m n t -> p (m n t)").bitcast(F32).rearrange(
+                "p (a j i) -> p a j i", a=3, i=PAIRS
+            )
             return [
-                (parts[0][:], n_old, c, ALU.mult),
-                (parts[1][:], s_old, r, ALU.mult),
-                (minus_cos[:, block_rows(s)], parts[0][:], parts[1][:], ALU.add),
-                (parts[2][:], s_old, c, ALU.mult),
-                (parts[3][:], n_old, r, ALU.mult),
-                (sin[:, block_rows(s)], parts[2][:], parts[3][:], ALU.subtract),
+                (parts[:, 2], minus_cos[:, old], advance[:, 3:4].to_broadcast(shape), ALU.mult),
+                (parts[:, 1], sin[:, old], advance[:, 2:3].to_broadcast(shape), ALU.mult),
+                (parts[:, 0], cross[:, old, :, 1], advance[:, 0:1].to_broadcast(shape), ALU.mult),
+                (minus_cos[:, new], parts[:, 0], parts[:, 1], ALU.add),
+                (sin[:, new], parts[:, 0], parts[:, 2], ALU.subtract),
             ] + cross_work(s)
 
         def on_gpsimd(work_list):
@@ -226,11 +236,11 @@ def tile_slidingwindowattention_pa_t_kernel(tc, x, ln_w, wq, wk, wv, out_0, out_
                 )
 
         def square_on_vector(g, tiles):
+            unread = cross[:, 0:TILES].rearrange("p j i h -> p (j i h)").bitcast(BF16)
             mean_sqs[g] = small.tile([P, TILES], F32, name="mean_sq")
             for j in tiles:
-                squares = work.tile([P, D], BF16, name="squares_v")
                 nc.vector.scalar_tensor_tensor(
-                    out=squares[:],
+                    out=unread[:, j % 2 * D : (j % 2 + 1) * D],
                     in0=x_tiles[g][j][:],
                     scalar=1.0 / D,
                     in1=x_tiles[g][j][:],
@@ -382,12 +392,17 @@ def tile_slidingwindowattention_pa_t_kernel(tc, x, ln_w, wq, wk, wv, out_0, out_
                 stage(index)
 
         first_sines()
-        on_gpsimd(cross_work(0))
+        nc.vector.tensor_scalar(
+            out=identity[:], in0=ramp[:], scalar1=float(TILES), scalar2=partition_4, op0=ALU.mult, op1=ALU.is_equal
+        )
         square_on_vector(0, range(TILES))
-        group_weights(nc, w_raw, w_grouped)
-        on_gpsimd(block_work(1))
-        on_gpsimd(block_work(2))
-        later = block_work(3)
+        on_gpsimd(
+            cross_work(0)
+            + [
+                (advance[:, 2:3], advance[:, 1:2], advance[:, 0:1], ALU.subtract),
+                (advance[:, 3:4], advance[:, 1:2], advance[:, 0:1], ALU.add),
+            ]
+        )
         for step in range(-3, GROUPS):
             run(copy_v, step, GROUPS)
             run(last_squares, step + 3, GROUPS)
@@ -396,12 +411,18 @@ def tile_slidingwindowattention_pa_t_kernel(tc, x, ln_w, wq, wk, wv, out_0, out_
             run(turn, step + 2, GROUPS)
             run(multiply_own_q, step, GROUPS)
             run(multiply_own_k, step, GROUPS)
-            if step + 1 == 0:
+            if step + 2 == 0:
+                group_weights(nc, w_raw, w_grouped)
                 quantise_weights(nc, w_grouped, w_codes, w_scales, split_codes, split_scales)
+                on_gpsimd(block_work(1))
+                table_work = block_work(2) + block_work(3)
+            if step == GROUPS - 2:
+                run(multiply_shared, step, GROUPS)
             run(quantise, step + 1, GROUPS)
             run(project, step + 1, GROUPS)
             run(regroup, step + 2, GROUPS)
-            run(multiply_shared, step, GROUPS)
+            if step != GROUPS - 2:
+                run(multiply_shared, step, GROUPS)
             run(add_and_store, step, GROUPS)
-            if 4 <= step < 8:
-                on_gpsimd(later[2 * (step - 4) : 2 * (step - 3)])
+            if 0 <= step < TABLE_STEPS:
+                on_gpsimd(table_work[step * len(table_work) // TABLE_STEPS : (step + 1) * len(table_work) // TABLE_STEPS])

@@ -404,9 +404,9 @@ def tile_slidingwindowattention_pa_t_kernel(tc, x, ln_w, wq, wk, wv, out_0, out_
             ]
         )
         for step in range(-3, GROUPS):
-            run(copy_v, step, GROUPS)
             run(last_squares, step + 3, GROUPS)
             run(first_squares, step + 4, GROUPS)
+            run(copy_v, step, GROUPS)
             run(normalise, step + 2, GROUPS)
             run(turn, step + 2, GROUPS)
             run(multiply_own_q, step, GROUPS)

@@ -23,6 +23,7 @@ PAIRS = HD // 2
 TILES = 4
 GROUP = TILES * P
 GROUPS = BATCH * SEQ // GROUP
+LAST = GROUPS - 1
 BLOCKS = SEQ // GROUP
 ROUND_TO_INTEGER = 1.5 * 2.0**23
 
@@ -109,14 +110,14 @@ def rotation_angles(nc, const, ones, ramp, partition_4):
 def tile_slidingwindowattention_pa_t_kernel(tc, x, ln_w, wq, wk, wv, out_0, out_1, out_2):
     nc = tc.nc
     by_group = "b (s p j) h d -> s b p (j h d)"
-    x_tiles_hbm = x.rearrange("b (s p j) d -> s b j p d", p=P, j=TILES)
+    x_hbm = x.rearrange("b (s p j) d -> s b p j d", p=P, j=TILES)
     q_groups = out_0.rearrange(by_group, p=P, j=TILES)
     k_groups = out_1.rearrange(by_group, p=P, j=TILES)
     v_groups = out_2.rearrange(by_group, p=P, j=TILES)
 
     with ExitStack() as ctx:
         const = ctx.enter_context(tc.tile_pool(name="const", bufs=1))
-        loads = ctx.enter_context(tc.tile_pool(name="loads", bufs=GROUPS * TILES))
+        loads = ctx.enter_context(tc.tile_pool(name="loads", bufs=GROUPS))
         small = ctx.enter_context(tc.tile_pool(name="small", bufs=6))
         work = ctx.enter_context(tc.tile_pool(name="work", bufs=3))
         stores = ctx.enter_context(tc.tile_pool(name="stores", bufs=4))
@@ -126,6 +127,8 @@ def tile_slidingwindowattention_pa_t_kernel(tc, x, ln_w, wq, wk, wv, out_0, out_
         psum_out = ctx.enter_context(tc.psum_pool(name="psum_out", bufs=1))
         ctx.enter_context(tc.manual_schedule())
 
+        gain_row = const.tile([P, D], BF16, name="gain_row")
+        nc.vector.memset(gain_row[:], 0.0)
         unit = const.tile([P, 1], F32, name="unit")
         nc.vector.memset(unit[:], 1.0)
         ones = const.tile([P, P], F32, name="ones")
@@ -139,8 +142,6 @@ def tile_slidingwindowattention_pa_t_kernel(tc, x, ln_w, wq, wk, wv, out_0, out_
         start_ps = psum_out.tile([P, TILES, HD], F32, name="q_ps")
         nc.tensor.matmul(out=start_ps[:, 0, 0:8], lhsT=ramp[:], rhs=fraction[:], start=True, stop=True)
         partition_4 = start_ps[:, 0, 0:1]
-        gain_row = const.tile([P, D], BF16, name="gain_row")
-        nc.vector.memset(gain_row[:], 0.0)
         ones_bf16 = const.tile([P, P], BF16, name="ones_bf16")
         nc.vector.memset(ones_bf16[:], 1.0)
 
@@ -152,23 +153,25 @@ def tile_slidingwindowattention_pa_t_kernel(tc, x, ln_w, wq, wk, wv, out_0, out_
         nc.scalar.mul(out=quarter_turn[:], in_=unit[:], mul=0.5 * math.pi)
         minus_quarter = const.tile([P, 1], F32, name="minus_quarter")
         nc.scalar.mul(out=minus_quarter[:], in_=unit[:], mul=-0.5 * math.pi)
-        nc.scalar.dma_start(out=gain_row[0:1, :], in_=ln_w.rearrange("(o d) -> o d", o=1))
-
         part, minus_abs = rotation_angles(nc, const, ones, ramp, partition_4)
 
-        x_tiles = [[loads.tile([P, D], BF16, name="x_t") for j in range(TILES)] for g in range(GROUPS)]
+        x_tiles = {}
         w_raw = const.tile([P, 3, PACK, HD], BF16, name="w_raw")
-        for g in range(1):
-            for j in range(TILES):
-                nc.sync.dma_start(out=x_tiles[g][j][:], in_=x_tiles_hbm[g // BATCH, g % BATCH, j])
-        for m, w in enumerate((wq, wk, wv)):
-            nc.sync.dma_start(
-                out=w_raw[:, m].rearrange("p (u e) n -> p u (e n)", u=2),
-                in_=w.rearrange("(u p e) n -> p u (e n)", u=2, e=2),
-            )
-        for g in range(1, GROUPS):
-            for j in range(TILES):
-                nc.sync.dma_start(out=x_tiles[g][j][:], in_=x_tiles_hbm[g // BATCH, g % BATCH, j])
+        for g in range(GROUPS):
+            group = loads.tile([P, TILES, D], BF16, name="x_g")
+            x_tiles[g] = [group[:, j] for j in range(TILES)]
+            pieces = {0: 4, 1: 2}.get(g, 1)
+            for piece in range(pieces):
+                rows = slice(piece * TILES // pieces, (piece + 1) * TILES // pieces)
+                nc.sync.dma_start(out=group[:, rows], in_=x_hbm[g // BATCH, g % BATCH][:, rows])
+            if g == 0:
+                nc.sync.dma_start(out=gain_row[0:1, :], in_=ln_w.rearrange("(o d) -> o d", o=1))
+            if g == 1:
+                for m, w in enumerate((wq, wk, wv)):
+                    nc.sync.dma_start(
+                        out=w_raw[:, m].rearrange("p (u e) n -> p u (e n)", u=2),
+                        in_=w.rearrange("(u p e) n -> p u (e n)", u=2, e=2),
+                    )
 
         gain = broadcast_gain(nc, psum_const, ones_bf16, gain_row)
         identity = const.tile([P, P], F32, name="identity")
@@ -229,7 +232,7 @@ def tile_slidingwindowattention_pa_t_kernel(tc, x, ln_w, wq, wk, wv, out_0, out_
                 squares = work.tile([P, D], BF16, name="squares")
                 nc.scalar.activation(
                     out=squares[:],
-                    in_=x_tiles[g][j][:],
+                    in_=x_tiles[g][j],
                     func=ACT.Square,
                     scale=1.0 / math.sqrt(D),
                     accum_out=mean_sqs[g][:, j : j + 1],
@@ -241,9 +244,9 @@ def tile_slidingwindowattention_pa_t_kernel(tc, x, ln_w, wq, wk, wv, out_0, out_
             for j in tiles:
                 nc.vector.scalar_tensor_tensor(
                     out=unread[:, j % 2 * D : (j % 2 + 1) * D],
-                    in0=x_tiles[g][j][:],
+                    in0=x_tiles[g][j],
                     scalar=1.0 / D,
-                    in1=x_tiles[g][j][:],
+                    in1=x_tiles[g][j],
                     op0=ALU.mult,
                     op1=ALU.mult,
                     accum_out=mean_sqs[g][:, j : j + 1],
@@ -266,7 +269,7 @@ def tile_slidingwindowattention_pa_t_kernel(tc, x, ln_w, wq, wk, wv, out_0, out_
                 cols = slice(j * D, (j + 1) * D)
                 nc.vector.scalar_tensor_tensor(
                     out=xn[:, cols],
-                    in0=x_tiles[g][j][:],
+                    in0=x_tiles[g][j],
                     scalar=rstds[g][:, j : j + 1],
                     in1=gain[:],
                     op0=ALU.mult,
@@ -369,16 +372,21 @@ def tile_slidingwindowattention_pa_t_kernel(tc, x, ln_w, wq, wk, wv, out_0, out_
 
         def add_and_store(g):
             own, shared = products[g]
-            rotated = stores.tile([P, 2, TILES, PAIRS, 2], F32, name="rotated")
-            if g < GROUPS - 1:
+            if g == LAST - 2:
+                rotated = groupeds[LAST][:].bitcast(F32).rearrange(
+                    "p (c j i h) -> p c j i h", c=2, j=TILES, h=2
+                )
+            else:
+                rotated = stores.tile([P, 2, TILES, PAIRS, 2], F32, name="rotated")[:]
+            if g < LAST - 1:
                 nc.gpsimd.tensor_tensor(
-                    out=rotated[:],
+                    out=rotated,
                     in0=own[:],
                     in1=shared[:].unsqueeze(4).to_broadcast([P, 2, TILES, PAIRS, 2]),
                     op=ALU.subtract,
                 )
             for c, hbm in enumerate((q_groups, k_groups)):
-                if g == GROUPS - 1:
+                if g >= LAST - 1:
                     nc.vector.tensor_tensor(
                         out=rotated[:, c],
                         in0=own[:, c],
@@ -411,18 +419,23 @@ def tile_slidingwindowattention_pa_t_kernel(tc, x, ln_w, wq, wk, wv, out_0, out_
             run(turn, step + 2, GROUPS)
             run(multiply_own_q, step, GROUPS)
             run(multiply_own_k, step, GROUPS)
+            if step == LAST:
+                add_and_store(step - 1)
             if step + 2 == 0:
                 group_weights(nc, w_raw, w_grouped)
                 quantise_weights(nc, w_grouped, w_codes, w_scales, split_codes, split_scales)
                 on_gpsimd(block_work(1))
                 table_work = block_work(2) + block_work(3)
-            if step == GROUPS - 2:
-                run(multiply_shared, step, GROUPS)
-            run(quantise, step + 1, GROUPS)
-            run(project, step + 1, GROUPS)
+            if step != LAST - 1:
+                run(quantise, step + 1, GROUPS)
+                run(project, step + 1, GROUPS)
             run(regroup, step + 2, GROUPS)
-            if step != GROUPS - 2:
-                run(multiply_shared, step, GROUPS)
-            run(add_and_store, step, GROUPS)
+            run(multiply_shared, step, GROUPS)
+            if step == LAST - 2:
+                quantise(LAST)
+            if step == LAST - 1:
+                project(LAST)
+            if step != LAST - 1:
+                run(add_and_store, step, GROUPS)
             if 0 <= step < TABLE_STEPS:
                 on_gpsimd(table_work[step * len(table_work) // TABLE_STEPS : (step + 1) * len(table_work) // TABLE_STEPS])

@@ -18,7 +18,6 @@ BASE = 10000.0
 
 P = 128
 PACK = 4
-TABLE_STEPS = 11
 PAIRS = HD // 2
 TILES = 4
 GROUP = TILES * P
@@ -127,8 +126,6 @@ def tile_slidingwindowattention_pa_t_kernel(tc, x, ln_w, wq, wk, wv, out_0, out_
         psum_out = ctx.enter_context(tc.psum_pool(name="psum_out", bufs=1))
         ctx.enter_context(tc.manual_schedule())
 
-        gain_row = const.tile([P, D], BF16, name="gain_row")
-        nc.vector.memset(gain_row[:], 0.0)
         unit = const.tile([P, 1], F32, name="unit")
         nc.vector.memset(unit[:], 1.0)
         ones = const.tile([P, P], F32, name="ones")
@@ -142,6 +139,8 @@ def tile_slidingwindowattention_pa_t_kernel(tc, x, ln_w, wq, wk, wv, out_0, out_
         start_ps = psum_out.tile([P, TILES, HD], F32, name="q_ps")
         nc.tensor.matmul(out=start_ps[:, 0, 0:8], lhsT=ramp[:], rhs=fraction[:], start=True, stop=True)
         partition_4 = start_ps[:, 0, 0:1]
+        gain_row = const.tile([P, D], BF16, name="gain_row")
+        nc.vector.memset(gain_row[:], 0.0)
         ones_bf16 = const.tile([P, P], BF16, name="ones_bf16")
         nc.vector.memset(ones_bf16[:], 1.0)
 
@@ -165,14 +164,12 @@ def tile_slidingwindowattention_pa_t_kernel(tc, x, ln_w, wq, wk, wv, out_0, out_
                 rows = slice(piece * TILES // pieces, (piece + 1) * TILES // pieces)
                 nc.sync.dma_start(out=group[:, rows], in_=x_hbm[g // BATCH, g % BATCH][:, rows])
             if g == 0:
-                nc.sync.dma_start(out=gain_row[0:1, :], in_=ln_w.rearrange("(o d) -> o d", o=1))
-            if g == 1:
                 for m, w in enumerate((wq, wk, wv)):
                     nc.sync.dma_start(
                         out=w_raw[:, m].rearrange("p (u e) n -> p u (e n)", u=2),
                         in_=w.rearrange("(u p e) n -> p u (e n)", u=2, e=2),
                     )
-
+                nc.sync.dma_start(out=gain_row[0:1, :], in_=ln_w.rearrange("(o d) -> o d", o=1))
         gain = broadcast_gain(nc, psum_const, ones_bf16, gain_row)
         identity = const.tile([P, P], F32, name="identity")
         w_grouped = const.tile([P, 3, HD, PACK], BF16, name="w_grouped", align_bytes=64)
@@ -182,42 +179,73 @@ def tile_slidingwindowattention_pa_t_kernel(tc, x, ln_w, wq, wk, wv, out_0, out_
         split_scales = const.tile([P, 2, HD], U8, name="split_scales", align_bytes=64)
 
         minus_cos = const.tile([P, BLOCKS * TILES, PAIRS], F32, name="minus_cos")
-        sin = const.tile([P, BLOCKS * TILES, PAIRS], F32, name="sin")
-        cross = const.tile([P, BLOCKS * TILES, PAIRS, 2], F32, name="cross")
-        advance = const.tile([P, 4, PAIRS], F32, name="advance")
+        sin = const.tile([P, 2 * TILES, PAIRS], F32, name="sin")
+        cross = [
+            w_raw[:].rearrange("p m t n -> p (m t n)").bitcast(F32)[:, 0 : 2 * TILES * PAIRS].rearrange(
+                "p (j i h) -> p j i h", i=PAIRS, h=2
+            ),
+        ]
+        for s in range(1, BLOCKS):
+            table = const.tile([P, TILES, PAIRS, 2], F32, name="cross_%d" % s)
+            cross.append(table[:])
+        advance = const.tile([P, 5, 1, PAIRS], F32, name="advance")
 
         def block_rows(s):
             return slice(s * TILES, (s + 1) * TILES)
 
         def first_sines():
-            for out, angle, rows, bias, scale in (
-                (minus_cos[:, 0:TILES], minus_abs, slice(0, TILES), minus_quarter, -2.0 * math.pi),
-                (advance[:, 0:1], minus_abs, slice(TILES, TILES + 1), quarter_turn, 2.0 * math.pi),
-            ):
-                nc.scalar.activation(out=out, in_=angle[:, rows], func=ACT.Sin, bias=bias[:], scale=scale)
-            for out, rows in ((sin[:, 0:TILES], slice(0, TILES)), (advance[:, 1:2], slice(TILES, TILES + 1))):
+            own, steps = slice(0, TILES), slice(TILES, TILES + 1)
+            for out, rows in ((sin[:, own], own), (advance[:, 1], steps)):
                 nc.scalar.activation(out=out, in_=part[:, rows], func=ACT.Sin, scale=2.0 * math.pi)
+            for out, rows, bias, scale in (
+                (minus_cos[:, own], own, minus_quarter, -2.0 * math.pi),
+                (advance[:, 0], steps, quarter_turn, 2.0 * math.pi),
+            ):
+                nc.scalar.activation(out=out, in_=minus_abs[:, rows], func=ACT.Sin, bias=bias[:], scale=scale)
 
         def cross_work(s):
             rows = block_rows(s)
             return [
-                (cross[:, rows, :, h], minus_cos[:, rows], sin[:, rows], op)
+                (cross[s][:, :, :, h], minus_cos[:, rows], sin[:, rows], op)
                 for h, op in ((0, ALU.subtract), (1, ALU.add))
             ]
 
-        def block_work(s):
-            shape = [P, TILES, PAIRS]
-            old, new = block_rows(s - 1), block_rows(s)
+        block_shape = [P, TILES, PAIRS]
+
+        def advance_by(kind):
+            return advance[:, kind].to_broadcast(block_shape)
+
+        def first_turn():
+            old, new = block_rows(0), block_rows(1)
             parts = w_grouped[:].rearrange("p m n t -> p (m n t)").bitcast(F32).rearrange(
                 "p (a j i) -> p a j i", a=3, i=PAIRS
             )
             return [
-                (parts[:, 2], minus_cos[:, old], advance[:, 3:4].to_broadcast(shape), ALU.mult),
-                (parts[:, 1], sin[:, old], advance[:, 2:3].to_broadcast(shape), ALU.mult),
-                (parts[:, 0], cross[:, old, :, 1], advance[:, 0:1].to_broadcast(shape), ALU.mult),
-                (minus_cos[:, new], parts[:, 0], parts[:, 1], ALU.add),
-                (sin[:, new], parts[:, 0], parts[:, 2], ALU.subtract),
-            ] + cross_work(s)
+                (parts[:, 2], cross[0][:, :, :, 1], advance_by(0), ALU.mult),
+                (advance[:, 2], advance[:, 1], advance[:, 0], ALU.subtract),
+                (advance[:, 3], advance[:, 1], advance[:, 0], ALU.add),
+                (advance[:, 4], advance[:, 0], advance[:, 0], ALU.add),
+                (parts[:, 1], sin[:, old], advance_by(2), ALU.mult),
+                (parts[:, 0], minus_cos[:, old], advance_by(3), ALU.mult),
+                (minus_cos[:, new], parts[:, 2], parts[:, 1], ALU.add),
+                (sin[:, new], parts[:, 2], parts[:, 0], ALU.subtract),
+            ] + cross_work(1)
+
+        def late_table(s):
+            half = TILES // 2
+            product = const.tile([P, half, PAIRS, 2], F32, name="product")
+            work_list = []
+            for rows in (slice(0, half), slice(half, TILES)):
+                doubled = advance[:, 4].unsqueeze(3).to_broadcast([P, half, PAIRS, 2])
+                work_list += [
+                    (product[:], cross[s - 1][:, rows], doubled, ALU.mult),
+                    (cross[s][:, rows], product[:], cross[s - 2][:, rows], ALU.subtract),
+                ]
+            turned = product[:].rearrange("p j i h -> p (j i h)").rearrange("p (j i) -> p j i", i=PAIRS)
+            return work_list + [
+                (turned, minus_cos[:, block_rows(s - 1)], advance_by(4), ALU.mult),
+                (minus_cos[:, block_rows(s)], turned, minus_cos[:, block_rows(s - 2)], ALU.subtract),
+            ]
 
         def on_gpsimd(work_list):
             for out, in0, in1, op in work_list:
@@ -239,8 +267,9 @@ def tile_slidingwindowattention_pa_t_kernel(tc, x, ln_w, wq, wk, wv, out_0, out_
                 )
 
         def square_on_vector(g, tiles):
-            unread = cross[:, 0:TILES].rearrange("p j i h -> p (j i h)").bitcast(BF16)
-            mean_sqs[g] = small.tile([P, TILES], F32, name="mean_sq")
+            unread = work.tile([P, 2 * D], BF16, name="unread")
+            if g not in mean_sqs:
+                mean_sqs[g] = small.tile([P, TILES], F32, name="mean_sq")
             for j in tiles:
                 nc.vector.scalar_tensor_tensor(
                     out=unread[:, j % 2 * D : (j % 2 + 1) * D],
@@ -264,18 +293,16 @@ def tile_slidingwindowattention_pa_t_kernel(tc, x, ln_w, wq, wk, wv, out_0, out_
             )
 
         def normalise(g):
-            xn = work.tile([P, TILES * D], BF16, name="xn")
+            xns[g] = work.tile([P, TILES * D], BF16, name="xn")
             for j in range(TILES):
-                cols = slice(j * D, (j + 1) * D)
                 nc.vector.scalar_tensor_tensor(
-                    out=xn[:, cols],
+                    out=xns[g][:, j * D : (j + 1) * D],
                     in0=x_tiles[g][j],
                     scalar=rstds[g][:, j : j + 1],
                     in1=gain[:],
                     op0=ALU.mult,
                     op1=ALU.mult,
                 )
-            xns[g] = xn
 
         def turn(g):
             words = xns[g][:].bitcast(F32).rearrange("p (j u w) -> p j u w", j=TILES, u=2)
@@ -338,23 +365,21 @@ def tile_slidingwindowattention_pa_t_kernel(tc, x, ln_w, wq, wk, wv, out_0, out_
             banks[g] = (sum_ps, q_ps, k_ps, v_ps)
 
         def multiply_shared(g):
-            rows = slice((g // BATCH) * TILES, (g // BATCH + 1) * TILES)
             shape = [P, TILES, 2, PAIRS]
             shared = work.tile([P, 2, TILES, PAIRS], F32, name="shared")
             nc.vector.tensor_tensor(
                 out=shared[:].rearrange("p c j i -> p j c i"),
                 in0=banks[g][0][:].rearrange("p j (c i) -> p j c i", c=2),
-                in1=minus_cos[:, rows].unsqueeze(2).to_broadcast(shape),
+                in1=minus_cos[:, block_rows(g // BATCH)].unsqueeze(2).to_broadcast(shape),
                 op=ALU.mult,
             )
             products[g].append(shared)
 
         def multiply_own(g, c):
-            rows = slice((g // BATCH) * TILES, (g // BATCH + 1) * TILES)
             nc.vector.tensor_tensor(
                 out=products[g][0][:, c],
                 in0=banks[g][1 + c][:].rearrange("p j (i h) -> p j i h", h=2),
-                in1=cross[:, rows],
+                in1=cross[g // BATCH],
                 op=ALU.mult,
             )
 
@@ -400,17 +425,15 @@ def tile_slidingwindowattention_pa_t_kernel(tc, x, ln_w, wq, wk, wv, out_0, out_
                 stage(index)
 
         first_sines()
+        nc.scalar.activation(out=warm[:], in_=unit[:], func=ACT.Abs_reciprocal_sqrt, scale=1.0)
+        square_on_vector(0, range(TILES - 1))
+        square(0, range(TILES - 1, TILES))
         nc.vector.tensor_scalar(
             out=identity[:], in0=ramp[:], scalar1=float(TILES), scalar2=partition_4, op0=ALU.mult, op1=ALU.is_equal
         )
-        square_on_vector(0, range(TILES))
-        on_gpsimd(
-            cross_work(0)
-            + [
-                (advance[:, 2:3], advance[:, 1:2], advance[:, 0:1], ALU.subtract),
-                (advance[:, 3:4], advance[:, 1:2], advance[:, 0:1], ALU.add),
-            ]
-        )
+        group_weights(nc, w_raw, w_grouped)
+        on_gpsimd(cross_work(0))
+        late_work = late_table(2) + late_table(3)
         for step in range(-3, GROUPS):
             run(last_squares, step + 3, GROUPS)
             run(first_squares, step + 4, GROUPS)
@@ -422,10 +445,8 @@ def tile_slidingwindowattention_pa_t_kernel(tc, x, ln_w, wq, wk, wv, out_0, out_
             if step == LAST:
                 add_and_store(step - 1)
             if step + 2 == 0:
-                group_weights(nc, w_raw, w_grouped)
                 quantise_weights(nc, w_grouped, w_codes, w_scales, split_codes, split_scales)
-                on_gpsimd(block_work(1))
-                table_work = block_work(2) + block_work(3)
+                on_gpsimd(first_turn())
             if step != LAST - 1:
                 run(quantise, step + 1, GROUPS)
                 run(project, step + 1, GROUPS)
@@ -437,5 +458,5 @@ def tile_slidingwindowattention_pa_t_kernel(tc, x, ln_w, wq, wk, wv, out_0, out_
                 project(LAST)
             if step != LAST - 1:
                 run(add_and_store, step, GROUPS)
-            if 0 <= step < TABLE_STEPS:
-                on_gpsimd(table_work[step * len(table_work) // TABLE_STEPS : (step + 1) * len(table_work) // TABLE_STEPS])
+            if 0 <= step + 1 < len(late_work):
+                on_gpsimd(late_work[step + 1 : step + 2])

@@ -23,6 +23,8 @@ TILES = 4
 GROUP = TILES * P
 GROUPS = BATCH * SEQ // GROUP
 LAST = GROUPS - 1
+FAST_PAIRS = 40
+assert GROUP * BASE ** (-FAST_PAIRS / PAIRS) / (2.0 * math.pi) <= 0.5
 BLOCKS = SEQ // GROUP
 ROUND_TO_INTEGER = 1.5 * 2.0**23
 
@@ -81,24 +83,24 @@ def rotation_angles(nc, const, ones, ramp, partition_4):
     )
 
     shape = [P, TILES + 1, PAIRS]
-    turns = const.tile(shape, F32, name="turns")
+    part = const.tile(shape, F32, name="part")
     nc.vector.tensor_tensor(
-        out=turns[:],
+        out=part[:],
         in0=position[:].unsqueeze(2).to_broadcast(shape),
         in1=frequency[:].unsqueeze(1).to_broadcast(shape),
         op=ALU.mult,
     )
-    whole = const.tile(shape, F32, name="whole")
+    fast = part[:, :, 0:FAST_PAIRS]
+    whole = const.tile([P, TILES + 1, FAST_PAIRS], F32, name="whole")
     nc.vector.tensor_scalar(
         out=whole[:],
-        in0=turns[:],
+        in0=fast,
         scalar1=ROUND_TO_INTEGER,
         scalar2=ROUND_TO_INTEGER,
         op0=ALU.add,
         op1=ALU.subtract,
     )
-    part = const.tile(shape, F32, name="part")
-    nc.vector.tensor_tensor(out=part[:], in0=turns[:], in1=whole[:], op=ALU.subtract)
+    nc.vector.tensor_tensor(out=fast, in0=fast, in1=whole[:], op=ALU.subtract)
     minus_abs = const.tile(shape, F32, name="minus_abs")
     nc.vector.scalar_tensor_tensor(
         out=minus_abs[:], in0=part[:], scalar=-1.0, in1=part[:], op0=ALU.mult, op1=ALU.min
@@ -393,7 +395,8 @@ def tile_slidingwindowattention_pa_t_kernel(tc, x, ln_w, wq, wk, wv, out_0, out_
         def copy_v(g):
             v_sb = stores.tile([P, TILES * HD], F32, name="v_sb")
             nc.scalar.copy(out=v_sb[:], in_=banks[g][3][:].rearrange("p j d -> p (j d)"))
-            nc.sync.dma_start(out=v_groups[g // BATCH, g % BATCH], in_=v_sb[:])
+            queue = nc.scalar if g >= LAST - 1 else nc.sync
+            queue.dma_start(out=v_groups[g // BATCH, g % BATCH], in_=v_sb[:])
 
         def add_and_store(g):
             own, shared = products[g]
@@ -411,14 +414,20 @@ def tile_slidingwindowattention_pa_t_kernel(tc, x, ln_w, wq, wk, wv, out_0, out_
                     op=ALU.subtract,
                 )
             for c, hbm in enumerate((q_groups, k_groups)):
-                if g >= LAST - 1:
-                    nc.vector.tensor_tensor(
-                        out=rotated[:, c],
-                        in0=own[:, c],
-                        in1=shared[:, c].unsqueeze(3).to_broadcast([P, TILES, PAIRS, 2]),
-                        op=ALU.subtract,
+                pieces = 2 if g == LAST and c == 1 else 1
+                for piece in range(pieces):
+                    tiles = slice(piece * TILES // pieces, (piece + 1) * TILES // pieces)
+                    if g >= LAST - 1:
+                        nc.vector.tensor_tensor(
+                            out=rotated[:, c, tiles],
+                            in0=own[:, c, tiles],
+                            in1=shared[:, c, tiles].unsqueeze(3).to_broadcast([P, TILES // pieces, PAIRS, 2]),
+                            op=ALU.subtract,
+                        )
+                    nc.sync.dma_start(
+                        out=hbm[g // BATCH, g % BATCH].rearrange("p (j d) -> p j d", j=TILES)[:, tiles],
+                        in_=rotated[:, c, tiles].rearrange("p j i h -> p j (i h)"),
                     )
-                nc.sync.dma_start(out=hbm[g // BATCH, g % BATCH], in_=rotated[:, c].rearrange("p j i h -> p (j i h)"))
 
         def run(stage, index, count):
             if 0 <= index < count:

@@ -23,6 +23,8 @@ TILES = 4
 GROUP = TILES * P
 GROUPS = BATCH * SEQ // GROUP
 LAST = GROUPS - 1
+LATE_STEPS = 6
+GROUPEDS = 13
 FAST_PAIRS = 40
 assert GROUP * BASE ** (-FAST_PAIRS / PAIRS) / (2.0 * math.pi) <= 0.5
 BLOCKS = SEQ // GROUP
@@ -121,7 +123,7 @@ def tile_slidingwindowattention_pa_t_kernel(tc, x, ln_w, wq, wk, wv, out_0, out_
         loads = ctx.enter_context(tc.tile_pool(name="loads", bufs=GROUPS))
         small = ctx.enter_context(tc.tile_pool(name="small", bufs=6))
         work = ctx.enter_context(tc.tile_pool(name="work", bufs=3))
-        stores = ctx.enter_context(tc.tile_pool(name="stores", bufs=4))
+        stores = ctx.enter_context(tc.tile_pool(name="stores", bufs=GROUPS))
         psum_const = ctx.enter_context(tc.psum_pool(name="psum_const", bufs=1))
         psum_turned = ctx.enter_context(tc.psum_pool(name="psum_turned", bufs=3))
         psum_sums = ctx.enter_context(tc.psum_pool(name="psum_sums", bufs=1))
@@ -138,7 +140,7 @@ def tile_slidingwindowattention_pa_t_kernel(tc, x, ln_w, wq, wk, wv, out_0, out_
         )
         fraction = const.tile([P, 8], F32, name="fraction")
         nc.vector.memset(fraction[:], TILES / P)
-        start_ps = psum_out.tile([P, TILES, HD], F32, name="q_ps")
+        start_ps = psum_out.tile([P, TILES, HD], F32, name="v_ps")
         nc.tensor.matmul(out=start_ps[:, 0, 0:8], lhsT=ramp[:], rhs=fraction[:], start=True, stop=True)
         partition_4 = start_ps[:, 0, 0:1]
         gain_row = const.tile([P, D], BF16, name="gain_row")
@@ -156,10 +158,11 @@ def tile_slidingwindowattention_pa_t_kernel(tc, x, ln_w, wq, wk, wv, out_0, out_
         nc.scalar.mul(out=minus_quarter[:], in_=unit[:], mul=-0.5 * math.pi)
         part, minus_abs = rotation_angles(nc, const, ones, ramp, partition_4)
 
-        x_tiles = {}
+        x_groups, x_tiles = {}, {}
         w_raw = const.tile([P, 3, PACK, HD], BF16, name="w_raw")
         for g in range(GROUPS):
             group = loads.tile([P, TILES, D], BF16, name="x_g")
+            x_groups[g] = group
             x_tiles[g] = [group[:, j] for j in range(TILES)]
             pieces = {0: 4, 1: 2}.get(g, 1)
             for piece in range(pieces):
@@ -180,16 +183,15 @@ def tile_slidingwindowattention_pa_t_kernel(tc, x, ln_w, wq, wk, wv, out_0, out_
         split_codes = const.tile([P, 2, HD], U32, name="split_codes", align_bytes=64)
         split_scales = const.tile([P, 2, HD], U8, name="split_scales", align_bytes=64)
 
-        minus_cos = const.tile([P, BLOCKS * TILES, PAIRS], F32, name="minus_cos")
+        minus_cos = const.tile([P, 2 * TILES, PAIRS], F32, name="minus_cos")
         sin = const.tile([P, 2 * TILES, PAIRS], F32, name="sin")
+        cross_1 = const.tile([P, TILES, PAIRS, 2], F32, name="cross_1")
         cross = [
             w_raw[:].rearrange("p m t n -> p (m t n)").bitcast(F32)[:, 0 : 2 * TILES * PAIRS].rearrange(
                 "p (j i h) -> p j i h", i=PAIRS, h=2
             ),
+            cross_1[:],
         ]
-        for s in range(1, BLOCKS):
-            table = const.tile([P, TILES, PAIRS, 2], F32, name="cross_%d" % s)
-            cross.append(table[:])
         advance = const.tile([P, 5, 1, PAIRS], F32, name="advance")
 
         def block_rows(s):
@@ -224,30 +226,43 @@ def tile_slidingwindowattention_pa_t_kernel(tc, x, ln_w, wq, wk, wv, out_0, out_
             )
             return [
                 (parts[:, 2], cross[0][:, :, :, 1], advance_by(0), ALU.mult),
-                (advance[:, 2], advance[:, 1], advance[:, 0], ALU.subtract),
-                (advance[:, 3], advance[:, 1], advance[:, 0], ALU.add),
-                (advance[:, 4], advance[:, 0], advance[:, 0], ALU.add),
                 (parts[:, 1], sin[:, old], advance_by(2), ALU.mult),
                 (parts[:, 0], minus_cos[:, old], advance_by(3), ALU.mult),
                 (minus_cos[:, new], parts[:, 2], parts[:, 1], ALU.add),
                 (sin[:, new], parts[:, 2], parts[:, 0], ALU.subtract),
             ] + cross_work(1)
 
-        def late_table(s):
-            half = TILES // 2
-            product = const.tile([P, half, PAIRS, 2], F32, name="product")
-            work_list = []
-            for rows in (slice(0, half), slice(half, TILES)):
-                doubled = advance[:, 4].unsqueeze(3).to_broadcast([P, half, PAIRS, 2])
-                work_list += [
-                    (product[:], cross[s - 1][:, rows], doubled, ALU.mult),
-                    (cross[s][:, rows], product[:], cross[s - 2][:, rows], ALU.subtract),
-                ]
-            turned = product[:].rearrange("p j i h -> p (j i h)").rearrange("p (j i) -> p j i", i=PAIRS)
-            return work_list + [
-                (turned, minus_cos[:, block_rows(s - 1)], advance_by(4), ALU.mult),
-                (minus_cos[:, block_rows(s)], turned, minus_cos[:, block_rows(s - 2)], ALU.subtract),
-            ]
+        half = TILES // 2 * PAIRS * 2
+
+        def hosted(g):
+            return groupeds[g][:].bitcast(F32)
+
+        def cross_half(s, part_of):
+            if s < 2:
+                return cross[s].rearrange("p j i h -> p (j i h)")[:, part_of * half : (part_of + 1) * half]
+            return hosted(LATE_STEPS * (s - 2) + 2 + 2 * part_of)[:, 0:half]
+
+        def minus_cosine(s):
+            if s < 2:
+                return minus_cos[:, block_rows(s)]
+            return hosted(LATE_STEPS * (s - 2) + 6)[:, 0:half].rearrange("p (j i) -> p j i", i=PAIRS)
+
+        def late_table(step):
+            s, phase = 2 + step // LATE_STEPS, step % LATE_STEPS
+            target, product = hosted(step + 1)[:, 0:half], hosted(step)[:, 0:half]
+            if phase < 4:
+                shape = [P, TILES // 2, PAIRS, 2]
+                doubled = advance[:, 4].unsqueeze(3).to_broadcast(shape)
+                older = cross_half(s - 1 - phase % 2, phase // 2)
+                pairs = "p (j i h) -> p j i h"
+                if phase % 2 == 0:
+                    out, in0 = (ap.rearrange(pairs, i=PAIRS, h=2) for ap in (target, older))
+                    return [(out, in0, doubled, ALU.mult)]
+                return [(target, product, older, ALU.subtract)]
+            target, product = (ap.rearrange("p (j i) -> p j i", i=PAIRS) for ap in (target, product))
+            if phase == 4:
+                return [(target, minus_cosine(s - 1), advance_by(4), ALU.mult)]
+            return [(target, product, minus_cosine(s - 2), ALU.subtract)]
 
         def on_gpsimd(work_list):
             for out, in0, in1, op in work_list:
@@ -317,7 +332,7 @@ def tile_slidingwindowattention_pa_t_kernel(tc, x, ln_w, wq, wk, wv, out_0, out_
                 turneds[g].append(turned)
 
         def regroup(g):
-            grouped = work.tile([P, GROUP * PACK], BF16, name="grouped", align_bytes=64)
+            grouped = work.tile([P, GROUP * PACK], BF16, name="grouped", align_bytes=64, bufs=GROUPEDS)
             words = grouped[:].bitcast(F32).rearrange("p (b j t u) -> p b j t u", b=2, j=2, u=2)
             for b, turned in enumerate(turneds[g]):
                 nc.scalar.copy(out=words[:, b], in_=turned[:].rearrange("p j u t -> p j t u"))
@@ -332,24 +347,26 @@ def tile_slidingwindowattention_pa_t_kernel(tc, x, ln_w, wq, wk, wv, out_0, out_
         def project(g):
             codes, scales = operands[g]
 
-            def passes(bank, operand, start, stop):
-                for j in range(TILES):
+            def passes(bank, operand, tiles):
+                for j in tiles:
                     tokens = slice(j * P, (j + 1) * P)
                     nc.tensor.matmul_mx(
-                        out=bank[:, j, :],
+                        out=bank[:, j - tiles[0], :],
                         lhsT=codes[:, tokens].bitcast(FP8X4),
                         lhsT_scale=scales[:, tokens],
                         rhs=w_codes[:, operand].bitcast(FP8X4),
                         rhs_scale=w_scales[:, operand],
-                        start=start,
-                        stop=stop,
+                        start=True,
+                        stop=True,
                     )
 
-            q_ps = psum_out.tile([P, TILES, HD], F32, name="q_ps")
-            k_ps = psum_out.tile([P, TILES, HD], F32, name="k_ps")
+            own_ps = [
+                psum_out.tile([P, 2, TILES // 2, HD], F32, name="own_ps_%d" % first) for first in range(2)
+            ]
             v_ps = psum_out.tile([P, TILES, HD], F32, name="v_ps")
-            passes(q_ps, 0, True, True)
-            passes(k_ps, 1, True, True)
+            for first in range(2):
+                for operand in range(2):
+                    passes(own_ps[first][:, operand], operand, range(2 * first, 2 * first + 2))
             sum_ps = psum_sums.tile([P, TILES, HD], F32, name="sum_ps")
             for j in range(TILES):
                 tokens = slice(j * P, (j + 1) * P)
@@ -363,54 +380,60 @@ def tile_slidingwindowattention_pa_t_kernel(tc, x, ln_w, wq, wk, wv, out_0, out_
                         start=(operand == 0),
                         stop=(operand == 1),
                     )
-            passes(v_ps, 2, True, True)
-            banks[g] = (sum_ps, q_ps, k_ps, v_ps)
+            passes(v_ps[:], 2, range(TILES))
+            banks[g] = (sum_ps, own_ps, v_ps)
 
         def multiply_shared(g):
             shape = [P, TILES, 2, PAIRS]
-            shared = work.tile([P, 2, TILES, PAIRS], F32, name="shared")
+            shared = hosted(g)[:, 2 * TILES * PAIRS :].rearrange("p (c j i) -> p c j i", c=2, j=TILES)
             nc.vector.tensor_tensor(
-                out=shared[:].rearrange("p c j i -> p j c i"),
+                out=shared.rearrange("p c j i -> p j c i"),
                 in0=banks[g][0][:].rearrange("p j (c i) -> p j c i", c=2),
-                in1=minus_cos[:, block_rows(g // BATCH)].unsqueeze(2).to_broadcast(shape),
+                in1=minus_cosine(g // BATCH).unsqueeze(2).to_broadcast(shape),
                 op=ALU.mult,
             )
             products[g].append(shared)
 
-        def multiply_own(g, c):
+        def multiply_own(g, first):
+            table = cross_half(g // BATCH, first)
             nc.vector.tensor_tensor(
-                out=products[g][0][:, c],
-                in0=banks[g][1 + c][:].rearrange("p j (i h) -> p j i h", h=2),
-                in1=cross[g // BATCH],
+                out=products[g][0].rearrange("p c j i h -> p c (j i h)")[:, :, first * half : (first + 1) * half],
+                in0=banks[g][1][first][:].rearrange("p c j d -> p c (j d)"),
+                in1=table.unsqueeze(1).to_broadcast([P, 2, half]),
                 op=ALU.mult,
             )
 
-        def multiply_own_q(g):
-            products[g] = [work.tile([P, 2, TILES, PAIRS, 2], F32, name="own")]
+        def multiply_first(g):
+            own = x_groups[g][:].rearrange("p j d -> p (j d)").bitcast(F32)
+            products[g] = [own.rearrange("p (c j i h) -> p c j i h", c=2, j=TILES, h=2)]
             multiply_own(g, 0)
 
-        def multiply_own_k(g):
+        def multiply_last(g):
             multiply_own(g, 1)
 
         def copy_v(g):
             v_sb = stores.tile([P, TILES * HD], F32, name="v_sb")
-            nc.scalar.copy(out=v_sb[:], in_=banks[g][3][:].rearrange("p j d -> p (j d)"))
+            nc.scalar.copy(out=v_sb[:], in_=banks[g][2][:].rearrange("p j d -> p (j d)"))
             queue = nc.scalar if g >= LAST - 1 else nc.sync
             queue.dma_start(out=v_groups[g // BATCH, g % BATCH], in_=v_sb[:])
 
         def add_and_store(g):
             own, shared = products[g]
+            rotated = [own[:, c] for c in range(2)]
             if g == LAST - 2:
-                rotated = groupeds[LAST][:].bitcast(F32).rearrange(
-                    "p (c j i h) -> p c j i h", c=2, j=TILES, h=2
-                )
-            else:
-                rotated = stores.tile([P, 2, TILES, PAIRS, 2], F32, name="rotated")[:]
-            if g < LAST - 1:
+                rotated[0] = hosted(LAST)[:, 0 : 2 * half].rearrange("p (j i h) -> p j i h", j=TILES, h=2)
+                for c in range(2):
+                    nc.gpsimd.tensor_tensor(
+                        out=rotated[c],
+                        in0=own[:, c],
+                        in1=shared[:, c].unsqueeze(3).to_broadcast([P, TILES, PAIRS, 2]),
+                        op=ALU.subtract,
+                    )
+            elif g < LAST - 2:
                 nc.gpsimd.tensor_tensor(
-                    out=rotated,
-                    in0=own[:],
-                    in1=shared[:].unsqueeze(4).to_broadcast([P, 2, TILES, PAIRS, 2]),
+                    out=own,
+                    in0=own,
+                    in1=shared.unsqueeze(4).to_broadcast([P, 2, TILES, PAIRS, 2]),
                     op=ALU.subtract,
                 )
             for c, hbm in enumerate((q_groups, k_groups)):
@@ -419,14 +442,14 @@ def tile_slidingwindowattention_pa_t_kernel(tc, x, ln_w, wq, wk, wv, out_0, out_
                     tiles = slice(piece * TILES // pieces, (piece + 1) * TILES // pieces)
                     if g >= LAST - 1:
                         nc.vector.tensor_tensor(
-                            out=rotated[:, c, tiles],
+                            out=rotated[c][:, tiles],
                             in0=own[:, c, tiles],
                             in1=shared[:, c, tiles].unsqueeze(3).to_broadcast([P, TILES // pieces, PAIRS, 2]),
                             op=ALU.subtract,
                         )
                     nc.sync.dma_start(
                         out=hbm[g // BATCH, g % BATCH].rearrange("p (j d) -> p j d", j=TILES)[:, tiles],
-                        in_=rotated[:, c, tiles].rearrange("p j i h -> p j (i h)"),
+                        in_=rotated[c][:, tiles].rearrange("p j i h -> p j (i h)"),
                     )
 
         def run(stage, index, count):
@@ -441,16 +464,22 @@ def tile_slidingwindowattention_pa_t_kernel(tc, x, ln_w, wq, wk, wv, out_0, out_
             out=identity[:], in0=ramp[:], scalar1=float(TILES), scalar2=partition_4, op0=ALU.mult, op1=ALU.is_equal
         )
         group_weights(nc, w_raw, w_grouped)
-        on_gpsimd(cross_work(0))
-        late_work = late_table(2) + late_table(3)
+        on_gpsimd(
+            cross_work(0)
+            + [
+                (advance[:, 2], advance[:, 1], advance[:, 0], ALU.subtract),
+                (advance[:, 3], advance[:, 1], advance[:, 0], ALU.add),
+                (advance[:, 4], advance[:, 0], advance[:, 0], ALU.add),
+            ]
+        )
         for step in range(-3, GROUPS):
             run(last_squares, step + 3, GROUPS)
             run(first_squares, step + 4, GROUPS)
             run(copy_v, step, GROUPS)
             run(normalise, step + 2, GROUPS)
             run(turn, step + 2, GROUPS)
-            run(multiply_own_q, step, GROUPS)
-            run(multiply_own_k, step, GROUPS)
+            run(multiply_first, step, GROUPS)
+            run(multiply_last, step, GROUPS)
             if step == LAST:
                 add_and_store(step - 1)
             if step + 2 == 0:
@@ -460,6 +489,8 @@ def tile_slidingwindowattention_pa_t_kernel(tc, x, ln_w, wq, wk, wv, out_0, out_
                 run(quantise, step + 1, GROUPS)
                 run(project, step + 1, GROUPS)
             run(regroup, step + 2, GROUPS)
+            if 0 <= step < LATE_STEPS * (BLOCKS - 2):
+                on_gpsimd(late_table(step))
             run(multiply_shared, step, GROUPS)
             if step == LAST - 2:
                 quantise(LAST)
@@ -467,5 +498,3 @@ def tile_slidingwindowattention_pa_t_kernel(tc, x, ln_w, wq, wk, wv, out_0, out_
                 project(LAST)
             if step != LAST - 1:
                 run(add_and_store, step, GROUPS)
-            if 0 <= step + 1 < len(late_work):
-                on_gpsimd(late_work[step + 1 : step + 2])

import math
from contextlib import ExitStack

import concourse.mybir as mybir

F32 = mybir.dt.float32
BF16 = mybir.dt.bfloat16
I32 = mybir.dt.int32
U32 = mybir.dt.uint32
U8 = mybir.dt.uint8
FP8X4 = mybir.dt.float8_e4m3fn_x4
ALU = mybir.AluOpType
ACT = mybir.ActivationFunctionType

BATCH, SEQ, D, HD = 4, 2048, 512, 128
EPS = 1e-6
BASE = 10000.0

P = 128
PACK = 4
PAIRS = HD // 2
TILES = 4
GROUP = TILES * P
GROUPS = BATCH * SEQ // GROUP
LAST = GROUPS - 1
LATE_STEPS = 6
GROUPEDS = 13
FAST_PAIRS = 40
assert GROUP * BASE ** (-FAST_PAIRS / PAIRS) / (2.0 * math.pi) <= 0.5
BLOCKS = SEQ // GROUP
ROUND_TO_INTEGER = 1.5 * 2.0**23

FLOPS = 2 * BATCH * SEQ * D * 3 * HD


def broadcast_gain(nc, psum_const, ones, gain_row):
    gain = psum_const.tile([P, D], F32, name="gain")
    nc.tensor.matmul(out=gain[:], lhsT=ones[:], rhs=gain_row[:], start=True, stop=True)
    return gain


def group_weights(nc, raw, grouped):
    pairs = grouped[:, 0:2].rearrange("p m (i h) t -> p h m i t", h=2)
    raw_pairs = raw[:, 0:2].rearrange("p m t (i h) -> p h m i t", h=2)
    for h in range(2):
        nc.vector.tensor_copy(out=pairs[:, h], in_=raw_pairs[:, 1 - h])
    nc.vector.tensor_copy(out=grouped[:, 2], in_=raw[:, 2].rearrange("p t n -> p n t"))


def quantise_weights(nc, grouped, codes, scales, split_codes, split_scales):
    def quantise(operands):
        nc.vector.quantize_mx(
            out=codes[:, operands].rearrange("p m n -> p (m n)").bitcast(FP8X4),
            scales=scales[:, operands].rearrange("p m n -> p (m n)"),
            in_=grouped[:, operands].rearrange("p m n t -> p (m n t)"),
        )

    quantise(slice(0, 2))
    for src, dst, dtype in ((codes, split_codes, I32), (scales, split_scales, U8)):
        source = src[:, 0:2].rearrange("p m n -> p (m n)").bitcast(dtype)
        target = dst[:].rearrange("p h n -> p (h n)").bitcast(dtype)
        nc.vector.tensor_copy(
            out=target.rearrange("p (h c) -> p c h", h=2), in_=source.rearrange("p (c h) -> p c h", h=2)
        )
    quantise(slice(2, 3))


def rotation_angles(nc, const, ones, ramp, partition_4):
    ratio = BASE ** (-1.0 / PAIRS)
    ratios = const.tile([P, PAIRS], F32, name="ratios")
    nc.vector.tensor_scalar_mul(out=ratios[:], in0=ones[:, 0:PAIRS], scalar1=ratio)
    frequency = const.tile([P, PAIRS], F32, name="frequency")
    nc.vector.tensor_tensor_scan(
        out=frequency[:],
        data0=ratios[:],
        data1=ones[:, 0:PAIRS],
        initial=1.0 / (2.0 * math.pi * ratio),
        op0=ALU.mult,
        op1=ALU.mult,
    )
    position = const.tile([P, TILES + 1], F32, name="position")
    nc.vector.memset(position[:, TILES : TILES + 1], float(GROUP))
    nc.vector.tensor_scalar(
        out=position[:, 0:TILES], in0=ramp[:, 0:TILES], scalar1=partition_4, scalar2=None, op0=ALU.add
    )

    shape = [P, TILES + 1, PAIRS]
    part = const.tile(shape, F32, name="part")
    nc.vector.tensor_tensor(
        out=part[:],
        in0=position[:].unsqueeze(2).to_broadcast(shape),
        in1=frequency[:].unsqueeze(1).to_broadcast(shape),
        op=ALU.mult,
    )
    fast = part[:, :, 0:FAST_PAIRS]
    whole = const.tile([P, TILES + 1, FAST_PAIRS], F32, name="whole")
    nc.vector.tensor_scalar(
        out=whole[:],
        in0=fast,
        scalar1=ROUND_TO_INTEGER,
        scalar2=ROUND_TO_INTEGER,
        op0=ALU.add,
        op1=ALU.subtract,
    )
    nc.vector.tensor_tensor(out=fast, in0=fast, in1=whole[:], op=ALU.subtract)
    minus_abs = const.tile(shape, F32, name="minus_abs")
    nc.vector.scalar_tensor_tensor(
        out=minus_abs[:], in0=part[:], scalar=-1.0, in1=part[:], op0=ALU.mult, op1=ALU.min
    )
    return part, minus_abs


def tile_slidingwindowattention_pa_t_kernel(tc, x, ln_w, wq, wk, wv, out_0, out_1, out_2):
    nc = tc.nc
    by_group = "b (s p j) h d -> s b p (j h d)"
    x_hbm = x.rearrange("b (s p j) d -> s b p j d", p=P, j=TILES)
    q_groups = out_0.rearrange(by_group, p=P, j=TILES)
    k_groups = out_1.rearrange(by_group, p=P, j=TILES)
    v_groups = out_2.rearrange(by_group, p=P, j=TILES)

    with ExitStack() as ctx:
        const = ctx.enter_context(tc.tile_pool(name="const", bufs=1))
        loads = ctx.enter_context(tc.tile_pool(name="loads", bufs=GROUPS))
        small = ctx.enter_context(tc.tile_pool(name="small", bufs=6))
        work = ctx.enter_context(tc.tile_pool(name="work", bufs=3))
        stores = ctx.enter_context(tc.tile_pool(name="stores", bufs=GROUPS))
        psum_const = ctx.enter_context(tc.psum_pool(name="psum_const", bufs=1))
        psum_turned = ctx.enter_context(tc.psum_pool(name="psum_turned", bufs=3))
        psum_sums = ctx.enter_context(tc.psum_pool(name="psum_sums", bufs=1))
        psum_out = ctx.enter_context(tc.psum_pool(name="psum_out", bufs=1))
        ctx.enter_context(tc.manual_schedule())

        unit = const.tile([P, 1], F32, name="unit")
        nc.vector.memset(unit[:], 1.0)
        ones = const.tile([P, P], F32, name="ones")
        nc.vector.memset(ones[:], 1.0)
        ramp = const.tile([P, P], F32, name="ramp")
        nc.vector.tensor_tensor_scan(
            out=ramp[:], data0=ones[:], data1=ones[:], initial=-1.0, op0=ALU.mult, op1=ALU.add
        )
        fraction = const.tile([P, 8], F32, name="fraction")
        nc.vector.memset(fraction[:], TILES / P)
        start_ps = psum_out.tile([P, TILES, HD], F32, name="v_ps")
        nc.tensor.matmul(out=start_ps[:, 0, 0:8], lhsT=ramp[:], rhs=fraction[:], start=True, stop=True)
        partition_4 = start_ps[:, 0, 0:1]
        gain_row = const.tile([P, D], BF16, name="gain_row")
        nc.vector.memset(gain_row[:], 0.0)
        ones_bf16 = const.tile([P, P], BF16, name="ones_bf16")
        nc.vector.memset(ones_bf16[:], 1.0)

        warm = const.tile([P, 1], F32, name="warm")
        nc.scalar.activation(out=warm[:], in_=unit[:], func=ACT.Sin, scale=1.0)
        eps = const.tile([P, 1], F32, name="eps")
        nc.scalar.mul(out=eps[:], in_=unit[:], mul=EPS)
        quarter_turn = const.tile([P, 1], F32, name="quarter_turn")
        nc.scalar.mul(out=quarter_turn[:], in_=unit[:], mul=0.5 * math.pi)
        minus_quarter = const.tile([P, 1], F32, name="minus_quarter")
        nc.scalar.mul(out=minus_quarter[:], in_=unit[:], mul=-0.5 * math.pi)
        part, minus_abs = rotation_angles(nc, const, ones, ramp, partition_4)

        x_groups, x_tiles = {}, {}
        w_raw = const.tile([P, 3, PACK, HD], BF16, name="w_raw")
        for g in range(GROUPS):
            group = loads.tile([P, TILES, D], BF16, name="x_g")
            x_groups[g] = group
            x_tiles[g] = [group[:, j] for j in range(TILES)]
            pieces = {0: 4, 1: 2}.get(g, 1)
            for piece in range(pieces):
                rows = slice(piece * TILES // pieces, (piece + 1) * TILES // pieces)
                nc.sync.dma_start(out=group[:, rows], in_=x_hbm[g // BATCH, g % BATCH][:, rows])
            if g == 0:
                for m, w in enumerate((wq, wk, wv)):
                    nc.sync.dma_start(
                        out=w_raw[:, m].rearrange("p (u e) n -> p u (e n)", u=2),
                        in_=w.rearrange("(u p e) n -> p u (e n)", u=2, e=2),
                    )
                nc.sync.dma_start(out=gain_row[0:1, :], in_=ln_w.rearrange("(o d) -> o d", o=1))
        gain = broadcast_gain(nc, psum_const, ones_bf16, gain_row)
        identity = const.tile([P, P], F32, name="identity")
        w_grouped = const.tile([P, 3, HD, PACK], BF16, name="w_grouped", align_bytes=64)
        w_codes = const.tile([P, 3, HD], U32, name="w_codes", align_bytes=64)
        w_scales = const.tile([P, 3, HD], U8, name="w_scales", align_bytes=64)
        split_codes = const.tile([P, 2, HD], U32, name="split_codes", align_bytes=64)
        split_scales = const.tile([P, 2, HD], U8, name="split_scales", align_bytes=64)

        minus_cos = const.tile([P, 2 * TILES, PAIRS], F32, name="minus_cos")
        sin = const.tile([P, 2 * TILES, PAIRS], F32, name="sin")
        cross_1 = const.tile([P, TILES, PAIRS, 2], F32, name="cross_1")
        cross = [
            w_raw[:].rearrange("p m t n -> p (m t n)").bitcast(F32)[:, 0 : 2 * TILES * PAIRS].rearrange(
                "p (j i h) -> p j i h", i=PAIRS, h=2
            ),
            cross_1[:],
        ]
        advance = const.tile([P, 5, 1, PAIRS], F32, name="advance")

        def block_rows(s):
            return slice(s * TILES, (s + 1) * TILES)

        def first_sines():
            own, steps = slice(0, TILES), slice(TILES, TILES + 1)
            for out, rows in ((sin[:, own], own), (advance[:, 1], steps)):
                nc.scalar.activation(out=out, in_=part[:, rows], func=ACT.Sin, scale=2.0 * math.pi)
            for out, rows, bias, scale in (
                (minus_cos[:, own], own, minus_quarter, -2.0 * math.pi),
                (advance[:, 0], steps, quarter_turn, 2.0 * math.pi),
            ):
                nc.scalar.activation(out=out, in_=minus_abs[:, rows], func=ACT.Sin, bias=bias[:], scale=scale)

        def cross_work(s):
            rows = block_rows(s)
            return [
                (cross[s][:, :, :, h], minus_cos[:, rows], sin[:, rows], op)
                for h, op in ((0, ALU.subtract), (1, ALU.add))
            ]

        block_shape = [P, TILES, PAIRS]

        def advance_by(kind):
            return advance[:, kind].to_broadcast(block_shape)

        def first_turn():
            old, new = block_rows(0), block_rows(1)
            parts = w_grouped[:].rearrange("p m n t -> p (m n t)").bitcast(F32).rearrange(
                "p (a j i) -> p a j i", a=3, i=PAIRS
            )
            return [
                (parts[:, 2], cross[0][:, :, :, 1], advance_by(0), ALU.mult),
                (parts[:, 1], sin[:, old], advance_by(2), ALU.mult),
                (parts[:, 0], minus_cos[:, old], advance_by(3), ALU.mult),
                (minus_cos[:, new], parts[:, 2], parts[:, 1], ALU.add),
                (sin[:, new], parts[:, 2], parts[:, 0], ALU.subtract),
            ] + cross_work(1)

        half = TILES // 2 * PAIRS * 2

        def hosted(g):
            return groupeds[g][:].bitcast(F32)

        def cross_half(s, part_of):
            if s < 2:
                return cross[s].rearrange("p j i h -> p (j i h)")[:, part_of * half : (part_of + 1) * half]
            return hosted(LATE_STEPS * (s - 2) + 2 + 2 * part_of)[:, 0:half]

        def minus_cosine(s):
            if s < 2:
                return minus_cos[:, block_rows(s)]
            return hosted(LATE_STEPS * (s - 2) + 6)[:, 0:half].rearrange("p (j i) -> p j i", i=PAIRS)

        def late_table(step):
            s, phase = 2 + step // LATE_STEPS, step % LATE_STEPS
            target, product = hosted(step + 1)[:, 0:half], hosted(step)[:, 0:half]
            if phase < 4:
                shape = [P, TILES // 2, PAIRS, 2]
                doubled = advance[:, 4].unsqueeze(3).to_broadcast(shape)
                older = cross_half(s - 1 - phase % 2, phase // 2)
                pairs = "p (j i h) -> p j i h"
                if phase % 2 == 0:
                    out, in0 = (ap.rearrange(pairs, i=PAIRS, h=2) for ap in (target, older))
                    return [(out, in0, doubled, ALU.mult)]
                return [(target, product, older, ALU.subtract)]
            target, product = (ap.rearrange("p (j i) -> p j i", i=PAIRS) for ap in (target, product))
            if phase == 4:
                return [(target, minus_cosine(s - 1), advance_by(4), ALU.mult)]
            return [(target, product, minus_cosine(s - 2), ALU.subtract)]

        def on_gpsimd(work_list):
            for out, in0, in1, op in work_list:
                nc.gpsimd.tensor_tensor(out=out, in0=in0, in1=in1, op=op)

        mean_sqs, rstds, xns, turneds, groupeds, operands, banks, products = {}, {}, {}, {}, {}, {}, {}, {}

        def square(g, tiles):
            if g not in mean_sqs:
                mean_sqs[g] = small.tile([P, TILES], F32, name="mean_sq")
            for j in tiles:
                squares = work.tile([P, D], BF16, name="squares")
                nc.scalar.activation(
                    out=squares[:],
                    in_=x_tiles[g][j],
                    func=ACT.Square,
                    scale=1.0 / math.sqrt(D),
                    accum_out=mean_sqs[g][:, j : j + 1],
                )

        def square_on_vector(g, tiles):
            unread = work.tile([P, 2 * D], BF16, name="unread")
            if g not in mean_sqs:
                mean_sqs[g] = small.tile([P, TILES], F32, name="mean_sq")
            for j in tiles:
                nc.vector.scalar_tensor_tensor(
                    out=unread[:, j % 2 * D : (j % 2 + 1) * D],
                    in0=x_tiles[g][j],
                    scalar=1.0 / D,
                    in1=x_tiles[g][j],
                    op0=ALU.mult,
                    op1=ALU.mult,
                    accum_out=mean_sqs[g][:, j : j + 1],
                )

        def first_squares(g):
            square(g, range(0, TILES // 2))

        def last_squares(g):
            if g > 0:
                square(g, range(TILES // 2, TILES))
            rstds[g] = small.tile([P, TILES], F32, name="rstd")
            nc.scalar.activation(
                out=rstds[g][:], in_=mean_sqs[g][:], func=ACT.Abs_reciprocal_sqrt, bias=eps[:], scale=1.0
            )

        def normalise(g):
            xns[g] = work.tile([P, TILES * D], BF16, name="xn")
            for j in range(TILES):
                nc.vector.scalar_tensor_tensor(
                    out=xns[g][:, j * D : (j + 1) * D],
                    in0=x_tiles[g][j],
                    scalar=rstds[g][:, j : j + 1],
                    in1=gain[:],
                    op0=ALU.mult,
                    op1=ALU.mult,
                )

        def turn(g):
            words = xns[g][:].bitcast(F32).rearrange("p (j u w) -> p j u w", j=TILES, u=2)
            turneds[g] = []
            for first in range(0, TILES, 2):
                turned = psum_turned.tile([P, 2, 2, P], F32, name="turned")
                for j in range(2):
                    for u in range(2):
                        nc.tensor.transpose(out=turned[:, j, u, :], in_=words[:, first + j, u, :], identity=identity[:])
                turneds[g].append(turned)

        def regroup(g):
            grouped = work.tile([P, GROUP * PACK], BF16, name="grouped", align_bytes=64, bufs=GROUPEDS)
            words = grouped[:].bitcast(F32).rearrange("p (b j t u) -> p b j t u", b=2, j=2, u=2)
            for b, turned in enumerate(turneds[g]):
                nc.scalar.copy(out=words[:, b], in_=turned[:].rearrange("p j u t -> p j t u"))
            groupeds[g] = grouped

        def quantise(g):
            codes = work.tile([P, GROUP], U32, name="codes", align_bytes=64)
            scales = work.tile([P, GROUP], U8, name="scales", align_bytes=64)
            nc.vector.quantize_mx(out=codes[:].bitcast(FP8X4), scales=scales[:], in_=groupeds[g][:])
            operands[g] = (codes, scales)

        def project(g):
            codes, scales = operands[g]

            def passes(bank, operand, tiles):
                for j in tiles:
                    tokens = slice(j * P, (j + 1) * P)
                    nc.tensor.matmul_mx(
                        out=bank[:, j - tiles[0], :],
                        lhsT=codes[:, tokens].bitcast(FP8X4),
                        lhsT_scale=scales[:, tokens],
                        rhs=w_codes[:, operand].bitcast(FP8X4),
                        rhs_scale=w_scales[:, operand],
                        start=True,
                        stop=True,
                    )

            own_ps = [
                psum_out.tile([P, 2, TILES // 2, HD], F32, name="own_ps_%d" % first) for first in range(2)
            ]
            v_ps = psum_out.tile([P, TILES, HD], F32, name="v_ps")
            for first in range(2):
                for operand in range(2):
                    passes(own_ps[first][:, operand], operand, range(2 * first, 2 * first + 2))
            sum_ps = psum_sums.tile([P, TILES, HD], F32, name="sum_ps")
            for j in range(TILES):
                tokens = slice(j * P, (j + 1) * P)
                for operand in range(2):
                    nc.tensor.matmul_mx(
                        out=sum_ps[:, j, :],
                        lhsT=codes[:, tokens].bitcast(FP8X4),
                        lhsT_scale=scales[:, tokens],
                        rhs=split_codes[:, operand].bitcast(FP8X4),
                        rhs_scale=split_scales[:, operand],
                        start=(operand == 0),
                        stop=(operand == 1),
                    )
            passes(v_ps[:], 2, range(TILES))
            banks[g] = (sum_ps, own_ps, v_ps)

        def multiply_shared(g):
            shape = [P, TILES, 2, PAIRS]
            shared = hosted(g)[:, 2 * TILES * PAIRS :].rearrange("p (c j i) -> p c j i", c=2, j=TILES)
            nc.vector.tensor_tensor(
                out=shared.rearrange("p c j i -> p j c i"),
                in0=banks[g][0][:].rearrange("p j (c i) -> p j c i", c=2),
                in1=minus_cosine(g // BATCH).unsqueeze(2).to_broadcast(shape),
                op=ALU.mult,
            )
            products[g].append(shared)

        def multiply_own(g, first):
            table = cross_half(g // BATCH, first)
            nc.vector.tensor_tensor(
                out=products[g][0].rearrange("p c j i h -> p c (j i h)")[:, :, first * half : (first + 1) * half],
                in0=banks[g][1][first][:].rearrange("p c j d -> p c (j d)"),
                in1=table.unsqueeze(1).to_broadcast([P, 2, half]),
                op=ALU.mult,
            )

        def multiply_first(g):
            own = x_groups[g][:].rearrange("p j d -> p (j d)").bitcast(F32)
            products[g] = [own.rearrange("p (c j i h) -> p c j i h", c=2, j=TILES, h=2)]
            multiply_own(g, 0)

        def multiply_last(g):
            multiply_own(g, 1)

        def copy_v(g):
            v_sb = stores.tile([P, TILES * HD], F32, name="v_sb")
            nc.scalar.copy(out=v_sb[:], in_=banks[g][2][:].rearrange("p j d -> p (j d)"))
            queue = nc.scalar if g >= LAST - 1 else nc.sync
            queue.dma_start(out=v_groups[g // BATCH, g % BATCH], in_=v_sb[:])

        def add_and_store(g):
            own, shared = products[g]
            rotated = [own[:, c] for c in range(2)]
            if g == LAST - 2:
                rotated[0] = hosted(LAST)[:, 0 : 2 * half].rearrange("p (j i h) -> p j i h", j=TILES, h=2)
                for c in range(2):
                    nc.gpsimd.tensor_tensor(
                        out=rotated[c],
                        in0=own[:, c],
                        in1=shared[:, c].unsqueeze(3).to_broadcast([P, TILES, PAIRS, 2]),
                        op=ALU.subtract,
                    )
            elif g < LAST - 2:
                nc.gpsimd.tensor_tensor(
                    out=own,
                    in0=own,
                    in1=shared.unsqueeze(4).to_broadcast([P, 2, TILES, PAIRS, 2]),
                    op=ALU.subtract,
                )
            for c, hbm in enumerate((q_groups, k_groups)):
                pieces = 2 if g == LAST and c == 1 else 1
                for piece in range(pieces):
                    tiles = slice(piece * TILES // pieces, (piece + 1) * TILES // pieces)
                    if g >= LAST - 1:
                        nc.vector.tensor_tensor(
                            out=rotated[c][:, tiles],
                            in0=own[:, c, tiles],
                            in1=shared[:, c, tiles].unsqueeze(3).to_broadcast([P, TILES // pieces, PAIRS, 2]),
                            op=ALU.subtract,
                        )
                    nc.sync.dma_start(
                        out=hbm[g // BATCH, g % BATCH].rearrange("p (j d) -> p j d", j=TILES)[:, tiles],
                        in_=rotated[c][:, tiles].rearrange("p j i h -> p j (i h)"),
                    )

        def run(stage, index, count):
            if 0 <= index < count:
                stage(index)

        first_sines()
        nc.scalar.activation(out=warm[:], in_=unit[:], func=ACT.Abs_reciprocal_sqrt, scale=1.0)
        square_on_vector(0, range(TILES - 1))
        square(0, range(TILES - 1, TILES))
        nc.vector.tensor_scalar(
            out=identity[:], in0=ramp[:], scalar1=float(TILES), scalar2=partition_4, op0=ALU.mult, op1=ALU.is_equal
        )
        group_weights(nc, w_raw, w_grouped)
        on_gpsimd(
            cross_work(0)
            + [
                (advance[:, 2], advance[:, 1], advance[:, 0], ALU.subtract),
                (advance[:, 3], advance[:, 1], advance[:, 0], ALU.add),
                (advance[:, 4], advance[:, 0], advance[:, 0], ALU.add),
            ]
        )
        for step in range(-3, GROUPS):
            run(last_squares, step + 3, GROUPS)
            run(first_squares, step + 4, GROUPS)
            run(copy_v, step, GROUPS)
            run(normalise, step + 2, GROUPS)
            run(turn, step + 2, GROUPS)
            run(multiply_first, step, GROUPS)
            run(multiply_last, step, GROUPS)
            if step == LAST:
                add_and_store(step - 1)
            if step + 2 == 0:
                quantise_weights(nc, w_grouped, w_codes, w_scales, split_codes, split_scales)
                on_gpsimd(first_turn())
            if step != LAST - 1:
                run(quantise, step + 1, GROUPS)
                run(project, step + 1, GROUPS)
            run(regroup, step + 2, GROUPS)
            if 0 <= step < LATE_STEPS * (BLOCKS - 2):
                on_gpsimd(late_table(step))
            run(multiply_shared, step, GROUPS)
            if step == LAST - 2:
                quantise(LAST)
            if step == LAST - 1:
                project(LAST)
            if step != LAST - 1:
                run(add_and_store, step, GROUPS)
